import numpy as np
import ml_dtypes


def mxq(x, axis, fmt="e4m3"):
    dtype, down = {"e4m3": (ml_dtypes.float8_e4m3fn, 7), "e5m2": (ml_dtypes.float8_e5m2, 14)}[fmt]
    v = np.moveaxis(np.asarray(x, np.float32).astype(ml_dtypes.bfloat16).astype(np.float64), axis, -1)
    blocks = v.reshape(v.shape[:-1] + (-1, 32))
    amax = np.abs(blocks).max(-1, keepdims=True)
    byte = np.maximum(np.where(amax > 0, np.frexp(amax)[1] - 1 + 127, 0) - down, 1)
    scale = np.exp2(byte - 127.0)
    codes = (blocks / scale).astype(np.float32).astype(dtype).astype(np.float64)
    return np.moveaxis((codes * scale).reshape(v.shape), -1, axis)


WIDE = False


def mx_kscale(k):
    if not WIDE:
        return np.ones(k)
    levels = np.array([10, -10, 5, -5, 0])
    a = np.random.permutation(np.resize(levels, k // 512 * 4)).reshape(k // 512, 4)
    idx = np.arange(k)
    return np.exp2(a[idx // 512, idx % 128 // 32])


BF16 = ml_dtypes.bfloat16


def bf(x):
    return np.asarray(x, np.float32).astype(BF16)


def f64(x):
    return np.asarray(x).astype(np.float64)


B, S, D = 4, 1024, 512
EPS = 1e-8


def layer_norm(v, w, b):
    mu = v.mean(-1, keepdims=True)
    var = ((v - mu) ** 2).mean(-1, keepdims=True)
    return (v - mu) / np.sqrt(var + EPS) * w + b


def setup_inputs():
    s = mx_kscale(D)
    xr = np.random.standard_normal((B, S, D)) + np.random.uniform(-1.2, 1.2, (B, S, 1))
    xi = np.random.standard_normal((B, S, D)) + np.random.uniform(-1.2, 1.2, (B, S, 1))
    return {"x_real": bf(xr * s), "x_imag": bf(xi * s),
            "phase_matrix": bf(np.random.standard_normal((D, D)) / np.sqrt(D) / s[:, None]),
            "coherence_factor": bf(np.random.uniform(0.35, 0.5, 1)),
            "ln_weight": bf(1.0 + 0.1 * np.random.standard_normal(D)),
            "ln_bias": bf(0.3 * np.random.standard_normal(D))}


def reference(x_real, x_imag, phase_matrix, coherence_factor, ln_weight, ln_bias):
    xr, xi = f64(x_real), f64(x_imag)
    a, b = xr + EPS, xi + EPS
    r = np.sqrt(a * a + b * b)
    sc = (a / r).sum(-1, keepdims=True)
    ss = (b / r).sum(-1, keepdims=True)
    coherence = (sc * sc + ss * ss) / (D * D)
    p = mxq(xr, 2, "e4m3") @ mxq(f64(phase_matrix), 0, "e4m3")
    p = p * f64(coherence_factor) * (1.0 - coherence)
    c, sn = np.cos(p), np.sin(p)
    new_real = xr * c - xi * sn
    new_imag = xr * sn + xi * c
    norm = np.sqrt(new_real ** 2 + new_imag ** 2 + EPS)
    new_real = new_real / norm
    new_imag = new_imag / norm
    w, bb = f64(ln_weight), f64(ln_bias)
    return (layer_norm(new_real, w, bb), layer_norm(new_imag, w, bb))

@@ -1,0 +1,302 @@
+import math
+from contextlib import ExitStack
+
+import concourse.bass as bass
+import concourse.mybir as mybir
+import concourse.tile as tile
+from concourse.masks import make_identity
+
+F32 = mybir.dt.float32
+BF16 = mybir.dt.bfloat16
+I32 = mybir.dt.int32
+U32 = mybir.dt.uint32
+U8 = mybir.dt.uint8
+FP8X4 = mybir.dt.float8_e4m3fn_x4
+ALU = mybir.AluOpType
+ACT = mybir.ActivationFunctionType
+
+P = 128
+D = 512
+ROWS = 4096
+NT = ROWS // P
+G = 4
+NG = NT // G
+EPS = 1e-8
+TWO_PI = 2.0 * math.pi
+
+FLOPS = 2 * ROWS * D * D
+
+
+def tile_quantumcoherencelayer_t_kernel(
+    tc, x_real, x_imag, phase_matrix, coherence_factor, ln_weight, ln_bias, out_0, out_1
+):
+    nc = tc.nc
+    xr_d = x_real.flatten_outer_dims().rearrange("(p t) d -> p t d", t=NT)
+    xi_d = x_imag.flatten_outer_dims().rearrange("(p t) d -> p t d", t=NT)
+    or_d = out_0.flatten_outer_dims().rearrange("(p t) d -> p t d", t=NT)
+    oi_d = out_1.flatten_outer_dims().rearrange("(p t) d -> p t d", t=NT)
+
+    with ExitStack() as ctx:
+        keep = ctx.enter_context(tc.tile_pool(name="keep", bufs=1))
+        work = ctx.enter_context(tc.tile_pool(name="work", bufs=1))
+        small = ctx.enter_context(tc.tile_pool(name="small", bufs=3))
+        ps_keep = ctx.enter_context(tc.psum_pool(name="ps_keep", bufs=1))
+        ps_p = ctx.enter_context(tc.psum_pool(name="ps_p", bufs=4))
+        ps_t = ctx.enter_context(tc.psum_pool(name="ps_t", bufs=2))
+        ctx.enter_context(tc.manual_schedule())
+
+        xr_all = keep.tile([P, NT, D], BF16, name="xr_all", align_bytes=64)
+        xi_all = keep.tile([P, NT, D], BF16, name="xi_all", align_bytes=64)
+        ph_raw = keep.tile([P, 4, D], BF16, name="ph_raw")
+        ph_grp = keep.tile([P, D, 4], BF16, name="ph_grp", align_bytes=64)
+        ph_codes = keep.tile([P, D], U32, name="ph_codes", align_bytes=64)
+        ph_scales = keep.tile([P, D], U8, name="ph_scales", align_bytes=64)
+        wb_row = keep.tile([P, 2 * D], BF16, name="wb_row")
+        ones = keep.tile([P, P], BF16, name="ones")
+        ident = keep.tile([P, P], F32, name="ident")
+        cf_bf = keep.tile([P, 1], BF16, name="cf_bf")
+        cfs = keep.tile([P, 1], F32, name="cfs")
+        ncf = keep.tile([P, 1], F32, name="ncf")
+        eps_t = keep.tile([P, 1], F32, name="eps_t")
+        hpi_t = keep.tile([P, 1], F32, name="hpi_t")
+        one_t = keep.tile([P, 1], F32, name="one_t")
+        mhalf = keep.tile([P, 2 * G], F32, name="mhalf")
+        w_ps = ps_keep.tile([P, D], F32, name="w_ps")
+        b_ps = ps_keep.tile([P, D], F32, name="b_ps")
+
+        nc.vector.memset(wb_row[:], 0.0)
+        nc.vector.memset(ones[:], 1.0)
+        nc.vector.memset(eps_t[:], EPS)
+        nc.vector.memset(one_t[:], 1.0)
+        nc.vector.tensor_scalar(out=hpi_t[:], in0=one_t[:], scalar1=0.5 * math.pi, scalar2=None, op0=ALU.mult)
+        nc.vector.memset(mhalf[:], -0.5)
+        make_identity(nc, ident[:])
+
+        def load(s):
+            sl = slice(G * s, G * s + G)
+            nc.sync.dma_start(out=xr_all[:, sl, :], in_=xr_d[:, sl, :])
+            nc.sync.dma_start(out=xi_all[:, sl, :], in_=xi_d[:, sl, :])
+
+        load(0)
+        nc.sync.dma_start(out=ph_raw[:], in_=phase_matrix.rearrange("(p j) n -> p j n", j=4))
+        nc.sync.dma_start(out=wb_row[0:1, 0:D], in_=ln_weight.unsqueeze(0))
+        nc.sync.dma_start(out=wb_row[0:1, D : 2 * D], in_=ln_bias.unsqueeze(0))
+        nc.sync.dma_start(out=cf_bf[:], in_=coherence_factor.partition_broadcast(P))
+        for s in range(1, NG):
+            load(s)
+
+        nc.vector.tensor_copy(out=ph_grp[:], in_=ph_raw[:].rearrange("p j n -> p n j"))
+        nc.vector.tensor_scalar(out=cfs[:], in0=cf_bf[:], scalar1=1.0 / TWO_PI, scalar2=None, op0=ALU.mult)
+        nc.vector.tensor_scalar(
+            out=ncf[:], in0=cf_bf[:], scalar1=-1.0 / (TWO_PI * D * D), scalar2=None, op0=ALU.mult
+        )
+        nc.vector.quantize_mx(
+            out=ph_codes[:].bitcast(FP8X4), scales=ph_scales[:], in_=ph_grp[:].rearrange("p n j -> p (n j)")
+        )
+        nc.tensor.matmul(out=w_ps[:], lhsT=ones[:], rhs=wb_row[:, 0:D], start=True, stop=True)
+        nc.tensor.matmul(out=b_ps[:], lhsT=ones[:], rhs=wb_row[:, D : 2 * D], start=True, stop=True)
+
+        xr_words = xr_all[:].rearrange("p t d -> p (t d)").bitcast(F32).rearrange(
+            "p (t j u) -> p t u j", t=NT, u=2
+        )
+
+        st = {}
+
+        def in_range(s):
+            return 0 <= s < NG
+
+        def pe_transposes(s):
+            xts = []
+            for h in range(G // 2):
+                xt = ps_t.tile([P, 2, 2, P], F32, name="xt")
+                for tt in range(2):
+                    for u in range(2):
+                        nc.tensor.transpose(xt[:, tt, u, :], xr_words[:, G * s + 2 * h + tt, u, :], ident[:])
+                xts.append(xt)
+            st[("xt", s)] = xts
+
+        def act_a(s):
+            sl = slice(G * s, G * s + G)
+            xg = work.tile([P, G * P * 4], BF16, name="xg", bufs=2, align_bytes=64)
+            xg_w = xg[:].bitcast(F32).rearrange("p (t r u) -> p t r u", t=G, u=2)
+            for h in range(G // 2):
+                xt = st[("xt", s)][h]
+                nc.scalar.copy(out=xg_w[:, 2 * h : 2 * h + 2, :, :], in_=xt[:].rearrange("p t u r -> p t r u"))
+            sa = work.tile([P, G, D], F32, name="sa", bufs=2)
+            sb = work.tile([P, G, D], F32, name="sb", bufs=1)
+            sr = work.tile([P, G, D], F32, name="sr", bufs=3)
+            si = work.tile([P, G, D], F32, name="si", bufs=1)
+            nc.scalar.activation(out=sa[:], in_=xr_all[:, sl, :], func=ACT.Square, bias=eps_t[:])
+            nc.scalar.activation(out=sb[:], in_=xi_all[:, sl, :], func=ACT.Square, bias=eps_t[:])
+            nc.scalar.activation(out=sr[:], in_=xr_all[:, sl, :], func=ACT.Square)
+            nc.scalar.activation(out=si[:], in_=xi_all[:, sl, :], func=ACT.Square)
+            st[("xg", s)] = xg
+            st[("sa", s)] = sa
+            st[("sb", s)] = sb
+            st[("sr", s)] = sr
+            st[("si", s)] = si
+
+        def dve_a(s):
+            xc = work.tile([P, G * P], U32, name="xc", bufs=2, align_bytes=64)
+            xs = work.tile([P, G * P], U8, name="xs", bufs=2, align_bytes=64)
+            nc.vector.quantize_mx(out=xc[:].bitcast(FP8X4), scales=xs[:], in_=st[("xg", s)][:])
+            sa, sb, sr, si = st[("sa", s)], st[("sb", s)], st[("sr", s)], st[("si", s)]
+            nc.vector.tensor_tensor(out=sa[:], in0=sa[:], in1=sb[:], op=ALU.add)
+            nc.vector.tensor_tensor(out=sr[:], in0=sr[:], in1=si[:], op=ALU.add)
+            pts = []
+            for tt in range(G):
+                pt = ps_p.tile([P, D], F32, name="pt")
+                cols = slice(P * tt, P * tt + P)
+                nc.tensor.matmul_mx(
+                    out=pt[:],
+                    lhsT=xc[:, cols].bitcast(FP8X4),
+                    lhsT_scale=xs[:, cols],
+                    rhs=ph_codes[:].bitcast(FP8X4),
+                    rhs_scale=ph_scales[:],
+                    start=True,
+                    stop=True,
+                )
+                pts.append(pt)
+            st[("pt", s)] = pts
+
+        def act_b(s):
+            sa, sr = st[("sa", s)], st[("sr", s)]
+            nc.scalar.activation(out=sa[:], in_=sa[:], func=ACT.Abs_reciprocal_sqrt)
+            nc.scalar.activation(out=sr[:], in_=sr[:], func=ACT.Abs_reciprocal_sqrt, bias=eps_t[:])
+
+        def dve_b1(s):
+            sa = st[("sa", s)]
+            coh = small.tile([P, 2, G], F32, name="coh")
+            for tt in range(G):
+                t = G * s + tt
+                for o, x_all in enumerate((xr_all, xi_all)):
+                    junk = work.tile([P, D], F32, name="vjunk", bufs=2)
+                    nc.vector.scalar_tensor_tensor(
+                        out=junk[:], in0=x_all[:, t, :], scalar=EPS, in1=sa[:, tt, :],
+                        op0=ALU.add, op1=ALU.mult, accum_out=coh[:, o, tt : tt + 1],
+                    )
+            st[("coh", s)] = coh
+
+        def dve_b2(s):
+            coh = st[("coh", s)]
+            csq = small.tile([P, 2, G], F32, name="csq")
+            csum = small.tile([P, G], F32, name="csum")
+            gq = small.tile([P, G], F32, name="gq")
+            nc.vector.tensor_tensor(out=csq[:], in0=coh[:], in1=coh[:], op=ALU.mult)
+            nc.vector.tensor_tensor(out=csum[:], in0=csq[:, 0, :], in1=csq[:, 1, :], op=ALU.add)
+            nc.vector.tensor_scalar(
+                out=gq[:], in0=csum[:], scalar1=ncf[:], scalar2=cfs[:], op0=ALU.mult, op1=ALU.add
+            )
+            fr = work.tile([P, G, D], F32, name="fr", bufs=1)
+            for tt in range(G):
+                pt = st[("pt", s)][tt]
+                kk = work.tile([P, D], I32, name="kk", bufs=2)
+                nc.vector.tensor_scalar(
+                    out=kk[:], in0=pt[:], scalar1=gq[:, tt : tt + 1], scalar2=None, op0=ALU.mult
+                )
+                nc.vector.scalar_tensor_tensor(
+                    out=fr[:, tt, :], in0=pt[:], scalar=gq[:, tt : tt + 1], in1=kk[:],
+                    op0=ALU.mult, op1=ALU.subtract,
+                )
+            st[("fr", s)] = fr
+
+        def act_c(s):
+            fr = st[("fr", s)]
+            cc = work.tile([P, G, D], F32, name="cc", bufs=1)
+            ss = work.tile([P, G, D], F32, name="ss", bufs=1)
+            nc.scalar.activation(out=cc[:], in_=fr[:], func=ACT.Abs)
+            nc.scalar.activation(out=ss[:], in_=fr[:], func=ACT.Sin, scale=TWO_PI)
+            nc.scalar.activation(out=cc[:], in_=cc[:], func=ACT.Sin, scale=-TWO_PI, bias=hpi_t[:])
+            st[("cc", s)] = cc
+            st[("ss", s)] = ss
+
+        def dve_c(s):
+            sl = slice(G * s, G * s + G)
+            q, cc, ss = st[("sr", s)], st[("cc", s)], st[("ss", s)]
+            c0 = work.tile([P, G, D], F32, name="c0", bufs=1)
+            x1 = work.tile([P, G, D], F32, name="x1", bufs=2)
+            x2 = work.tile([P, G, D], F32, name="x2", bufs=2)
+            sums = small.tile([P, 2, G], F32, name="sums")
+            nc.vector.tensor_tensor(out=c0[:], in0=xr_all[:, sl, :], in1=q[:], op=ALU.mult)
+            nc.vector.tensor_tensor(out=q[:], in0=xi_all[:, sl, :], in1=q[:], op=ALU.mult)
+            nc.vector.tensor_tensor(out=x1[:], in0=c0[:], in1=cc[:], op=ALU.mult)
+            nc.vector.tensor_tensor(out=x2[:], in0=q[:], in1=cc[:], op=ALU.mult)
+            nc.vector.tensor_tensor(out=c0[:], in0=c0[:], in1=ss[:], op=ALU.mult)
+            nc.vector.tensor_tensor(out=q[:], in0=q[:], in1=ss[:], op=ALU.mult)
+            for tt in range(G):
+                nc.vector.scalar_tensor_tensor(
+                    out=x1[:, tt, :], in0=x1[:, tt, :], scalar=1.0, in1=q[:, tt, :],
+                    op0=ALU.mult, op1=ALU.subtract, accum_out=sums[:, 0, tt : tt + 1],
+                )
+                nc.vector.scalar_tensor_tensor(
+                    out=x2[:, tt, :], in0=x2[:, tt, :], scalar=1.0, in1=c0[:, tt, :],
+                    op0=ALU.mult, op1=ALU.add, accum_out=sums[:, 1, tt : tt + 1],
+                )
+            st[("x1", s)] = x1
+            st[("x2", s)] = x2
+            st[("sums", s)] = sums
+
+        def act_d(s):
+            ssq = small.tile([P, 2, G], F32, name="ssq")
+            for tt in range(G):
+                for o, x in enumerate((st[("x1", s)], st[("x2", s)])):
+                    junk = work.tile([P, D], F32, name="ajunk", bufs=2)
+                    nc.scalar.activation(
+                        out=junk[:], in_=x[:, tt, :], func=ACT.Square, accum_out=ssq[:, o, tt : tt + 1]
+                    )
+            st[("ssq", s)] = ssq
+
+        def stats(s):
+            sums, ssq = st[("sums", s)], st[("ssq", s)]
+            mean = small.tile([P, 2, G], F32, name="mean")
+            msq = small.tile([P, 2, G], F32, name="msq")
+            var = small.tile([P, 2, G], F32, name="var")
+            vare = small.tile([P, 2, G], F32, name="vare")
+            rstd = small.tile([P, 2, G], F32, name="rstd")
+            nc.vector.tensor_scalar(out=mean[:], in0=sums[:], scalar1=1.0 / D, scalar2=None, op0=ALU.mult)
+            nc.vector.tensor_tensor(out=msq[:], in0=mean[:], in1=mean[:], op=ALU.mult)
+            nc.vector.scalar_tensor_tensor(
+                out=var[:], in0=ssq[:], scalar=1.0 / D, in1=msq[:], op0=ALU.mult, op1=ALU.subtract
+            )
+            nc.gpsimd.tensor_scalar(out=vare[:], in0=var[:], scalar1=0.0, scalar2=EPS, op0=ALU.max, op1=ALU.add)
+            nc.gpsimd.tensor_tensor(
+                out=rstd[:].rearrange("p o t -> p (o t)"), in0=vare[:].rearrange("p o t -> p (o t)"),
+                in1=mhalf[:], op=ALU.pow,
+            )
+            st[("mean", s)] = mean
+            st[("rstd", s)] = rstd
+
+        def dve_d(s):
+            sl = slice(G * s, G * s + G)
+            mean, rstd = st[("mean", s)], st[("rstd", s)]
+            for o, (x, o_d) in enumerate(((st[("x1", s)], or_d), (st[("x2", s)], oi_d))):
+                for tt in range(G):
+                    nc.vector.scalar_tensor_tensor(
+                        out=x[:, tt, :], in0=x[:, tt, :], scalar=mean[:, o, tt : tt + 1], in1=w_ps[:],
+                        op0=ALU.subtract, op1=ALU.mult,
+                    )
+                    nc.vector.scalar_tensor_tensor(
+                        out=x[:, tt, :], in0=x[:, tt, :], scalar=rstd[:, o, tt : tt + 1], in1=b_ps[:],
+                        op0=ALU.mult, op1=ALU.add,
+                    )
+                nc.sync.dma_start(out=o_d[:, sl, :], in_=x[:])
+
+        for i in range(-2, NG):
+            if in_range(i + 1):
+                dve_a(i + 1)
+                act_b(i + 1)
+            if in_range(i):
+                dve_c(i)
+                act_d(i)
+            if in_range(i + 2):
+                pe_transposes(i + 2)
+                act_a(i + 2)
+            if in_range(i + 1):
+                dve_b1(i + 1)
+            if in_range(i):
+                stats(i)
+            if in_range(i + 1):
+                dve_b2(i + 1)
+                act_c(i + 1)
+            if in_range(i):
+                dve_d(i)

@@ -140,9 +140,6 @@ def tile_quantumcoherencelayer_t_kernel(
             xc = work.tile([P, G * P], U32, name="xc", bufs=2, align_bytes=64)
             xs = work.tile([P, G * P], U8, name="xs", bufs=2, align_bytes=64)
             nc.vector.quantize_mx(out=xc[:].bitcast(FP8X4), scales=xs[:], in_=st[("xg", s)][:])
-            sa, sb, sr, si = st[("sa", s)], st[("sb", s)], st[("sr", s)], st[("si", s)]
-            nc.vector.tensor_tensor(out=sa[:], in0=sa[:], in1=sb[:], op=ALU.add)
-            nc.vector.tensor_tensor(out=sr[:], in0=sr[:], in1=si[:], op=ALU.add)
             pts = []
             for tt in range(G):
                 pt = ps_p.tile([P, D], F32, name="pt")
@@ -158,6 +155,12 @@ def tile_quantumcoherencelayer_t_kernel(
                 )
                 pts.append(pt)
             st[("pt", s)] = pts
+
+        def gp_adds(s):
+            sa, sb, sr, si = st[("sa", s)], st[("sb", s)], st[("sr", s)], st[("si", s)]
+            for acc, oth in ((sa, sb), (sr, si)):
+                for tt in range(G):
+                    nc.gpsimd.tensor_tensor(out=acc[:, tt, :], in0=acc[:, tt, :], in1=oth[:, tt, :], op=ALU.add)
 
         def act_b(s):
             sa, sr = st[("sa", s)], st[("sr", s)]
@@ -285,16 +288,18 @@ def tile_quantumcoherencelayer_t_kernel(
             if in_range(i + 1):
                 dve_a(i + 1)
                 act_b(i + 1)
-            if in_range(i):
-                dve_c(i)
-                act_d(i)
             if in_range(i + 2):
                 pe_transposes(i + 2)
                 act_a(i + 2)
+            if in_range(i):
+                dve_c(i)
+                act_d(i)
             if in_range(i + 1):
                 dve_b1(i + 1)
             if in_range(i):
                 stats(i)
+            if in_range(i + 2):
+                gp_adds(i + 2)
             if in_range(i + 1):
                 dve_b2(i + 1)
                 act_c(i + 1)

@@ -19,7 +19,7 @@ P = 128
 D = 512
 ROWS = 4096
 NT = ROWS // P
-G = 4
+G = 2
 NG = NT // G
 EPS = 1e-8
 TWO_PI = 2.0 * math.pi
@@ -39,11 +39,10 @@ def tile_quantumcoherencelayer_t_kernel(
     with ExitStack() as ctx:
         keep = ctx.enter_context(tc.tile_pool(name="keep", bufs=1))
         work = ctx.enter_context(tc.tile_pool(name="work", bufs=1))
-        small = ctx.enter_context(tc.tile_pool(name="small", bufs=3))
+        small = ctx.enter_context(tc.tile_pool(name="small", bufs=6))
         ps_keep = ctx.enter_context(tc.psum_pool(name="ps_keep", bufs=1))
         ps_p = ctx.enter_context(tc.psum_pool(name="ps_p", bufs=4))
         ps_t = ctx.enter_context(tc.psum_pool(name="ps_t", bufs=2))
-        ctx.enter_context(tc.manual_schedule())
 
         xr_all = keep.tile([P, NT, D], BF16, name="xr_all", align_bytes=64)
         xi_all = keep.tile([P, NT, D], BF16, name="xi_all", align_bytes=64)
@@ -117,15 +116,15 @@ def tile_quantumcoherencelayer_t_kernel(
 
         def act_a(s):
             sl = slice(G * s, G * s + G)
-            xg = work.tile([P, G * P * 4], BF16, name="xg", bufs=2, align_bytes=64)
+            xg = work.tile([P, G * P * 4], BF16, name="xg", bufs=3, align_bytes=64)
             xg_w = xg[:].bitcast(F32).rearrange("p (t r u) -> p t r u", t=G, u=2)
             for h in range(G // 2):
                 xt = st[("xt", s)][h]
                 nc.scalar.copy(out=xg_w[:, 2 * h : 2 * h + 2, :, :], in_=xt[:].rearrange("p t u r -> p t r u"))
-            sa = work.tile([P, G, D], F32, name="sa", bufs=2)
-            sb = work.tile([P, G, D], F32, name="sb", bufs=1)
-            sr = work.tile([P, G, D], F32, name="sr", bufs=3)
-            si = work.tile([P, G, D], F32, name="si", bufs=1)
+            sa = work.tile([P, G, D], F32, name="sa", bufs=3)
+            sb = work.tile([P, G, D], F32, name="sb", bufs=2)
+            sr = work.tile([P, G, D], F32, name="sr", bufs=5)
+            si = work.tile([P, G, D], F32, name="si", bufs=2)
             nc.scalar.activation(out=sa[:], in_=xr_all[:, sl, :], func=ACT.Square, bias=eps_t[:])
             nc.scalar.activation(out=sb[:], in_=xi_all[:, sl, :], func=ACT.Square, bias=eps_t[:])
             nc.scalar.activation(out=sr[:], in_=xr_all[:, sl, :], func=ACT.Square)
@@ -137,8 +136,8 @@ def tile_quantumcoherencelayer_t_kernel(
             st[("si", s)] = si
 
         def dve_a(s):
-            xc = work.tile([P, G * P], U32, name="xc", bufs=2, align_bytes=64)
-            xs = work.tile([P, G * P], U8, name="xs", bufs=2, align_bytes=64)
+            xc = work.tile([P, G * P], U32, name="xc", bufs=3, align_bytes=64)
+            xs = work.tile([P, G * P], U8, name="xs", bufs=3, align_bytes=64)
             nc.vector.quantize_mx(out=xc[:].bitcast(FP8X4), scales=xs[:], in_=st[("xg", s)][:])
             pts = []
             for tt in range(G):
@@ -190,7 +189,7 @@ def tile_quantumcoherencelayer_t_kernel(
             nc.vector.tensor_scalar(
                 out=gq[:], in0=csum[:], scalar1=ncf[:], scalar2=cfs[:], op0=ALU.mult, op1=ALU.add
             )
-            fr = work.tile([P, G, D], F32, name="fr", bufs=1)
+            fr = work.tile([P, G, D], F32, name="fr", bufs=2)
             for tt in range(G):
                 pt = st[("pt", s)][tt]
                 kk = work.tile([P, D], I32, name="kk", bufs=2)
@@ -205,8 +204,8 @@ def tile_quantumcoherencelayer_t_kernel(
 
         def act_c(s):
             fr = st[("fr", s)]
-            cc = work.tile([P, G, D], F32, name="cc", bufs=1)
-            ss = work.tile([P, G, D], F32, name="ss", bufs=1)
+            cc = work.tile([P, G, D], F32, name="cc", bufs=2)
+            ss = work.tile([P, G, D], F32, name="ss", bufs=2)
             nc.scalar.activation(out=cc[:], in_=fr[:], func=ACT.Abs)
             nc.scalar.activation(out=ss[:], in_=fr[:], func=ACT.Sin, scale=TWO_PI)
             nc.scalar.activation(out=cc[:], in_=cc[:], func=ACT.Sin, scale=-TWO_PI, bias=hpi_t[:])
@@ -216,12 +215,13 @@ def tile_quantumcoherencelayer_t_kernel(
         def dve_c(s):
             sl = slice(G * s, G * s + G)
             q, cc, ss = st[("sr", s)], st[("cc", s)], st[("ss", s)]
-            c0 = work.tile([P, G, D], F32, name="c0", bufs=1)
-            x1 = work.tile([P, G, D], F32, name="x1", bufs=2)
-            x2 = work.tile([P, G, D], F32, name="x2", bufs=2)
+            c0 = work.tile([P, G, D], F32, name="c0", bufs=2)
+            x1 = work.tile([P, G, D], F32, name="x1", bufs=3)
+            x2 = work.tile([P, G, D], F32, name="x2", bufs=3)
             sums = small.tile([P, 2, G], F32, name="sums")
-            nc.vector.tensor_tensor(out=c0[:], in0=xr_all[:, sl, :], in1=q[:], op=ALU.mult)
-            nc.vector.tensor_tensor(out=q[:], in0=xi_all[:, sl, :], in1=q[:], op=ALU.mult)
+            for tt in range(G):
+                nc.gpsimd.tensor_tensor(out=c0[:, tt, :], in0=xr_all[:, G * s + tt, :], in1=q[:, tt, :], op=ALU.mult)
+                nc.gpsimd.tensor_tensor(out=q[:, tt, :], in0=xi_all[:, G * s + tt, :], in1=q[:, tt, :], op=ALU.mult)
             nc.vector.tensor_tensor(out=x1[:], in0=c0[:], in1=cc[:], op=ALU.mult)
             nc.vector.tensor_tensor(out=x2[:], in0=q[:], in1=cc[:], op=ALU.mult)
             nc.vector.tensor_tensor(out=c0[:], in0=c0[:], in1=ss[:], op=ALU.mult)

@@ -41,8 +41,10 @@ def tile_quantumcoherencelayer_t_kernel(
         work = ctx.enter_context(tc.tile_pool(name="work", bufs=1))
         small = ctx.enter_context(tc.tile_pool(name="small", bufs=6))
         ps_keep = ctx.enter_context(tc.psum_pool(name="ps_keep", bufs=1))
-        ps_p = ctx.enter_context(tc.psum_pool(name="ps_p", bufs=4))
-        ps_t = ctx.enter_context(tc.psum_pool(name="ps_t", bufs=2))
+        ps_p = ctx.enter_context(tc.psum_pool(name="ps_p", bufs=2))
+        ps_t = ctx.enter_context(tc.psum_pool(name="ps_t", bufs=1))
+        ps_f = ctx.enter_context(tc.psum_pool(name="ps_f", bufs=2))
+        ps_cs = ctx.enter_context(tc.psum_pool(name="ps_cs", bufs=2))
 
         xr_all = keep.tile([P, NT, D], BF16, name="xr_all", align_bytes=64)
         xi_all = keep.tile([P, NT, D], BF16, name="xi_all", align_bytes=64)
@@ -60,8 +62,9 @@ def tile_quantumcoherencelayer_t_kernel(
         hpi_t = keep.tile([P, 1], F32, name="hpi_t")
         one_t = keep.tile([P, 1], F32, name="one_t")
         mhalf = keep.tile([P, 2 * G], F32, name="mhalf")
-        w_ps = ps_keep.tile([P, D], F32, name="w_ps")
-        b_ps = ps_keep.tile([P, D], F32, name="b_ps")
+        wb_ps = ps_keep.tile([P, 2 * D], BF16, name="wb_ps")
+        w_ps = wb_ps[:, 0:D]
+        b_ps = wb_ps[:, D : 2 * D]
 
         nc.vector.memset(wb_row[:], 0.0)
         nc.vector.memset(ones[:], 1.0)
@@ -92,8 +95,8 @@ def tile_quantumcoherencelayer_t_kernel(
         nc.vector.quantize_mx(
             out=ph_codes[:].bitcast(FP8X4), scales=ph_scales[:], in_=ph_grp[:].rearrange("p n j -> p (n j)")
         )
-        nc.tensor.matmul(out=w_ps[:], lhsT=ones[:], rhs=wb_row[:, 0:D], start=True, stop=True)
-        nc.tensor.matmul(out=b_ps[:], lhsT=ones[:], rhs=wb_row[:, D : 2 * D], start=True, stop=True)
+        nc.tensor.matmul(out=w_ps, lhsT=ones[:], rhs=wb_row[:, 0:D], start=True, stop=True)
+        nc.tensor.matmul(out=b_ps, lhsT=ones[:], rhs=wb_row[:, D : 2 * D], start=True, stop=True)
 
         xr_words = xr_all[:].rearrange("p t d -> p (t d)").bitcast(F32).rearrange(
             "p (t j u) -> p t u j", t=NT, u=2
@@ -184,9 +187,9 @@ def tile_quantumcoherencelayer_t_kernel(
             csq = small.tile([P, 2, G], F32, name="csq")
             csum = small.tile([P, G], F32, name="csum")
             gq = small.tile([P, G], F32, name="gq")
-            nc.vector.tensor_tensor(out=csq[:], in0=coh[:], in1=coh[:], op=ALU.mult)
-            nc.vector.tensor_tensor(out=csum[:], in0=csq[:, 0, :], in1=csq[:, 1, :], op=ALU.add)
-            nc.vector.tensor_scalar(
+            nc.gpsimd.tensor_tensor(out=csq[:], in0=coh[:], in1=coh[:], op=ALU.mult)
+            nc.gpsimd.tensor_tensor(out=csum[:], in0=csq[:, 0, :], in1=csq[:, 1, :], op=ALU.add)
+            nc.gpsimd.tensor_scalar(
                 out=gq[:], in0=csum[:], scalar1=ncf[:], scalar2=cfs[:], op0=ALU.mult, op1=ALU.add
             )
             fr = work.tile([P, G, D], F32, name="fr", bufs=2)
@@ -204,17 +207,24 @@ def tile_quantumcoherencelayer_t_kernel(
 
         def act_c(s):
             fr = st[("fr", s)]
-            cc = work.tile([P, G, D], F32, name="cc", bufs=2)
-            ss = work.tile([P, G, D], F32, name="ss", bufs=2)
-            nc.scalar.activation(out=cc[:], in_=fr[:], func=ACT.Abs)
-            nc.scalar.activation(out=ss[:], in_=fr[:], func=ACT.Sin, scale=TWO_PI)
-            nc.scalar.activation(out=cc[:], in_=cc[:], func=ACT.Sin, scale=-TWO_PI, bias=hpi_t[:])
-            st[("cc", s)] = cc
-            st[("ss", s)] = ss
+            cts, sts = [], []
+            for tt in range(G):
+                ft = ps_f.tile([P, 4, P], F32, name="ft")
+                for c in range(4):
+                    nc.tensor.transpose(ft[:, c, :], fr[:, tt, P * c : P * c + P], ident[:])
+                ct = work.tile([P, 4, P], F32, name="ct", bufs=4)
+                sn = work.tile([P, 4, P], F32, name="sn", bufs=4)
+                nc.scalar.activation(out=ct[:], in_=ft[:], func=ACT.Abs)
+                nc.scalar.activation(out=sn[:], in_=ft[:], func=ACT.Sin, scale=TWO_PI)
+                nc.scalar.activation(out=ct[:], in_=ct[:], func=ACT.Sin, scale=-TWO_PI, bias=hpi_t[:])
+                cts.append(ct)
+                sts.append(sn)
+            st[("ct", s)] = cts
+            st[("sn", s)] = sts
 
         def dve_c(s):
             sl = slice(G * s, G * s + G)
-            q, cc, ss = st[("sr", s)], st[("cc", s)], st[("ss", s)]
+            q = st[("sr", s)]
             c0 = work.tile([P, G, D], F32, name="c0", bufs=2)
             x1 = work.tile([P, G, D], F32, name="x1", bufs=3)
             x2 = work.tile([P, G, D], F32, name="x2", bufs=3)
@@ -222,11 +232,17 @@ def tile_quantumcoherencelayer_t_kernel(
             for tt in range(G):
                 nc.gpsimd.tensor_tensor(out=c0[:, tt, :], in0=xr_all[:, G * s + tt, :], in1=q[:, tt, :], op=ALU.mult)
                 nc.gpsimd.tensor_tensor(out=q[:, tt, :], in0=xi_all[:, G * s + tt, :], in1=q[:, tt, :], op=ALU.mult)
-            nc.vector.tensor_tensor(out=x1[:], in0=c0[:], in1=cc[:], op=ALU.mult)
-            nc.vector.tensor_tensor(out=x2[:], in0=q[:], in1=cc[:], op=ALU.mult)
-            nc.vector.tensor_tensor(out=c0[:], in0=c0[:], in1=ss[:], op=ALU.mult)
-            nc.vector.tensor_tensor(out=q[:], in0=q[:], in1=ss[:], op=ALU.mult)
             for tt in range(G):
+                c_ps = ps_cs.tile([P, D], F32, name="cs_ps")
+                for c in range(4):
+                    nc.tensor.transpose(c_ps[:, P * c : P * c + P], st[("ct", s)][tt][:, c, :], ident[:])
+                nc.vector.tensor_tensor(out=x1[:, tt, :], in0=c0[:, tt, :], in1=c_ps[:], op=ALU.mult)
+                nc.vector.tensor_tensor(out=x2[:, tt, :], in0=q[:, tt, :], in1=c_ps[:], op=ALU.mult)
+                s_ps = ps_cs.tile([P, D], F32, name="cs_ps")
+                for c in range(4):
+                    nc.tensor.transpose(s_ps[:, P * c : P * c + P], st[("sn", s)][tt][:, c, :], ident[:])
+                nc.vector.tensor_tensor(out=c0[:, tt, :], in0=c0[:, tt, :], in1=s_ps[:], op=ALU.mult)
+                nc.vector.tensor_tensor(out=q[:, tt, :], in0=q[:, tt, :], in1=s_ps[:], op=ALU.mult)
                 nc.vector.scalar_tensor_tensor(
                     out=x1[:, tt, :], in0=x1[:, tt, :], scalar=1.0, in1=q[:, tt, :],
                     op0=ALU.mult, op1=ALU.subtract, accum_out=sums[:, 0, tt : tt + 1],
@@ -256,11 +272,11 @@ def tile_quantumcoherencelayer_t_kernel(
             var = small.tile([P, 2, G], F32, name="var")
             vare = small.tile([P, 2, G], F32, name="vare")
             rstd = small.tile([P, 2, G], F32, name="rstd")
-            nc.vector.tensor_scalar(out=mean[:], in0=sums[:], scalar1=1.0 / D, scalar2=None, op0=ALU.mult)
-            nc.vector.tensor_tensor(out=msq[:], in0=mean[:], in1=mean[:], op=ALU.mult)
-            nc.vector.scalar_tensor_tensor(
-                out=var[:], in0=ssq[:], scalar=1.0 / D, in1=msq[:], op0=ALU.mult, op1=ALU.subtract
-            )
+            ex2 = small.tile([P, 2, G], F32, name="ex2")
+            nc.gpsimd.tensor_scalar(out=mean[:], in0=sums[:], scalar1=1.0 / D, scalar2=0.0, op0=ALU.mult, op1=ALU.add)
+            nc.gpsimd.tensor_scalar(out=ex2[:], in0=ssq[:], scalar1=1.0 / D, scalar2=0.0, op0=ALU.mult, op1=ALU.add)
+            nc.gpsimd.tensor_tensor(out=msq[:], in0=mean[:], in1=mean[:], op=ALU.mult)
+            nc.gpsimd.tensor_tensor(out=var[:], in0=ex2[:], in1=msq[:], op=ALU.subtract)
             nc.gpsimd.tensor_scalar(out=vare[:], in0=var[:], scalar1=0.0, scalar2=EPS, op0=ALU.max, op1=ALU.add)
             nc.gpsimd.tensor_tensor(
                 out=rstd[:].rearrange("p o t -> p (o t)"), in0=vare[:].rearrange("p o t -> p (o t)"),
@@ -275,11 +291,11 @@ def tile_quantumcoherencelayer_t_kernel(
             for o, (x, o_d) in enumerate(((st[("x1", s)], or_d), (st[("x2", s)], oi_d))):
                 for tt in range(G):
                     nc.vector.scalar_tensor_tensor(
-                        out=x[:, tt, :], in0=x[:, tt, :], scalar=mean[:, o, tt : tt + 1], in1=w_ps[:],
+                        out=x[:, tt, :], in0=x[:, tt, :], scalar=mean[:, o, tt : tt + 1], in1=w_ps,
                         op0=ALU.subtract, op1=ALU.mult,
                     )
                     nc.vector.scalar_tensor_tensor(
-                        out=x[:, tt, :], in0=x[:, tt, :], scalar=rstd[:, o, tt : tt + 1], in1=b_ps[:],
+                        out=x[:, tt, :], in0=x[:, tt, :], scalar=rstd[:, o, tt : tt + 1], in1=b_ps,
                         op0=ALU.mult, op1=ALU.add,
                     )
                 nc.sync.dma_start(out=o_d[:, sl, :], in_=x[:])

@@ -41,10 +41,8 @@ def tile_quantumcoherencelayer_t_kernel(
         work = ctx.enter_context(tc.tile_pool(name="work", bufs=1))
         small = ctx.enter_context(tc.tile_pool(name="small", bufs=6))
         ps_keep = ctx.enter_context(tc.psum_pool(name="ps_keep", bufs=1))
-        ps_p = ctx.enter_context(tc.psum_pool(name="ps_p", bufs=2))
-        ps_t = ctx.enter_context(tc.psum_pool(name="ps_t", bufs=1))
-        ps_f = ctx.enter_context(tc.psum_pool(name="ps_f", bufs=2))
-        ps_cs = ctx.enter_context(tc.psum_pool(name="ps_cs", bufs=2))
+        ps_p = ctx.enter_context(tc.psum_pool(name="ps_p", bufs=4))
+        ps_t = ctx.enter_context(tc.psum_pool(name="ps_t", bufs=2))
 
         xr_all = keep.tile([P, NT, D], BF16, name="xr_all", align_bytes=64)
         xi_all = keep.tile([P, NT, D], BF16, name="xi_all", align_bytes=64)
@@ -62,9 +60,8 @@ def tile_quantumcoherencelayer_t_kernel(
         hpi_t = keep.tile([P, 1], F32, name="hpi_t")
         one_t = keep.tile([P, 1], F32, name="one_t")
         mhalf = keep.tile([P, 2 * G], F32, name="mhalf")
-        wb_ps = ps_keep.tile([P, 2 * D], BF16, name="wb_ps")
-        w_ps = wb_ps[:, 0:D]
-        b_ps = wb_ps[:, D : 2 * D]
+        w_ps = ps_keep.tile([P, D], F32, name="w_ps")
+        b_ps = ps_keep.tile([P, D], F32, name="b_ps")
 
         nc.vector.memset(wb_row[:], 0.0)
         nc.vector.memset(ones[:], 1.0)
@@ -95,8 +92,8 @@ def tile_quantumcoherencelayer_t_kernel(
         nc.vector.quantize_mx(
             out=ph_codes[:].bitcast(FP8X4), scales=ph_scales[:], in_=ph_grp[:].rearrange("p n j -> p (n j)")
         )
-        nc.tensor.matmul(out=w_ps, lhsT=ones[:], rhs=wb_row[:, 0:D], start=True, stop=True)
-        nc.tensor.matmul(out=b_ps, lhsT=ones[:], rhs=wb_row[:, D : 2 * D], start=True, stop=True)
+        nc.tensor.matmul(out=w_ps[:], lhsT=ones[:], rhs=wb_row[:, 0:D], start=True, stop=True)
+        nc.tensor.matmul(out=b_ps[:], lhsT=ones[:], rhs=wb_row[:, D : 2 * D], start=True, stop=True)
 
         xr_words = xr_all[:].rearrange("p t d -> p (t d)").bitcast(F32).rearrange(
             "p (t j u) -> p t u j", t=NT, u=2
@@ -187,9 +184,9 @@ def tile_quantumcoherencelayer_t_kernel(
             csq = small.tile([P, 2, G], F32, name="csq")
             csum = small.tile([P, G], F32, name="csum")
             gq = small.tile([P, G], F32, name="gq")
-            nc.gpsimd.tensor_tensor(out=csq[:], in0=coh[:], in1=coh[:], op=ALU.mult)
-            nc.gpsimd.tensor_tensor(out=csum[:], in0=csq[:, 0, :], in1=csq[:, 1, :], op=ALU.add)
-            nc.gpsimd.tensor_scalar(
+            nc.vector.tensor_tensor(out=csq[:], in0=coh[:], in1=coh[:], op=ALU.mult)
+            nc.vector.tensor_tensor(out=csum[:], in0=csq[:, 0, :], in1=csq[:, 1, :], op=ALU.add)
+            nc.vector.tensor_scalar(
                 out=gq[:], in0=csum[:], scalar1=ncf[:], scalar2=cfs[:], op0=ALU.mult, op1=ALU.add
             )
             fr = work.tile([P, G, D], F32, name="fr", bufs=2)
@@ -207,42 +204,28 @@ def tile_quantumcoherencelayer_t_kernel(
 
         def act_c(s):
             fr = st[("fr", s)]
-            cts, sts = [], []
-            for tt in range(G):
-                ft = ps_f.tile([P, 4, P], F32, name="ft")
-                for c in range(4):
-                    nc.tensor.transpose(ft[:, c, :], fr[:, tt, P * c : P * c + P], ident[:])
-                ct = work.tile([P, 4, P], F32, name="ct", bufs=4)
-                sn = work.tile([P, 4, P], F32, name="sn", bufs=4)
-                nc.scalar.activation(out=ct[:], in_=ft[:], func=ACT.Abs)
-                nc.scalar.activation(out=sn[:], in_=ft[:], func=ACT.Sin, scale=TWO_PI)
-                nc.scalar.activation(out=ct[:], in_=ct[:], func=ACT.Sin, scale=-TWO_PI, bias=hpi_t[:])
-                cts.append(ct)
-                sts.append(sn)
-            st[("ct", s)] = cts
-            st[("sn", s)] = sts
+            cc = work.tile([P, G, D], F32, name="cc", bufs=2)
+            ss = work.tile([P, G, D], F32, name="ss", bufs=2)
+            nc.scalar.activation(out=cc[:], in_=fr[:], func=ACT.Abs)
+            nc.scalar.activation(out=ss[:], in_=fr[:], func=ACT.Sin, scale=TWO_PI)
+            nc.scalar.activation(out=cc[:], in_=cc[:], func=ACT.Sin, scale=-TWO_PI, bias=hpi_t[:])
+            st[("cc", s)] = cc
+            st[("ss", s)] = ss
 
         def dve_c(s):
             sl = slice(G * s, G * s + G)
-            q = st[("sr", s)]
+            q, cc, ss = st[("sr", s)], st[("cc", s)], st[("ss", s)]
             c0 = work.tile([P, G, D], F32, name="c0", bufs=2)
             x1 = work.tile([P, G, D], F32, name="x1", bufs=3)
             x2 = work.tile([P, G, D], F32, name="x2", bufs=3)
             sums = small.tile([P, 2, G], F32, name="sums")
+            nc.vector.tensor_tensor(out=c0[:], in0=xr_all[:, sl, :], in1=q[:], op=ALU.mult)
+            nc.vector.tensor_tensor(out=q[:], in0=xi_all[:, sl, :], in1=q[:], op=ALU.mult)
+            nc.vector.tensor_tensor(out=x1[:], in0=c0[:], in1=cc[:], op=ALU.mult)
+            nc.vector.tensor_tensor(out=x2[:], in0=q[:], in1=cc[:], op=ALU.mult)
+            nc.vector.tensor_tensor(out=c0[:], in0=c0[:], in1=ss[:], op=ALU.mult)
+            nc.vector.tensor_tensor(out=q[:], in0=q[:], in1=ss[:], op=ALU.mult)
             for tt in range(G):
-                nc.gpsimd.tensor_tensor(out=c0[:, tt, :], in0=xr_all[:, G * s + tt, :], in1=q[:, tt, :], op=ALU.mult)
-                nc.gpsimd.tensor_tensor(out=q[:, tt, :], in0=xi_all[:, G * s + tt, :], in1=q[:, tt, :], op=ALU.mult)
-            for tt in range(G):
-                c_ps = ps_cs.tile([P, D], F32, name="cs_ps")
-                for c in range(4):
-                    nc.tensor.transpose(c_ps[:, P * c : P * c + P], st[("ct", s)][tt][:, c, :], ident[:])
-                nc.vector.tensor_tensor(out=x1[:, tt, :], in0=c0[:, tt, :], in1=c_ps[:], op=ALU.mult)
-                nc.vector.tensor_tensor(out=x2[:, tt, :], in0=q[:, tt, :], in1=c_ps[:], op=ALU.mult)
-                s_ps = ps_cs.tile([P, D], F32, name="cs_ps")
-                for c in range(4):
-                    nc.tensor.transpose(s_ps[:, P * c : P * c + P], st[("sn", s)][tt][:, c, :], ident[:])
-                nc.vector.tensor_tensor(out=c0[:, tt, :], in0=c0[:, tt, :], in1=s_ps[:], op=ALU.mult)
-                nc.vector.tensor_tensor(out=q[:, tt, :], in0=q[:, tt, :], in1=s_ps[:], op=ALU.mult)
                 nc.vector.scalar_tensor_tensor(
                     out=x1[:, tt, :], in0=x1[:, tt, :], scalar=1.0, in1=q[:, tt, :],
                     op0=ALU.mult, op1=ALU.subtract, accum_out=sums[:, 0, tt : tt + 1],
@@ -272,11 +255,11 @@ def tile_quantumcoherencelayer_t_kernel(
             var = small.tile([P, 2, G], F32, name="var")
             vare = small.tile([P, 2, G], F32, name="vare")
             rstd = small.tile([P, 2, G], F32, name="rstd")
-            ex2 = small.tile([P, 2, G], F32, name="ex2")
-            nc.gpsimd.tensor_scalar(out=mean[:], in0=sums[:], scalar1=1.0 / D, scalar2=0.0, op0=ALU.mult, op1=ALU.add)
-            nc.gpsimd.tensor_scalar(out=ex2[:], in0=ssq[:], scalar1=1.0 / D, scalar2=0.0, op0=ALU.mult, op1=ALU.add)
-            nc.gpsimd.tensor_tensor(out=msq[:], in0=mean[:], in1=mean[:], op=ALU.mult)
-            nc.gpsimd.tensor_tensor(out=var[:], in0=ex2[:], in1=msq[:], op=ALU.subtract)
+            nc.vector.tensor_scalar(out=mean[:], in0=sums[:], scalar1=1.0 / D, scalar2=None, op0=ALU.mult)
+            nc.vector.tensor_tensor(out=msq[:], in0=mean[:], in1=mean[:], op=ALU.mult)
+            nc.vector.scalar_tensor_tensor(
+                out=var[:], in0=ssq[:], scalar=1.0 / D, in1=msq[:], op0=ALU.mult, op1=ALU.subtract
+            )
             nc.gpsimd.tensor_scalar(out=vare[:], in0=var[:], scalar1=0.0, scalar2=EPS, op0=ALU.max, op1=ALU.add)
             nc.gpsimd.tensor_tensor(
                 out=rstd[:].rearrange("p o t -> p (o t)"), in0=vare[:].rearrange("p o t -> p (o t)"),
@@ -291,11 +274,11 @@ def tile_quantumcoherencelayer_t_kernel(
             for o, (x, o_d) in enumerate(((st[("x1", s)], or_d), (st[("x2", s)], oi_d))):
                 for tt in range(G):
                     nc.vector.scalar_tensor_tensor(
-                        out=x[:, tt, :], in0=x[:, tt, :], scalar=mean[:, o, tt : tt + 1], in1=w_ps,
+                        out=x[:, tt, :], in0=x[:, tt, :], scalar=mean[:, o, tt : tt + 1], in1=w_ps[:],
                         op0=ALU.subtract, op1=ALU.mult,
                     )
                     nc.vector.scalar_tensor_tensor(
-                        out=x[:, tt, :], in0=x[:, tt, :], scalar=rstd[:, o, tt : tt + 1], in1=b_ps,
+                        out=x[:, tt, :], in0=x[:, tt, :], scalar=rstd[:, o, tt : tt + 1], in1=b_ps[:],
                         op0=ALU.mult, op1=ALU.add,
                     )
                 nc.sync.dma_start(out=o_d[:, sl, :], in_=x[:])

@@ -40,9 +40,10 @@ def tile_quantumcoherencelayer_t_kernel(
         keep = ctx.enter_context(tc.tile_pool(name="keep", bufs=1))
         work = ctx.enter_context(tc.tile_pool(name="work", bufs=1))
         small = ctx.enter_context(tc.tile_pool(name="small", bufs=6))
-        ps_keep = ctx.enter_context(tc.psum_pool(name="ps_keep", bufs=1))
-        ps_p = ctx.enter_context(tc.psum_pool(name="ps_p", bufs=4))
-        ps_t = ctx.enter_context(tc.psum_pool(name="ps_t", bufs=2))
+        ps_p = ctx.enter_context(tc.psum_pool(name="ps_p", bufs=2))
+        ps_t = ctx.enter_context(tc.psum_pool(name="ps_t", bufs=1))
+        ps_d = ctx.enter_context(tc.psum_pool(name="ps_d", bufs=2))
+        ps_y = ctx.enter_context(tc.psum_pool(name="ps_y", bufs=3))
 
         xr_all = keep.tile([P, NT, D], BF16, name="xr_all", align_bytes=64)
         xi_all = keep.tile([P, NT, D], BF16, name="xi_all", align_bytes=64)
@@ -50,7 +51,11 @@ def tile_quantumcoherencelayer_t_kernel(
         ph_grp = keep.tile([P, D, 4], BF16, name="ph_grp", align_bytes=64)
         ph_codes = keep.tile([P, D], U32, name="ph_codes", align_bytes=64)
         ph_scales = keep.tile([P, D], U8, name="ph_scales", align_bytes=64)
-        wb_row = keep.tile([P, 2 * D], BF16, name="wb_row")
+        b_row = keep.tile([P, D], BF16, name="b_row")
+        w_rows = keep.tile([P, P], BF16, name="w_rows")
+        ident_bf = keep.tile([P, P], BF16, name="ident_bf")
+        b_sb = keep.tile([P, D], F32, name="b_sb")
+        w_col = keep.tile([P, 4], F32, name="w_col")
         ones = keep.tile([P, P], BF16, name="ones")
         ident = keep.tile([P, P], F32, name="ident")
         cf_bf = keep.tile([P, 1], BF16, name="cf_bf")
@@ -60,16 +65,16 @@ def tile_quantumcoherencelayer_t_kernel(
         hpi_t = keep.tile([P, 1], F32, name="hpi_t")
         one_t = keep.tile([P, 1], F32, name="one_t")
         mhalf = keep.tile([P, 2 * G], F32, name="mhalf")
-        w_ps = ps_keep.tile([P, D], F32, name="w_ps")
-        b_ps = ps_keep.tile([P, D], F32, name="b_ps")
 
-        nc.vector.memset(wb_row[:], 0.0)
+        nc.vector.memset(b_row[:], 0.0)
+        nc.vector.memset(w_rows[:], 0.0)
         nc.vector.memset(ones[:], 1.0)
         nc.vector.memset(eps_t[:], EPS)
         nc.vector.memset(one_t[:], 1.0)
         nc.vector.tensor_scalar(out=hpi_t[:], in0=one_t[:], scalar1=0.5 * math.pi, scalar2=None, op0=ALU.mult)
         nc.vector.memset(mhalf[:], -0.5)
         make_identity(nc, ident[:])
+        make_identity(nc, ident_bf[:])
 
         def load(s):
             sl = slice(G * s, G * s + G)
@@ -78,8 +83,8 @@ def tile_quantumcoherencelayer_t_kernel(
 
         load(0)
         nc.sync.dma_start(out=ph_raw[:], in_=phase_matrix.rearrange("(p j) n -> p j n", j=4))
-        nc.sync.dma_start(out=wb_row[0:1, 0:D], in_=ln_weight.unsqueeze(0))
-        nc.sync.dma_start(out=wb_row[0:1, D : 2 * D], in_=ln_bias.unsqueeze(0))
+        nc.sync.dma_start(out=w_rows[0:4, :], in_=ln_weight.rearrange("(c j) -> c j", c=4))
+        nc.sync.dma_start(out=b_row[0:1, :], in_=ln_bias.unsqueeze(0))
         nc.sync.dma_start(out=cf_bf[:], in_=coherence_factor.partition_broadcast(P))
         for s in range(1, NG):
             load(s)
@@ -92,8 +97,12 @@ def tile_quantumcoherencelayer_t_kernel(
         nc.vector.quantize_mx(
             out=ph_codes[:].bitcast(FP8X4), scales=ph_scales[:], in_=ph_grp[:].rearrange("p n j -> p (n j)")
         )
-        nc.tensor.matmul(out=w_ps[:], lhsT=ones[:], rhs=wb_row[:, 0:D], start=True, stop=True)
-        nc.tensor.matmul(out=b_ps[:], lhsT=ones[:], rhs=wb_row[:, D : 2 * D], start=True, stop=True)
+        b_ps = ps_y.tile([P, D], F32, name="y_ps")
+        nc.tensor.matmul(out=b_ps[:], lhsT=ones[:], rhs=b_row[:], start=True, stop=True)
+        nc.vector.tensor_copy(out=b_sb[:], in_=b_ps[:])
+        w_ps = ps_d.tile([P, P], BF16, name="d_ps")
+        nc.tensor.transpose(w_ps[:], w_rows[:], ident_bf[:])
+        nc.vector.tensor_copy(out=w_col[:], in_=w_ps[:, 0:4])
 
         xr_words = xr_all[:].rearrange("p t d -> p (t d)").bitcast(F32).rearrange(
             "p (t j u) -> p t u j", t=NT, u=2
@@ -139,6 +148,9 @@ def tile_quantumcoherencelayer_t_kernel(
             xc = work.tile([P, G * P], U32, name="xc", bufs=3, align_bytes=64)
             xs = work.tile([P, G * P], U8, name="xs", bufs=3, align_bytes=64)
             nc.vector.quantize_mx(out=xc[:].bitcast(FP8X4), scales=xs[:], in_=st[("xg", s)][:])
+            sa, sb, sr, si = st[("sa", s)], st[("sb", s)], st[("sr", s)], st[("si", s)]
+            nc.vector.tensor_tensor(out=sa[:], in0=sa[:], in1=sb[:], op=ALU.add)
+            nc.vector.tensor_tensor(out=sr[:], in0=sr[:], in1=si[:], op=ALU.add)
             pts = []
             for tt in range(G):
                 pt = ps_p.tile([P, D], F32, name="pt")
@@ -154,12 +166,6 @@ def tile_quantumcoherencelayer_t_kernel(
                 )
                 pts.append(pt)
             st[("pt", s)] = pts
-
-        def gp_adds(s):
-            sa, sb, sr, si = st[("sa", s)], st[("sb", s)], st[("sr", s)], st[("si", s)]
-            for acc, oth in ((sa, sb), (sr, si)):
-                for tt in range(G):
-                    nc.gpsimd.tensor_tensor(out=acc[:, tt, :], in0=acc[:, tt, :], in1=oth[:, tt, :], op=ALU.add)
 
         def act_b(s):
             sa, sr = st[("sa", s)], st[("sr", s)]
@@ -218,25 +224,32 @@ def tile_quantumcoherencelayer_t_kernel(
             c0 = work.tile([P, G, D], F32, name="c0", bufs=2)
             x1 = work.tile([P, G, D], F32, name="x1", bufs=3)
             x2 = work.tile([P, G, D], F32, name="x2", bufs=3)
-            sums = small.tile([P, 2, G], F32, name="sums")
+            sm = small.tile([P, 2, 2, G], F32, name="sm")
+            msum = small.tile([P, 2, G], F32, name="msum")
+            mean = small.tile([P, 2, G], F32, name="mean")
             nc.vector.tensor_tensor(out=c0[:], in0=xr_all[:, sl, :], in1=q[:], op=ALU.mult)
             nc.vector.tensor_tensor(out=q[:], in0=xi_all[:, sl, :], in1=q[:], op=ALU.mult)
-            nc.vector.tensor_tensor(out=x1[:], in0=c0[:], in1=cc[:], op=ALU.mult)
-            nc.vector.tensor_tensor(out=x2[:], in0=q[:], in1=cc[:], op=ALU.mult)
-            nc.vector.tensor_tensor(out=c0[:], in0=c0[:], in1=ss[:], op=ALU.mult)
-            nc.vector.tensor_tensor(out=q[:], in0=q[:], in1=ss[:], op=ALU.mult)
+            for tt in range(G):
+                for out_t, in_t, sgn, trig, a, o in (
+                    (x1, c0, 1.0, cc, 0, 0), (x2, q, 1.0, cc, 1, 1), (c0, c0, 1.0, ss, 0, 1), (q, q, -1.0, ss, 1, 0),
+                ):
+                    nc.vector.scalar_tensor_tensor(
+                        out=out_t[:, tt, :], in0=in_t[:, tt, :], scalar=sgn, in1=trig[:, tt, :],
+                        op0=ALU.mult, op1=ALU.mult, accum_out=sm[:, a, o, tt : tt + 1],
+                    )
+            nc.vector.tensor_tensor(out=msum[:], in0=sm[:, 0, :, :], in1=sm[:, 1, :, :], op=ALU.add)
+            nc.vector.tensor_scalar(out=mean[:], in0=msum[:], scalar1=1.0 / D, scalar2=None, op0=ALU.mult)
             for tt in range(G):
                 nc.vector.scalar_tensor_tensor(
-                    out=x1[:, tt, :], in0=x1[:, tt, :], scalar=1.0, in1=q[:, tt, :],
-                    op0=ALU.mult, op1=ALU.subtract, accum_out=sums[:, 0, tt : tt + 1],
+                    out=x1[:, tt, :], in0=x1[:, tt, :], scalar=mean[:, 0, tt : tt + 1], in1=q[:, tt, :],
+                    op0=ALU.subtract, op1=ALU.add,
                 )
                 nc.vector.scalar_tensor_tensor(
-                    out=x2[:, tt, :], in0=x2[:, tt, :], scalar=1.0, in1=c0[:, tt, :],
-                    op0=ALU.mult, op1=ALU.add, accum_out=sums[:, 1, tt : tt + 1],
+                    out=x2[:, tt, :], in0=x2[:, tt, :], scalar=mean[:, 1, tt : tt + 1], in1=c0[:, tt, :],
+                    op0=ALU.subtract, op1=ALU.add,
                 )
             st[("x1", s)] = x1
             st[("x2", s)] = x2
-            st[("sums", s)] = sums
 
         def act_d(s):
             ssq = small.tile([P, 2, G], F32, name="ssq")
@@ -249,39 +262,37 @@ def tile_quantumcoherencelayer_t_kernel(
             st[("ssq", s)] = ssq
 
         def stats(s):
-            sums, ssq = st[("sums", s)], st[("ssq", s)]
-            mean = small.tile([P, 2, G], F32, name="mean")
-            msq = small.tile([P, 2, G], F32, name="msq")
-            var = small.tile([P, 2, G], F32, name="var")
+            ssq = st[("ssq", s)]
             vare = small.tile([P, 2, G], F32, name="vare")
             rstd = small.tile([P, 2, G], F32, name="rstd")
-            nc.vector.tensor_scalar(out=mean[:], in0=sums[:], scalar1=1.0 / D, scalar2=None, op0=ALU.mult)
-            nc.vector.tensor_tensor(out=msq[:], in0=mean[:], in1=mean[:], op=ALU.mult)
-            nc.vector.scalar_tensor_tensor(
-                out=var[:], in0=ssq[:], scalar=1.0 / D, in1=msq[:], op0=ALU.mult, op1=ALU.subtract
-            )
-            nc.gpsimd.tensor_scalar(out=vare[:], in0=var[:], scalar1=0.0, scalar2=EPS, op0=ALU.max, op1=ALU.add)
+            nc.gpsimd.tensor_scalar(out=vare[:], in0=ssq[:], scalar1=1.0 / D, scalar2=EPS, op0=ALU.mult, op1=ALU.add)
             nc.gpsimd.tensor_tensor(
                 out=rstd[:].rearrange("p o t -> p (o t)"), in0=vare[:].rearrange("p o t -> p (o t)"),
                 in1=mhalf[:], op=ALU.pow,
             )
-            st[("mean", s)] = mean
             st[("rstd", s)] = rstd
 
         def dve_d(s):
             sl = slice(G * s, G * s + G)
-            mean, rstd = st[("mean", s)], st[("rstd", s)]
-            for o, (x, o_d) in enumerate(((st[("x1", s)], or_d), (st[("x2", s)], oi_d))):
+            rstd = st[("rstd", s)]
+            xs_ = (st[("x1", s)], st[("x2", s)])
+            yt = work.tile([P, 4, 2, G, P], F32, name="yt", bufs=2)
+            for c in range(4):
+                d_ps = ps_d.tile([P, 2, G, P], F32, name="d_ps")
+                for o in range(2):
+                    for tt in range(G):
+                        nc.tensor.transpose(d_ps[:, o, tt, :], xs_[o][:, tt, P * c : P * c + P], ident[:])
+                nc.scalar.activation(out=yt[:, c, :, :, :], in_=d_ps[:], func=ACT.Copy, scale=w_col[:, c : c + 1])
+            for o, o_d in enumerate((or_d, oi_d)):
                 for tt in range(G):
+                    y_ps = ps_y.tile([P, D], F32, name="y_ps")
+                    for c in range(4):
+                        nc.tensor.transpose(y_ps[:, P * c : P * c + P], yt[:, c, o, tt, :], ident[:])
                     nc.vector.scalar_tensor_tensor(
-                        out=x[:, tt, :], in0=x[:, tt, :], scalar=mean[:, o, tt : tt + 1], in1=w_ps[:],
-                        op0=ALU.subtract, op1=ALU.mult,
-                    )
-                    nc.vector.scalar_tensor_tensor(
-                        out=x[:, tt, :], in0=x[:, tt, :], scalar=rstd[:, o, tt : tt + 1], in1=b_ps[:],
+                        out=xs_[o][:, tt, :], in0=y_ps[:], scalar=rstd[:, o, tt : tt + 1], in1=b_sb[:],
                         op0=ALU.mult, op1=ALU.add,
                     )
-                nc.sync.dma_start(out=o_d[:, sl, :], in_=x[:])
+                nc.sync.dma_start(out=o_d[:, sl, :], in_=xs_[o][:])
 
         for i in range(-2, NG):
             if in_range(i + 1):
@@ -297,8 +308,6 @@ def tile_quantumcoherencelayer_t_kernel(
                 dve_b1(i + 1)
             if in_range(i):
                 stats(i)
-            if in_range(i + 2):
-                gp_adds(i + 2)
             if in_range(i + 1):
                 dve_b2(i + 1)
                 act_c(i + 1)

@@ -21,6 +21,8 @@ ROWS = 4096
 NT = ROWS // P
 G = 2
 NG = NT // G
+GA = 4
+NA = NT // GA
 EPS = 1e-8
 TWO_PI = 2.0 * math.pi
 
@@ -47,8 +49,8 @@ def tile_quantumcoherencelayer_t_kernel(
 
         xr_all = keep.tile([P, NT, D], BF16, name="xr_all", align_bytes=64)
         xi_all = keep.tile([P, NT, D], BF16, name="xi_all", align_bytes=64)
-        ph_raw = keep.tile([P, 4, D], BF16, name="ph_raw")
-        ph_grp = keep.tile([P, D, 4], BF16, name="ph_grp", align_bytes=64)
+        ph_raw = work.tile([P, 4, D], BF16, name="ph_raw", tag="yt", bufs=2, align_bytes=64)
+        ph_grp = work.tile([P, D, 4], BF16, name="ph_grp", tag="yt", bufs=2, align_bytes=64)
         ph_codes = keep.tile([P, D], U32, name="ph_codes", align_bytes=64)
         ph_scales = keep.tile([P, D], U8, name="ph_scales", align_bytes=64)
         b_row = keep.tile([P, D], BF16, name="b_row")
@@ -77,7 +79,7 @@ def tile_quantumcoherencelayer_t_kernel(
         make_identity(nc, ident_bf[:])
 
         def load(s):
-            sl = slice(G * s, G * s + G)
+            sl = slice(GA * s, GA * s + GA)
             nc.sync.dma_start(out=xr_all[:, sl, :], in_=xr_d[:, sl, :])
             nc.sync.dma_start(out=xi_all[:, sl, :], in_=xi_d[:, sl, :])
 
@@ -86,7 +88,7 @@ def tile_quantumcoherencelayer_t_kernel(
         nc.sync.dma_start(out=w_rows[0:4, :], in_=ln_weight.rearrange("(c j) -> c j", c=4))
         nc.sync.dma_start(out=b_row[0:1, :], in_=ln_bias.unsqueeze(0))
         nc.sync.dma_start(out=cf_bf[:], in_=coherence_factor.partition_broadcast(P))
-        for s in range(1, NG):
+        for s in range(1, NA):
             load(s)
 
         nc.vector.tensor_copy(out=ph_grp[:], in_=ph_raw[:].rearrange("p j n -> p n j"))
@@ -109,52 +111,63 @@ def tile_quantumcoherencelayer_t_kernel(
         )
 
         st = {}
+        pending = []
 
         def in_range(s):
             return 0 <= s < NG
 
-        def pe_transposes(s):
+        def pe_transposes(a):
             xts = []
-            for h in range(G // 2):
+            for h in range(GA // 2):
                 xt = ps_t.tile([P, 2, 2, P], F32, name="xt")
                 for tt in range(2):
                     for u in range(2):
-                        nc.tensor.transpose(xt[:, tt, u, :], xr_words[:, G * s + 2 * h + tt, u, :], ident[:])
+                        nc.tensor.transpose(xt[:, tt, u, :], xr_words[:, GA * a + 2 * h + tt, u, :], ident[:])
                 xts.append(xt)
-            st[("xt", s)] = xts
+                copy_out(a, h, xt)
 
-        def act_a(s):
-            sl = slice(G * s, G * s + G)
-            xg = work.tile([P, G * P * 4], BF16, name="xg", bufs=3, align_bytes=64)
-            xg_w = xg[:].bitcast(F32).rearrange("p (t r u) -> p t r u", t=G, u=2)
-            for h in range(G // 2):
-                xt = st[("xt", s)][h]
-                nc.scalar.copy(out=xg_w[:, 2 * h : 2 * h + 2, :, :], in_=xt[:].rearrange("p t u r -> p t r u"))
-            sa = work.tile([P, G, D], F32, name="sa", bufs=3)
-            sb = work.tile([P, G, D], F32, name="sb", bufs=2)
-            sr = work.tile([P, G, D], F32, name="sr", bufs=5)
-            si = work.tile([P, G, D], F32, name="si", bufs=2)
+        def copy_out(a, h, xt):
+            if h == 0:
+                st[("xg", a)] = work.tile([P, GA * P * 4], BF16, name="xg", bufs=2, align_bytes=64)
+            xg_w = st[("xg", a)][:].bitcast(F32).rearrange("p (t r u) -> p t r u", t=GA, u=2)
+            nc.scalar.copy(out=xg_w[:, 2 * h : 2 * h + 2, :, :], in_=xt[:].rearrange("p t u r -> p t r u"))
+
+        def act_a(a):
+            sl = slice(GA * a, GA * a + GA)
+            sa = work.tile([P, GA, D], F32, name="sa", bufs=2)
+            sb = work.tile([P, GA, D], F32, name="sb", bufs=1)
+            s1 = work.tile([P, GA, D], F32, name="s1", bufs=1)
+            si = work.tile([P, GA, D], F32, name="si", bufs=1)
+            sr = work.tile([P, GA, D], F32, name="sr", bufs=3)
             nc.scalar.activation(out=sa[:], in_=xr_all[:, sl, :], func=ACT.Square, bias=eps_t[:])
             nc.scalar.activation(out=sb[:], in_=xi_all[:, sl, :], func=ACT.Square, bias=eps_t[:])
-            nc.scalar.activation(out=sr[:], in_=xr_all[:, sl, :], func=ACT.Square)
+            nc.scalar.activation(out=s1[:], in_=xr_all[:, sl, :], func=ACT.Square)
             nc.scalar.activation(out=si[:], in_=xi_all[:, sl, :], func=ACT.Square)
-            st[("xg", s)] = xg
-            st[("sa", s)] = sa
-            st[("sb", s)] = sb
-            st[("sr", s)] = sr
-            st[("si", s)] = si
+            st[("sa", a)] = sa
+            st[("sb", a)] = sb
+            st[("sr", a)] = sr
+            st[("si", a)] = si
+            st[("s1", a)] = s1
+            for tt in range(GA):
+                pending.append((a, tt))
 
-        def dve_a(s):
-            xc = work.tile([P, G * P], U32, name="xc", bufs=3, align_bytes=64)
-            xs = work.tile([P, G * P], U8, name="xs", bufs=3, align_bytes=64)
-            nc.vector.quantize_mx(out=xc[:].bitcast(FP8X4), scales=xs[:], in_=st[("xg", s)][:])
-            sa, sb, sr, si = st[("sa", s)], st[("sb", s)], st[("sr", s)], st[("si", s)]
+        def dve_a(a):
+            xc = work.tile([P, GA * P], U32, name="xc", bufs=2, align_bytes=64)
+            xs = work.tile([P, GA * P], U8, name="xs", bufs=2, align_bytes=64)
+            nc.vector.quantize_mx(out=xc[:].bitcast(FP8X4), scales=xs[:], in_=st[("xg", a)][:])
+            sa, sb = st[("sa", a)], st[("sb", a)]
             nc.vector.tensor_tensor(out=sa[:], in0=sa[:], in1=sb[:], op=ALU.add)
-            nc.vector.tensor_tensor(out=sr[:], in0=sr[:], in1=si[:], op=ALU.add)
+            gp_adds(None, GA)
+            st[("xc", a)] = xc
+            st[("xs", a)] = xs
+
+        def pe_mm(s):
+            a, h = divmod(s, GA // G)
+            xc, xs = st[("xc", a)], st[("xs", a)]
             pts = []
             for tt in range(G):
                 pt = ps_p.tile([P, D], F32, name="pt")
-                cols = slice(P * tt, P * tt + P)
+                cols = slice(P * (G * h + tt), P * (G * h + tt) + P)
                 nc.tensor.matmul_mx(
                     out=pt[:],
                     lhsT=xc[:, cols].bitcast(FP8X4),
@@ -167,13 +180,27 @@ def tile_quantumcoherencelayer_t_kernel(
                 pts.append(pt)
             st[("pt", s)] = pts
 
-        def act_b(s):
-            sa, sr = st[("sa", s)], st[("sr", s)]
-            nc.scalar.activation(out=sa[:], in_=sa[:], func=ACT.Abs_reciprocal_sqrt)
+        def gp_adds(gate, count):
+            for n in range(min(count, len(pending))):
+                a, tt = pending.pop(0)
+                s1, si, sr = st[("s1", a)], st[("si", a)], st[("sr", a)]
+                if gate is not None:
+                    nc.gpsimd.tensor_scalar(
+                        out=sr[:, tt, 0:1], in0=gate, scalar1=1.0, scalar2=0.0, op0=ALU.mult, op1=ALU.add
+                    )
+                nc.gpsimd.tensor_tensor(out=sr[:, tt, :], in0=s1[:, tt, :], in1=si[:, tt, :], op=ALU.add)
+
+        def act_b(a):
+            sa, sr = st[("sa", a)], st[("sr", a)]
             nc.scalar.activation(out=sr[:], in_=sr[:], func=ACT.Abs_reciprocal_sqrt, bias=eps_t[:])
+            nc.scalar.activation(out=sa[:], in_=sa[:], func=ACT.Abs_reciprocal_sqrt)
+
+        def half(name, s):
+            a, h = divmod(s, GA // G)
+            return st[(name, a)][:, G * h : G * h + G, :]
 
         def dve_b1(s):
-            sa = st[("sa", s)]
+            sa = half("sa", s)
             coh = small.tile([P, 2, G], F32, name="coh")
             for tt in range(G):
                 t = G * s + tt
@@ -195,7 +222,9 @@ def tile_quantumcoherencelayer_t_kernel(
             nc.vector.tensor_scalar(
                 out=gq[:], in0=csum[:], scalar1=ncf[:], scalar2=cfs[:], op0=ALU.mult, op1=ALU.add
             )
+            gp_adds(gq[:, 0:1], GA // 2)
             fr = work.tile([P, G, D], F32, name="fr", bufs=2)
+            pe_mm(s)
             for tt in range(G):
                 pt = st[("pt", s)][tt]
                 kk = work.tile([P, D], I32, name="kk", bufs=2)
@@ -220,15 +249,15 @@ def tile_quantumcoherencelayer_t_kernel(
 
         def dve_c(s):
             sl = slice(G * s, G * s + G)
-            q, cc, ss = st[("sr", s)], st[("cc", s)], st[("ss", s)]
+            q, cc, ss = half("sr", s), st[("cc", s)], st[("ss", s)]
             c0 = work.tile([P, G, D], F32, name="c0", bufs=2)
             x1 = work.tile([P, G, D], F32, name="x1", bufs=3)
             x2 = work.tile([P, G, D], F32, name="x2", bufs=3)
             sm = small.tile([P, 2, 2, G], F32, name="sm")
             msum = small.tile([P, 2, G], F32, name="msum")
             mean = small.tile([P, 2, G], F32, name="mean")
-            nc.vector.tensor_tensor(out=c0[:], in0=xr_all[:, sl, :], in1=q[:], op=ALU.mult)
-            nc.vector.tensor_tensor(out=q[:], in0=xi_all[:, sl, :], in1=q[:], op=ALU.mult)
+            nc.vector.tensor_tensor(out=c0[:], in0=xr_all[:, sl, :], in1=q, op=ALU.mult)
+            nc.vector.tensor_tensor(out=q, in0=xi_all[:, sl, :], in1=q, op=ALU.mult)
             for tt in range(G):
                 for out_t, in_t, sgn, trig, a, o in (
                     (x1, c0, 1.0, cc, 0, 0), (x2, q, 1.0, cc, 1, 1), (c0, c0, 1.0, ss, 0, 1), (q, q, -1.0, ss, 1, 0),
@@ -255,7 +284,7 @@ def tile_quantumcoherencelayer_t_kernel(
             ssq = small.tile([P, 2, G], F32, name="ssq")
             for tt in range(G):
                 for o, x in enumerate((st[("x1", s)], st[("x2", s)])):
-                    junk = work.tile([P, D], F32, name="ajunk", bufs=2)
+                    junk = work.tile([P, D], BF16, name="ajunk", bufs=2)
                     nc.scalar.activation(
                         out=junk[:], in_=x[:, tt, :], func=ACT.Square, accum_out=ssq[:, o, tt : tt + 1]
                     )
@@ -276,7 +305,7 @@ def tile_quantumcoherencelayer_t_kernel(
             sl = slice(G * s, G * s + G)
             rstd = st[("rstd", s)]
             xs_ = (st[("x1", s)], st[("x2", s)])
-            yt = work.tile([P, 4, 2, G, P], F32, name="yt", bufs=2)
+            yt = work.tile([P, 4, 2, G, P], F32, name="yt", tag="yt", bufs=2, align_bytes=64)
             for c in range(4):
                 d_ps = ps_d.tile([P, 2, G, P], F32, name="d_ps")
                 for o in range(2):
@@ -294,22 +323,28 @@ def tile_quantumcoherencelayer_t_kernel(
                     )
                 nc.sync.dma_start(out=o_d[:, sl, :], in_=xs_[o][:])
 
-        for i in range(-2, NG):
-            if in_range(i + 1):
-                dve_a(i + 1)
-                act_b(i + 1)
-            if in_range(i + 2):
-                pe_transposes(i + 2)
-                act_a(i + 2)
-            if in_range(i):
-                dve_c(i)
-                act_d(i)
-            if in_range(i + 1):
-                dve_b1(i + 1)
-            if in_range(i):
-                stats(i)
-            if in_range(i + 1):
-                dve_b2(i + 1)
-                act_c(i + 1)
-            if in_range(i):
-                dve_d(i)
+        def in_range_a(a):
+            return 0 <= a < NA
+
+        def round_b(s):
+            if in_range(s + 1):
+                dve_b1(s + 1)
+            if in_range(s):
+                dve_c(s)
+                act_d(s)
+            if in_range(s + 1):
+                dve_b2(s + 1)
+                act_c(s + 1)
+            if in_range(s):
+                stats(s)
+                dve_d(s)
+
+        for j in range(-2, NA):
+            round_b(2 * j)
+            if in_range_a(j + 1):
+                dve_a(j + 1)
+                act_b(j + 1)
+            if in_range_a(j + 2):
+                pe_transposes(j + 2)
+                act_a(j + 2)
+            round_b(2 * j + 1)

@@ -47,10 +47,8 @@ def tile_quantumcoherencelayer_t_kernel(
         ps_d = ctx.enter_context(tc.psum_pool(name="ps_d", bufs=2))
         ps_y = ctx.enter_context(tc.psum_pool(name="ps_y", bufs=3))
 
-        xr_all = keep.tile([P, NT, D], BF16, name="xr_all", align_bytes=64)
-        xi_all = keep.tile([P, NT, D], BF16, name="xi_all", align_bytes=64)
-        ph_raw = work.tile([P, 4, D], BF16, name="ph_raw", tag="yt", bufs=2, align_bytes=64)
-        ph_grp = work.tile([P, D, 4], BF16, name="ph_grp", tag="yt", bufs=2, align_bytes=64)
+        ph_raw = work.tile([P, 4, D], BF16, name="ph_raw", tag="yt", bufs=3, align_bytes=64)
+        ph_grp = work.tile([P, D, 4], BF16, name="ph_grp", tag="yt", bufs=3, align_bytes=64)
         ph_codes = keep.tile([P, D], U32, name="ph_codes", align_bytes=64)
         ph_scales = keep.tile([P, D], U8, name="ph_scales", align_bytes=64)
         b_row = keep.tile([P, D], BF16, name="b_row")
@@ -78,18 +76,25 @@ def tile_quantumcoherencelayer_t_kernel(
         make_identity(nc, ident[:])
         make_identity(nc, ident_bf[:])
 
-        def load(s):
-            sl = slice(GA * s, GA * s + GA)
-            nc.sync.dma_start(out=xr_all[:, sl, :], in_=xr_d[:, sl, :])
-            nc.sync.dma_start(out=xi_all[:, sl, :], in_=xi_d[:, sl, :])
+        st = {}
+        pending = []
+
+        def load(a):
+            sl = slice(GA * a, GA * a + GA)
+            xr = work.tile([P, GA, D], BF16, name="xr", bufs=4, align_bytes=64)
+            xi = work.tile([P, GA, D], BF16, name="xi", bufs=4, align_bytes=64)
+            nc.sync.dma_start(out=xr[:], in_=xr_d[:, sl, :])
+            nc.sync.dma_start(out=xi[:], in_=xi_d[:, sl, :])
+            st[("xr", a)] = xr
+            st[("xi", a)] = xi
 
         load(0)
         nc.sync.dma_start(out=ph_raw[:], in_=phase_matrix.rearrange("(p j) n -> p j n", j=4))
         nc.sync.dma_start(out=w_rows[0:4, :], in_=ln_weight.rearrange("(c j) -> c j", c=4))
         nc.sync.dma_start(out=b_row[0:1, :], in_=ln_bias.unsqueeze(0))
         nc.sync.dma_start(out=cf_bf[:], in_=coherence_factor.partition_broadcast(P))
-        for s in range(1, NA):
-            load(s)
+        load(1)
+        load(2)
 
         nc.vector.tensor_copy(out=ph_grp[:], in_=ph_raw[:].rearrange("p j n -> p n j"))
         nc.vector.tensor_scalar(out=cfs[:], in0=cf_bf[:], scalar1=1.0 / TWO_PI, scalar2=None, op0=ALU.mult)
@@ -106,24 +111,19 @@ def tile_quantumcoherencelayer_t_kernel(
         nc.tensor.transpose(w_ps[:], w_rows[:], ident_bf[:])
         nc.vector.tensor_copy(out=w_col[:], in_=w_ps[:, 0:4])
 
-        xr_words = xr_all[:].rearrange("p t d -> p (t d)").bitcast(F32).rearrange(
-            "p (t j u) -> p t u j", t=NT, u=2
-        )
-
-        st = {}
-        pending = []
 
         def in_range(s):
             return 0 <= s < NG
 
         def pe_transposes(a):
-            xts = []
+            xr_words = st[("xr", a)][:].rearrange("p t d -> p (t d)").bitcast(F32).rearrange(
+                "p (t j u) -> p t u j", t=GA, u=2
+            )
             for h in range(GA // 2):
                 xt = ps_t.tile([P, 2, 2, P], F32, name="xt")
                 for tt in range(2):
                     for u in range(2):
-                        nc.tensor.transpose(xt[:, tt, u, :], xr_words[:, GA * a + 2 * h + tt, u, :], ident[:])
-                xts.append(xt)
+                        nc.tensor.transpose(xt[:, tt, u, :], xr_words[:, 2 * h + tt, u, :], ident[:])
                 copy_out(a, h, xt)
 
         def copy_out(a, h, xt):
@@ -133,22 +133,22 @@ def tile_quantumcoherencelayer_t_kernel(
             nc.scalar.copy(out=xg_w[:, 2 * h : 2 * h + 2, :, :], in_=xt[:].rearrange("p t u r -> p t r u"))
 
         def act_a(a):
-            sl = slice(GA * a, GA * a + GA)
+            xr, xi = st[("xr", a)], st[("xi", a)]
             sa = work.tile([P, GA, D], F32, name="sa", bufs=2)
             sb = work.tile([P, GA, D], F32, name="sb", bufs=1)
             s1 = work.tile([P, GA, D], F32, name="s1", bufs=1)
             si = work.tile([P, GA, D], F32, name="si", bufs=1)
             sr = work.tile([P, GA, D], F32, name="sr", bufs=3)
-            nc.scalar.activation(out=sa[:], in_=xr_all[:, sl, :], func=ACT.Square, bias=eps_t[:])
-            nc.scalar.activation(out=sb[:], in_=xi_all[:, sl, :], func=ACT.Square, bias=eps_t[:])
-            nc.scalar.activation(out=s1[:], in_=xr_all[:, sl, :], func=ACT.Square)
-            nc.scalar.activation(out=si[:], in_=xi_all[:, sl, :], func=ACT.Square)
+            nc.scalar.activation(out=sa[:], in_=xr[:], func=ACT.Square, bias=eps_t[:])
+            nc.scalar.activation(out=sb[:], in_=xi[:], func=ACT.Square, bias=eps_t[:])
+            nc.scalar.activation(out=s1[:], in_=xr[:], func=ACT.Square)
+            nc.scalar.activation(out=si[:], in_=xi[:], func=ACT.Square)
             st[("sa", a)] = sa
             st[("sb", a)] = sb
             st[("sr", a)] = sr
             st[("si", a)] = si
             st[("s1", a)] = s1
-            for tt in range(GA):
+            for tt in range(0, GA, G):
                 pending.append((a, tt))
 
         def dve_a(a):
@@ -188,7 +188,9 @@ def tile_quantumcoherencelayer_t_kernel(
                     nc.gpsimd.tensor_scalar(
                         out=sr[:, tt, 0:1], in0=gate, scalar1=1.0, scalar2=0.0, op0=ALU.mult, op1=ALU.add
                     )
-                nc.gpsimd.tensor_tensor(out=sr[:, tt, :], in0=s1[:, tt, :], in1=si[:, tt, :], op=ALU.add)
+                nc.gpsimd.tensor_tensor(
+                    out=sr[:, tt : tt + G, :], in0=s1[:, tt : tt + G, :], in1=si[:, tt : tt + G, :], op=ALU.add
+                )
 
         def act_b(a):
             sa, sr = st[("sa", a)], st[("sr", a)]
@@ -203,11 +205,10 @@ def tile_quantumcoherencelayer_t_kernel(
             sa = half("sa", s)
             coh = small.tile([P, 2, G], F32, name="coh")
             for tt in range(G):
-                t = G * s + tt
-                for o, x_all in enumerate((xr_all, xi_all)):
+                for o, x_h in enumerate((half("xr", s), half("xi", s))):
                     junk = work.tile([P, D], F32, name="vjunk", bufs=2)
                     nc.vector.scalar_tensor_tensor(
-                        out=junk[:], in0=x_all[:, t, :], scalar=EPS, in1=sa[:, tt, :],
+                        out=junk[:], in0=x_h[:, tt, :], scalar=EPS, in1=sa[:, tt, :],
                         op0=ALU.add, op1=ALU.mult, accum_out=coh[:, o, tt : tt + 1],
                     )
             st[("coh", s)] = coh
@@ -222,7 +223,7 @@ def tile_quantumcoherencelayer_t_kernel(
             nc.vector.tensor_scalar(
                 out=gq[:], in0=csum[:], scalar1=ncf[:], scalar2=cfs[:], op0=ALU.mult, op1=ALU.add
             )
-            gp_adds(gq[:, 0:1], GA // 2)
+            gp_adds(gq[:, 0:1], 1)
             fr = work.tile([P, G, D], F32, name="fr", bufs=2)
             pe_mm(s)
             for tt in range(G):
@@ -251,13 +252,13 @@ def tile_quantumcoherencelayer_t_kernel(
             sl = slice(G * s, G * s + G)
             q, cc, ss = half("sr", s), st[("cc", s)], st[("ss", s)]
             c0 = work.tile([P, G, D], F32, name="c0", bufs=2)
-            x1 = work.tile([P, G, D], F32, name="x1", bufs=3)
-            x2 = work.tile([P, G, D], F32, name="x2", bufs=3)
+            x1 = work.tile([P, G, D], F32, name="x1", bufs=4)
+            x2 = work.tile([P, G, D], F32, name="x2", bufs=4)
             sm = small.tile([P, 2, 2, G], F32, name="sm")
             msum = small.tile([P, 2, G], F32, name="msum")
             mean = small.tile([P, 2, G], F32, name="mean")
-            nc.vector.tensor_tensor(out=c0[:], in0=xr_all[:, sl, :], in1=q, op=ALU.mult)
-            nc.vector.tensor_tensor(out=q, in0=xi_all[:, sl, :], in1=q, op=ALU.mult)
+            nc.vector.tensor_tensor(out=c0[:], in0=half("xr", s), in1=q, op=ALU.mult)
+            nc.vector.tensor_tensor(out=q, in0=half("xi", s), in1=q, op=ALU.mult)
             for tt in range(G):
                 for out_t, in_t, sgn, trig, a, o in (
                     (x1, c0, 1.0, cc, 0, 0), (x2, q, 1.0, cc, 1, 1), (c0, c0, 1.0, ss, 0, 1), (q, q, -1.0, ss, 1, 0),
@@ -301,17 +302,21 @@ def tile_quantumcoherencelayer_t_kernel(
             )
             st[("rstd", s)] = rstd
 
-        def dve_d(s):
-            sl = slice(G * s, G * s + G)
-            rstd = st[("rstd", s)]
+        def d_mid(s):
             xs_ = (st[("x1", s)], st[("x2", s)])
-            yt = work.tile([P, 4, 2, G, P], F32, name="yt", tag="yt", bufs=2, align_bytes=64)
+            yt = work.tile([P, 4, 2, G, P], F32, name="yt", tag="yt", bufs=3, align_bytes=64)
             for c in range(4):
                 d_ps = ps_d.tile([P, 2, G, P], F32, name="d_ps")
                 for o in range(2):
                     for tt in range(G):
                         nc.tensor.transpose(d_ps[:, o, tt, :], xs_[o][:, tt, P * c : P * c + P], ident[:])
                 nc.scalar.activation(out=yt[:, c, :, :, :], in_=d_ps[:], func=ACT.Copy, scale=w_col[:, c : c + 1])
+            st[("yt", s)] = yt
+
+        def d_fin(s):
+            sl = slice(G * s, G * s + G)
+            rstd, yt = st[("rstd", s)], st[("yt", s)]
+            xs_ = (st[("x1", s)], st[("x2", s)])
             for o, o_d in enumerate((or_d, oi_d)):
                 for tt in range(G):
                     y_ps = ps_y.tile([P, D], F32, name="y_ps")
@@ -332,18 +337,23 @@ def tile_quantumcoherencelayer_t_kernel(
             if in_range(s):
                 dve_c(s)
                 act_d(s)
+                d_mid(s)
             if in_range(s + 1):
                 dve_b2(s + 1)
+            if in_range(s - 1):
+                d_fin(s - 1)
+            if in_range(s + 1):
                 act_c(s + 1)
             if in_range(s):
                 stats(s)
-                dve_d(s)
 
-        for j in range(-2, NA):
+        for j in range(-2, NA + 1):
             round_b(2 * j)
             if in_range_a(j + 1):
                 dve_a(j + 1)
                 act_b(j + 1)
+            if j >= 0 and in_range_a(j + 3):
+                load(j + 3)
             if in_range_a(j + 2):
                 pe_transposes(j + 2)
                 act_a(j + 2)

@@ -14,6 +14,7 @@ U8 = mybir.dt.uint8
 FP8X4 = mybir.dt.float8_e4m3fn_x4
 ALU = mybir.AluOpType
 ACT = mybir.ActivationFunctionType
+ENG = mybir.EngineType
 
 P = 128
 D = 512
@@ -21,10 +22,9 @@ ROWS = 4096
 NT = ROWS // P
 G = 2
 NG = NT // G
-GA = 4
-NA = NT // GA
 EPS = 1e-8
 TWO_PI = 2.0 * math.pi
+LOADS_AHEAD = 6
 
 FLOPS = 2 * ROWS * D * D
 
@@ -47,8 +47,8 @@ def tile_quantumcoherencelayer_t_kernel(
         ps_d = ctx.enter_context(tc.psum_pool(name="ps_d", bufs=2))
         ps_y = ctx.enter_context(tc.psum_pool(name="ps_y", bufs=3))
 
-        ph_raw = work.tile([P, 4, D], BF16, name="ph_raw", tag="yt", bufs=3, align_bytes=64)
-        ph_grp = work.tile([P, D, 4], BF16, name="ph_grp", tag="yt", bufs=3, align_bytes=64)
+        ph_raw = work.tile([P, 4, D], BF16, name="ph_raw", tag="yt", bufs=2, align_bytes=64)
+        ph_grp = work.tile([P, D, 4], BF16, name="ph_grp", tag="yt", bufs=2, align_bytes=64)
         ph_codes = keep.tile([P, D], U32, name="ph_codes", align_bytes=64)
         ph_scales = keep.tile([P, D], U8, name="ph_scales", align_bytes=64)
         b_row = keep.tile([P, D], BF16, name="b_row")
@@ -77,24 +77,23 @@ def tile_quantumcoherencelayer_t_kernel(
         make_identity(nc, ident_bf[:])
 
         st = {}
-        pending = []
 
-        def load(a):
-            sl = slice(GA * a, GA * a + GA)
-            xr = work.tile([P, GA, D], BF16, name="xr", bufs=4, align_bytes=64)
-            xi = work.tile([P, GA, D], BF16, name="xi", bufs=4, align_bytes=64)
+        def load(g):
+            sl = slice(G * g, G * g + G)
+            xr = work.tile([P, G, D], BF16, name="xr", bufs=LOADS_AHEAD, align_bytes=64)
+            xi = work.tile([P, G, D], BF16, name="xi", bufs=LOADS_AHEAD, align_bytes=64)
             nc.sync.dma_start(out=xr[:], in_=xr_d[:, sl, :])
             nc.sync.dma_start(out=xi[:], in_=xi_d[:, sl, :])
-            st[("xr", a)] = xr
-            st[("xi", a)] = xi
+            st[("xr", g)] = xr
+            st[("xi", g)] = xi
 
         load(0)
         nc.sync.dma_start(out=ph_raw[:], in_=phase_matrix.rearrange("(p j) n -> p j n", j=4))
         nc.sync.dma_start(out=w_rows[0:4, :], in_=ln_weight.rearrange("(c j) -> c j", c=4))
         nc.sync.dma_start(out=b_row[0:1, :], in_=ln_bias.unsqueeze(0))
         nc.sync.dma_start(out=cf_bf[:], in_=coherence_factor.partition_broadcast(P))
-        load(1)
-        load(2)
+        for g in range(1, LOADS_AHEAD):
+            load(g)
 
         nc.vector.tensor_copy(out=ph_grp[:], in_=ph_raw[:].rearrange("p j n -> p n j"))
         nc.vector.tensor_scalar(out=cfs[:], in0=cf_bf[:], scalar1=1.0 / TWO_PI, scalar2=None, op0=ALU.mult)
@@ -111,63 +110,67 @@ def tile_quantumcoherencelayer_t_kernel(
         nc.tensor.transpose(w_ps[:], w_rows[:], ident_bf[:])
         nc.vector.tensor_copy(out=w_col[:], in_=w_ps[:, 0:4])
 
+        def ok(g):
+            return 0 <= g < NG
 
-        def in_range(s):
-            return 0 <= s < NG
-
-        def pe_transposes(a):
-            xr_words = st[("xr", a)][:].rearrange("p t d -> p (t d)").bitcast(F32).rearrange(
-                "p (t j u) -> p t u j", t=GA, u=2
-            )
-            for h in range(GA // 2):
-                xt = ps_t.tile([P, 2, 2, P], F32, name="xt")
-                for tt in range(2):
-                    for u in range(2):
-                        nc.tensor.transpose(xt[:, tt, u, :], xr_words[:, 2 * h + tt, u, :], ident[:])
-                copy_out(a, h, xt)
-
-        def copy_out(a, h, xt):
-            if h == 0:
-                st[("xg", a)] = work.tile([P, GA * P * 4], BF16, name="xg", bufs=2, align_bytes=64)
-            xg_w = st[("xg", a)][:].bitcast(F32).rearrange("p (t r u) -> p t r u", t=GA, u=2)
-            nc.scalar.copy(out=xg_w[:, 2 * h : 2 * h + 2, :, :], in_=xt[:].rearrange("p t u r -> p t r u"))
-
-        def act_a(a):
-            xr, xi = st[("xr", a)], st[("xi", a)]
-            sa = work.tile([P, GA, D], F32, name="sa", bufs=2)
-            sb = work.tile([P, GA, D], F32, name="sb", bufs=1)
-            s1 = work.tile([P, GA, D], F32, name="s1", bufs=1)
-            si = work.tile([P, GA, D], F32, name="si", bufs=1)
-            sr = work.tile([P, GA, D], F32, name="sr", bufs=3)
-            nc.scalar.activation(out=sa[:], in_=xr[:], func=ACT.Square, bias=eps_t[:])
-            nc.scalar.activation(out=sb[:], in_=xi[:], func=ACT.Square, bias=eps_t[:])
+        def squares(g):
+            xr, xi = st[("xr", g)], st[("xi", g)]
+            s1 = work.tile([P, G, D], F32, name="s1", bufs=2)
+            si = work.tile([P, G, D], F32, name="si", bufs=2)
+            sa = work.tile([P, G, D], F32, name="sa", bufs=5)
+            sb = work.tile([P, G, D], F32, name="sb", bufs=2)
             nc.scalar.activation(out=s1[:], in_=xr[:], func=ACT.Square)
             nc.scalar.activation(out=si[:], in_=xi[:], func=ACT.Square)
-            st[("sa", a)] = sa
-            st[("sb", a)] = sb
-            st[("sr", a)] = sr
-            st[("si", a)] = si
-            st[("s1", a)] = s1
-            for tt in range(0, GA, G):
-                pending.append((a, tt))
+            nc.scalar.activation(out=sa[:], in_=xr[:], func=ACT.Square, bias=eps_t[:])
+            nc.scalar.activation(out=sb[:], in_=xi[:], func=ACT.Square, bias=eps_t[:])
+            st[("s1", g)] = s1
+            st[("si", g)] = si
+            st[("sa", g)] = sa
+            st[("sb", g)] = sb
 
-        def dve_a(a):
-            xc = work.tile([P, GA * P], U32, name="xc", bufs=2, align_bytes=64)
-            xs = work.tile([P, GA * P], U8, name="xs", bufs=2, align_bytes=64)
-            nc.vector.quantize_mx(out=xc[:].bitcast(FP8X4), scales=xs[:], in_=st[("xg", a)][:])
-            sa, sb = st[("sa", a)], st[("sb", a)]
+        def square_sum(g):
+            sr = work.tile([P, G, D], F32, name="sr", bufs=5)
+            nc.gpsimd.tensor_tensor(out=sr[:], in0=st[("s1", g)][:], in1=st[("si", g)][:], op=ALU.add)
+            st[("sr", g)] = sr
+
+        def eps_sum(g):
+            sa, sb = st[("sa", g)], st[("sb", g)]
             nc.vector.tensor_tensor(out=sa[:], in0=sa[:], in1=sb[:], op=ALU.add)
-            gp_adds(None, GA)
-            st[("xc", a)] = xc
-            st[("xs", a)] = xs
 
-        def pe_mm(s):
-            a, h = divmod(s, GA // G)
-            xc, xs = st[("xc", a)], st[("xs", a)]
+        def roots(gs):
+            for g in gs:
+                sa = st[("sa", g)]
+                nc.scalar.activation(out=sa[:], in_=sa[:], func=ACT.Abs_reciprocal_sqrt)
+            for g in gs:
+                sr = st[("sr", g)]
+                nc.scalar.activation(out=sr[:], in_=sr[:], func=ACT.Abs_reciprocal_sqrt, bias=eps_t[:])
+
+        def x_transposes(g):
+            xr_words = st[("xr", g)][:].rearrange("p t d -> p (t d)").bitcast(F32).rearrange(
+                "p (t j u) -> p t u j", t=G, u=2
+            )
+            xt = ps_t.tile([P, G, 2, P], F32, name="xt")
+            for tt in range(G):
+                for u in range(2):
+                    nc.tensor.transpose(xt[:, tt, u, :], xr_words[:, tt, u, :], ident[:])
+            xg = work.tile([P, G * P * 4], BF16, name="xg", bufs=2, align_bytes=64)
+            xg_w = xg[:].bitcast(F32).rearrange("p (t r u) -> p t r u", t=G, u=2)
+            nc.scalar.copy(out=xg_w, in_=xt[:].rearrange("p t u r -> p t r u"))
+            st[("xg", g)] = xg
+
+        def quantise(g):
+            xc = work.tile([P, G * P], U32, name="xc", bufs=3, align_bytes=64)
+            xs = work.tile([P, G * P], U8, name="xs", bufs=3, align_bytes=64)
+            nc.vector.quantize_mx(out=xc[:].bitcast(FP8X4), scales=xs[:], in_=st[("xg", g)][:])
+            st[("xc", g)] = xc
+            st[("xs", g)] = xs
+
+        def pe_mm(g):
+            xc, xs = st[("xc", g)], st[("xs", g)]
             pts = []
             for tt in range(G):
                 pt = ps_p.tile([P, D], F32, name="pt")
-                cols = slice(P * (G * h + tt), P * (G * h + tt) + P)
+                cols = slice(P * tt, P * tt + P)
                 nc.tensor.matmul_mx(
                     out=pt[:],
                     lhsT=xc[:, cols].bitcast(FP8X4),
@@ -178,97 +181,99 @@ def tile_quantumcoherencelayer_t_kernel(
                     stop=True,
                 )
                 pts.append(pt)
-            st[("pt", s)] = pts
+            st[("pt", g)] = pts
 
-        def gp_adds(gate, count):
-            for n in range(min(count, len(pending))):
-                a, tt = pending.pop(0)
-                s1, si, sr = st[("s1", a)], st[("si", a)], st[("sr", a)]
-                if gate is not None:
-                    nc.gpsimd.tensor_scalar(
-                        out=sr[:, tt, 0:1], in0=gate, scalar1=1.0, scalar2=0.0, op0=ALU.mult, op1=ALU.add
-                    )
-                nc.gpsimd.tensor_tensor(
-                    out=sr[:, tt : tt + G, :], in0=s1[:, tt : tt + G, :], in1=si[:, tt : tt + G, :], op=ALU.add
-                )
-
-        def act_b(a):
-            sa, sr = st[("sa", a)], st[("sr", a)]
-            nc.scalar.activation(out=sr[:], in_=sr[:], func=ACT.Abs_reciprocal_sqrt, bias=eps_t[:])
-            nc.scalar.activation(out=sa[:], in_=sa[:], func=ACT.Abs_reciprocal_sqrt)
-
-        def half(name, s):
-            a, h = divmod(s, GA // G)
-            return st[(name, a)][:, G * h : G * h + G, :]
-
-        def dve_b1(s):
-            sa = half("sa", s)
+        def coh_sums(g):
+            sa = st[("sa", g)]
             coh = small.tile([P, 2, G], F32, name="coh")
             for tt in range(G):
-                for o, x_h in enumerate((half("xr", s), half("xi", s))):
+                for o, x_h in enumerate((st[("xr", g)], st[("xi", g)])):
                     junk = work.tile([P, D], F32, name="vjunk", bufs=2)
                     nc.vector.scalar_tensor_tensor(
                         out=junk[:], in0=x_h[:, tt, :], scalar=EPS, in1=sa[:, tt, :],
                         op0=ALU.add, op1=ALU.mult, accum_out=coh[:, o, tt : tt + 1],
                     )
-            st[("coh", s)] = coh
+            st[("coh", g)] = coh
 
-        def dve_b2(s):
-            coh = st[("coh", s)]
+        def gain_a(g):
+            coh = st[("coh", g)]
             csq = small.tile([P, 2, G], F32, name="csq")
-            csum = small.tile([P, G], F32, name="csum")
-            gq = small.tile([P, G], F32, name="gq")
             nc.vector.tensor_tensor(out=csq[:], in0=coh[:], in1=coh[:], op=ALU.mult)
+            st[("csq", g)] = csq
+
+        def gain_b(g):
+            csq = st[("csq", g)]
+            csum = small.tile([P, G], F32, name="csum")
             nc.vector.tensor_tensor(out=csum[:], in0=csq[:, 0, :], in1=csq[:, 1, :], op=ALU.add)
+            st[("csum", g)] = csum
+
+        def gain_c(g):
+            gq = small.tile([P, G], F32, name="gq")
             nc.vector.tensor_scalar(
-                out=gq[:], in0=csum[:], scalar1=ncf[:], scalar2=cfs[:], op0=ALU.mult, op1=ALU.add
+                out=gq[:], in0=st[("csum", g)][:], scalar1=ncf[:], scalar2=cfs[:], op0=ALU.mult, op1=ALU.add
             )
-            gp_adds(gq[:, 0:1], 1)
+            st[("gq", g)] = gq
+
+        def reduce_range(g):
+            gq, pts = st[("gq", g)], st[("pt", g)]
             fr = work.tile([P, G, D], F32, name="fr", bufs=2)
-            pe_mm(s)
+            kks = []
             for tt in range(G):
-                pt = st[("pt", s)][tt]
                 kk = work.tile([P, D], I32, name="kk", bufs=2)
                 nc.vector.tensor_scalar(
-                    out=kk[:], in0=pt[:], scalar1=gq[:, tt : tt + 1], scalar2=None, op0=ALU.mult
+                    out=kk[:], in0=pts[tt][:], scalar1=gq[:, tt : tt + 1], scalar2=None, op0=ALU.mult
                 )
+                kks.append(kk)
+            for tt in range(G):
                 nc.vector.scalar_tensor_tensor(
-                    out=fr[:, tt, :], in0=pt[:], scalar=gq[:, tt : tt + 1], in1=kk[:],
+                    out=fr[:, tt, :], in0=pts[tt][:], scalar=gq[:, tt : tt + 1], in1=kks[tt][:],
                     op0=ALU.mult, op1=ALU.subtract,
                 )
-            st[("fr", s)] = fr
+            st[("fr", g)] = fr
 
-        def act_c(s):
-            fr = st[("fr", s)]
+        def trig(g):
+            fr = st[("fr", g)]
             cc = work.tile([P, G, D], F32, name="cc", bufs=2)
             ss = work.tile([P, G, D], F32, name="ss", bufs=2)
             nc.scalar.activation(out=cc[:], in_=fr[:], func=ACT.Abs)
             nc.scalar.activation(out=ss[:], in_=fr[:], func=ACT.Sin, scale=TWO_PI)
             nc.scalar.activation(out=cc[:], in_=cc[:], func=ACT.Sin, scale=-TWO_PI, bias=hpi_t[:])
-            st[("cc", s)] = cc
-            st[("ss", s)] = ss
+            st[("cc", g)] = cc
+            st[("ss", g)] = ss
 
-        def dve_c(s):
-            sl = slice(G * s, G * s + G)
-            q, cc, ss = half("sr", s), st[("cc", s)], st[("ss", s)]
+        def unit_real(g):
             c0 = work.tile([P, G, D], F32, name="c0", bufs=2)
-            x1 = work.tile([P, G, D], F32, name="x1", bufs=4)
-            x2 = work.tile([P, G, D], F32, name="x2", bufs=4)
-            sm = small.tile([P, 2, 2, G], F32, name="sm")
+            nc.vector.tensor_tensor(out=c0[:], in0=st[("xr", g)][:], in1=st[("sr", g)][:], op=ALU.mult)
+            st[("c0", g)] = c0
+            st[("x1", g)] = work.tile([P, G, D], F32, name="x1", bufs=4)
+            st[("x2", g)] = work.tile([P, G, D], F32, name="x2", bufs=4)
+            st[("sm", g)] = small.tile([P, 2, 2, G], F32, name="sm")
+
+        def unit_imag(g):
+            q = st[("sr", g)]
+            nc.vector.tensor_tensor(out=q[:], in0=st[("xi", g)][:], in1=q[:], op=ALU.mult)
+
+        def product(g, tt, k):
+            c0, q, cc, ss = st[("c0", g)], st[("sr", g)], st[("cc", g)], st[("ss", g)]
+            out_t, in_t, sgn, trg, a, o = (
+                (st[("x1", g)], c0, 1.0, cc, 0, 0), (st[("x2", g)], q, 1.0, cc, 1, 1),
+                (c0, c0, 1.0, ss, 0, 1), (q, q, -1.0, ss, 1, 0),
+            )[k]
+            nc.vector.scalar_tensor_tensor(
+                out=out_t[:, tt, :], in0=in_t[:, tt, :], scalar=sgn, in1=trg[:, tt, :],
+                op0=ALU.mult, op1=ALU.mult, accum_out=st[("sm", g)][:, a, o, tt : tt + 1],
+            )
+
+        def means(g):
+            sm = st[("sm", g)]
             msum = small.tile([P, 2, G], F32, name="msum")
             mean = small.tile([P, 2, G], F32, name="mean")
-            nc.vector.tensor_tensor(out=c0[:], in0=half("xr", s), in1=q, op=ALU.mult)
-            nc.vector.tensor_tensor(out=q, in0=half("xi", s), in1=q, op=ALU.mult)
-            for tt in range(G):
-                for out_t, in_t, sgn, trig, a, o in (
-                    (x1, c0, 1.0, cc, 0, 0), (x2, q, 1.0, cc, 1, 1), (c0, c0, 1.0, ss, 0, 1), (q, q, -1.0, ss, 1, 0),
-                ):
-                    nc.vector.scalar_tensor_tensor(
-                        out=out_t[:, tt, :], in0=in_t[:, tt, :], scalar=sgn, in1=trig[:, tt, :],
-                        op0=ALU.mult, op1=ALU.mult, accum_out=sm[:, a, o, tt : tt + 1],
-                    )
-            nc.vector.tensor_tensor(out=msum[:], in0=sm[:, 0, :, :], in1=sm[:, 1, :, :], op=ALU.add)
-            nc.vector.tensor_scalar(out=mean[:], in0=msum[:], scalar1=1.0 / D, scalar2=None, op0=ALU.mult)
+            nc.gpsimd.tensor_tensor(out=msum[:], in0=sm[:, 0, :, :], in1=sm[:, 1, :, :], op=ALU.add)
+            nc.gpsimd.tensor_scalar(out=mean[:], in0=msum[:], scalar1=1.0 / D, scalar2=0.0, op0=ALU.mult, op1=ALU.add)
+            st[("mean", g)] = mean
+
+        def centre(g):
+            x1, x2, c0, q, mean = st[("x1", g)], st[("x2", g)], st[("c0", g)], st[("sr", g)], st[("mean", g)]
             for tt in range(G):
                 nc.vector.scalar_tensor_tensor(
                     out=x1[:, tt, :], in0=x1[:, tt, :], scalar=mean[:, 0, tt : tt + 1], in1=q[:, tt, :],
@@ -278,21 +283,19 @@ def tile_quantumcoherencelayer_t_kernel(
                     out=x2[:, tt, :], in0=x2[:, tt, :], scalar=mean[:, 1, tt : tt + 1], in1=c0[:, tt, :],
                     op0=ALU.subtract, op1=ALU.add,
                 )
-            st[("x1", s)] = x1
-            st[("x2", s)] = x2
 
-        def act_d(s):
+        def var_sums(g):
             ssq = small.tile([P, 2, G], F32, name="ssq")
             for tt in range(G):
-                for o, x in enumerate((st[("x1", s)], st[("x2", s)])):
+                for o, x in enumerate((st[("x1", g)], st[("x2", g)])):
                     junk = work.tile([P, D], BF16, name="ajunk", bufs=2)
                     nc.scalar.activation(
                         out=junk[:], in_=x[:, tt, :], func=ACT.Square, accum_out=ssq[:, o, tt : tt + 1]
                     )
-            st[("ssq", s)] = ssq
+            st[("ssq", g)] = ssq
 
-        def stats(s):
-            ssq = st[("ssq", s)]
+        def stats(g):
+            ssq = st[("ssq", g)]
             vare = small.tile([P, 2, G], F32, name="vare")
             rstd = small.tile([P, 2, G], F32, name="rstd")
             nc.gpsimd.tensor_scalar(out=vare[:], in0=ssq[:], scalar1=1.0 / D, scalar2=EPS, op0=ALU.mult, op1=ALU.add)
@@ -300,23 +303,23 @@ def tile_quantumcoherencelayer_t_kernel(
                 out=rstd[:].rearrange("p o t -> p (o t)"), in0=vare[:].rearrange("p o t -> p (o t)"),
                 in1=mhalf[:], op=ALU.pow,
             )
-            st[("rstd", s)] = rstd
+            st[("rstd", g)] = rstd
 
-        def d_mid(s):
-            xs_ = (st[("x1", s)], st[("x2", s)])
-            yt = work.tile([P, 4, 2, G, P], F32, name="yt", tag="yt", bufs=3, align_bytes=64)
+        def weigh(g):
+            xs_ = (st[("x1", g)], st[("x2", g)])
+            yt = work.tile([P, 4, 2, G, P], F32, name="yt", tag="yt", bufs=2, align_bytes=64)
             for c in range(4):
                 d_ps = ps_d.tile([P, 2, G, P], F32, name="d_ps")
                 for o in range(2):
                     for tt in range(G):
                         nc.tensor.transpose(d_ps[:, o, tt, :], xs_[o][:, tt, P * c : P * c + P], ident[:])
                 nc.scalar.activation(out=yt[:, c, :, :, :], in_=d_ps[:], func=ACT.Copy, scale=w_col[:, c : c + 1])
-            st[("yt", s)] = yt
+            st[("yt", g)] = yt
 
-        def d_fin(s):
-            sl = slice(G * s, G * s + G)
-            rstd, yt = st[("rstd", s)], st[("yt", s)]
-            xs_ = (st[("x1", s)], st[("x2", s)])
+        def finish(g):
+            sl = slice(G * g, G * g + G)
+            rstd, yt = st[("rstd", g)], st[("yt", g)]
+            xs_ = (st[("x1", g)], st[("x2", g)])
             for o, o_d in enumerate((or_d, oi_d)):
                 for tt in range(G):
                     y_ps = ps_y.tile([P, D], F32, name="y_ps")
@@ -328,33 +331,59 @@ def tile_quantumcoherencelayer_t_kernel(
                     )
                 nc.sync.dma_start(out=o_d[:, sl, :], in_=xs_[o][:])
 
-        def in_range_a(a):
-            return 0 <= a < NA
+        ctx.enter_context(tc.manual_schedule(engines={ENG.DVE, ENG.Activation, ENG.Pool}))
 
-        def round_b(s):
-            if in_range(s + 1):
-                dve_b1(s + 1)
-            if in_range(s):
-                dve_c(s)
-                act_d(s)
-                d_mid(s)
-            if in_range(s + 1):
-                dve_b2(s + 1)
-            if in_range(s - 1):
-                d_fin(s - 1)
-            if in_range(s + 1):
-                act_c(s + 1)
-            if in_range(s):
-                stats(s)
+        def step(r):
+            nxt, cur, prv = r + 1, r, r - 1
+            if ok(r + 4):
+                squares(r + 4)
+            if ok(nxt):
+                coh_sums(nxt)
+            if ok(prv):
+                var_sums(prv)
+                weigh(prv)
+            if ok(cur):
+                unit_real(cur)
+            if ok(nxt):
+                gain_a(nxt)
+            if ok(cur):
+                unit_imag(cur)
+            if ok(nxt):
+                gain_b(nxt)
+            if ok(cur):
+                product(cur, 0, 0)
+            if ok(nxt):
+                gain_c(nxt)
+            if ok(cur):
+                for tt in range(G):
+                    for k in range(4):
+                        if (tt, k) != (0, 0):
+                            product(cur, tt, k)
+            if ok(r + 2):
+                x_transposes(r + 2)
+            if r % 2 == 0:
+                roots([g for g in (r + 2, r + 3) if ok(g)])
+            if ok(nxt):
+                pe_mm(nxt)
+                reduce_range(nxt)
+            if ok(cur):
+                means(cur)
+            if ok(prv):
+                stats(prv)
+            if ok(r + 4):
+                square_sum(r + 4)
+            if ok(nxt):
+                trig(nxt)
+            if ok(prv):
+                finish(prv)
+            if ok(cur):
+                centre(cur)
+            if ok(r + 2):
+                quantise(r + 2)
+            if ok(r + 4):
+                eps_sum(r + 4)
+            if r >= 0 and ok(r + LOADS_AHEAD):
+                load(r + LOADS_AHEAD)
 
-        for j in range(-2, NA + 1):
-            round_b(2 * j)
-            if in_range_a(j + 1):
-                dve_a(j + 1)
-                act_b(j + 1)
-            if j >= 0 and in_range_a(j + 3):
-                load(j + 3)
-            if in_range_a(j + 2):
-                pe_transposes(j + 2)
-                act_a(j + 2)
-            round_b(2 * j + 1)
+        for r in range(-4, NG + 1):
+            step(r)

@@ -1,9 +1,7 @@
 import math
 from contextlib import ExitStack
 
-import concourse.bass as bass
 import concourse.mybir as mybir
-import concourse.tile as tile
 from concourse.masks import make_identity
 
 F32 = mybir.dt.float32
@@ -25,6 +23,8 @@ NG = NT // G
 EPS = 1e-8
 TWO_PI = 2.0 * math.pi
 LOADS_AHEAD = 6
+AHEAD = 3
+HEAD = 2
 
 FLOPS = 2 * ROWS * D * D
 
@@ -44,8 +44,7 @@ def tile_quantumcoherencelayer_t_kernel(
         small = ctx.enter_context(tc.tile_pool(name="small", bufs=6))
         ps_p = ctx.enter_context(tc.psum_pool(name="ps_p", bufs=2))
         ps_t = ctx.enter_context(tc.psum_pool(name="ps_t", bufs=1))
-        ps_d = ctx.enter_context(tc.psum_pool(name="ps_d", bufs=2))
-        ps_y = ctx.enter_context(tc.psum_pool(name="ps_y", bufs=3))
+        ps_y = ctx.enter_context(tc.psum_pool(name="ps_y", bufs=5))
 
         ph_raw = work.tile([P, 4, D], BF16, name="ph_raw", tag="yt", bufs=2, align_bytes=64)
         ph_grp = work.tile([P, D, 4], BF16, name="ph_grp", tag="yt", bufs=2, align_bytes=64)
@@ -64,19 +63,13 @@ def tile_quantumcoherencelayer_t_kernel(
         eps_t = keep.tile([P, 1], F32, name="eps_t")
         hpi_t = keep.tile([P, 1], F32, name="hpi_t")
         one_t = keep.tile([P, 1], F32, name="one_t")
+        warm = keep.tile([P, 1], F32, name="warm")
         mhalf = keep.tile([P, 2 * G], F32, name="mhalf")
 
-        nc.vector.memset(b_row[:], 0.0)
-        nc.vector.memset(w_rows[:], 0.0)
-        nc.vector.memset(ones[:], 1.0)
-        nc.vector.memset(eps_t[:], EPS)
-        nc.vector.memset(one_t[:], 1.0)
-        nc.vector.tensor_scalar(out=hpi_t[:], in0=one_t[:], scalar1=0.5 * math.pi, scalar2=None, op0=ALU.mult)
-        nc.vector.memset(mhalf[:], -0.5)
-        make_identity(nc, ident[:])
-        make_identity(nc, ident_bf[:])
-
         st = {}
+
+        def ok(g):
+            return 0 <= g < NG
 
         def load(g):
             sl = slice(G * g, G * g + G)
@@ -89,63 +82,76 @@ def tile_quantumcoherencelayer_t_kernel(
 
         load(0)
         nc.sync.dma_start(out=ph_raw[:], in_=phase_matrix.rearrange("(p j) n -> p j n", j=4))
+        load(1)
+        nc.vector.memset(one_t[:], 1.0)
+        nc.vector.memset(eps_t[:], EPS)
+        nc.vector.memset(b_row[:], 0.0)
+        nc.vector.memset(w_rows[:], 0.0)
+        nc.sync.dma_start(out=cf_bf[:], in_=coherence_factor.partition_broadcast(P))
         nc.sync.dma_start(out=w_rows[0:4, :], in_=ln_weight.rearrange("(c j) -> c j", c=4))
         nc.sync.dma_start(out=b_row[0:1, :], in_=ln_bias.unsqueeze(0))
-        nc.sync.dma_start(out=cf_bf[:], in_=coherence_factor.partition_broadcast(P))
-        for g in range(1, LOADS_AHEAD):
+        for g in range(2, LOADS_AHEAD):
             load(g)
+        nc.vector.memset(ones[:], 1.0)
+        nc.vector.tensor_scalar(out=hpi_t[:], in0=one_t[:], scalar1=0.5 * math.pi, scalar2=None, op0=ALU.mult)
+        nc.vector.memset(mhalf[:], -0.5)
+        make_identity(nc, ident[:])
+        make_identity(nc, ident_bf[:])
 
-        nc.vector.tensor_copy(out=ph_grp[:], in_=ph_raw[:].rearrange("p j n -> p n j"))
-        nc.vector.tensor_scalar(out=cfs[:], in0=cf_bf[:], scalar1=1.0 / TWO_PI, scalar2=None, op0=ALU.mult)
-        nc.vector.tensor_scalar(
-            out=ncf[:], in0=cf_bf[:], scalar1=-1.0 / (TWO_PI * D * D), scalar2=None, op0=ALU.mult
-        )
-        nc.vector.quantize_mx(
-            out=ph_codes[:].bitcast(FP8X4), scales=ph_scales[:], in_=ph_grp[:].rearrange("p n j -> p (n j)")
-        )
-        b_ps = ps_y.tile([P, D], F32, name="y_ps")
-        nc.tensor.matmul(out=b_ps[:], lhsT=ones[:], rhs=b_row[:], start=True, stop=True)
-        nc.vector.tensor_copy(out=b_sb[:], in_=b_ps[:])
-        w_ps = ps_d.tile([P, P], BF16, name="d_ps")
-        nc.tensor.transpose(w_ps[:], w_rows[:], ident_bf[:])
-        nc.vector.tensor_copy(out=w_col[:], in_=w_ps[:, 0:4])
+        def phase_codes():
+            nc.vector.tensor_copy(out=ph_grp[:], in_=ph_raw[:].rearrange("p j n -> p n j"))
+            nc.vector.tensor_scalar(out=cfs[:], in0=cf_bf[:], scalar1=1.0 / TWO_PI, scalar2=None, op0=ALU.mult)
+            nc.vector.tensor_scalar(
+                out=ncf[:], in0=cf_bf[:], scalar1=-1.0 / (TWO_PI * D * D), scalar2=None, op0=ALU.mult
+            )
+            nc.vector.quantize_mx(
+                out=ph_codes[:].bitcast(FP8X4), scales=ph_scales[:], in_=ph_grp[:].rearrange("p n j -> p (n j)")
+            )
 
-        def ok(g):
-            return 0 <= g < NG
+        def norm_constants():
+            b_ps = ps_y.tile([P, D], F32, name="b_ps", tag="turn")
+            nc.tensor.matmul(out=b_ps[:], lhsT=ones[:], rhs=b_row[:], start=True, stop=True)
+            nc.vector.tensor_copy(out=b_sb[:], in_=b_ps[:])
+            w_ps = ps_y.tile([P, P], BF16, name="w_ps", tag="turn")
+            nc.tensor.transpose(w_ps[:], w_rows[:], ident_bf[:])
+            nc.vector.tensor_copy(out=w_col[:], in_=w_ps[:, 0:4])
 
-        def squares(g):
+        def squares_plain(g):
             xr, xi = st[("xr", g)], st[("xi", g)]
             s1 = work.tile([P, G, D], F32, name="s1", bufs=2)
             si = work.tile([P, G, D], F32, name="si", bufs=2)
-            sa = work.tile([P, G, D], F32, name="sa", bufs=5)
-            sb = work.tile([P, G, D], F32, name="sb", bufs=2)
             nc.scalar.activation(out=s1[:], in_=xr[:], func=ACT.Square)
             nc.scalar.activation(out=si[:], in_=xi[:], func=ACT.Square)
-            nc.scalar.activation(out=sa[:], in_=xr[:], func=ACT.Square, bias=eps_t[:])
-            nc.scalar.activation(out=sb[:], in_=xi[:], func=ACT.Square, bias=eps_t[:])
             st[("s1", g)] = s1
             st[("si", g)] = si
+
+        def squares_eps(g):
+            xr, xi = st[("xr", g)], st[("xi", g)]
+            sa = work.tile([P, G, D], F32, name="sa", bufs=5)
+            sb = work.tile([P, G, D], F32, name="sb", bufs=2)
+            nc.scalar.activation(out=sa[:], in_=xr[:], func=ACT.Square, bias=eps_t[:])
+            nc.scalar.activation(out=sb[:], in_=xi[:], func=ACT.Square, bias=eps_t[:])
             st[("sa", g)] = sa
             st[("sb", g)] = sb
 
-        def square_sum(g):
+        def square_sum(g, eng):
             sr = work.tile([P, G, D], F32, name="sr", bufs=5)
-            nc.gpsimd.tensor_tensor(out=sr[:], in0=st[("s1", g)][:], in1=st[("si", g)][:], op=ALU.add)
+            eng.tensor_tensor(out=sr[:], in0=st[("s1", g)][:], in1=st[("si", g)][:], op=ALU.add)
             st[("sr", g)] = sr
 
         def eps_sum(g):
             sa, sb = st[("sa", g)], st[("sb", g)]
             nc.vector.tensor_tensor(out=sa[:], in0=sa[:], in1=sb[:], op=ALU.add)
 
-        def roots(gs):
-            for g in gs:
-                sa = st[("sa", g)]
-                nc.scalar.activation(out=sa[:], in_=sa[:], func=ACT.Abs_reciprocal_sqrt)
-            for g in gs:
-                sr = st[("sr", g)]
-                nc.scalar.activation(out=sr[:], in_=sr[:], func=ACT.Abs_reciprocal_sqrt, bias=eps_t[:])
+        def root_eps(g):
+            sa = st[("sa", g)]
+            nc.scalar.activation(out=sa[:], in_=sa[:], func=ACT.Abs_reciprocal_sqrt)
 
-        def x_transposes(g):
+        def root_plain(g):
+            sr = st[("sr", g)]
+            nc.scalar.activation(out=sr[:], in_=sr[:], func=ACT.Abs_reciprocal_sqrt, bias=eps_t[:])
+
+        def x_transposes(g, copy):
             xr_words = st[("xr", g)][:].rearrange("p t d -> p (t d)").bitcast(F32).rearrange(
                 "p (t j u) -> p t u j", t=G, u=2
             )
@@ -155,7 +161,7 @@ def tile_quantumcoherencelayer_t_kernel(
                     nc.tensor.transpose(xt[:, tt, u, :], xr_words[:, tt, u, :], ident[:])
             xg = work.tile([P, G * P * 4], BF16, name="xg", bufs=2, align_bytes=64)
             xg_w = xg[:].bitcast(F32).rearrange("p (t r u) -> p t r u", t=G, u=2)
-            nc.scalar.copy(out=xg_w, in_=xt[:].rearrange("p t u r -> p t r u"))
+            copy(out=xg_w, in_=xt[:].rearrange("p t u r -> p t r u"))
             st[("xg", g)] = xg
 
         def quantise(g):
@@ -241,23 +247,22 @@ def tile_quantumcoherencelayer_t_kernel(
             st[("cc", g)] = cc
             st[("ss", g)] = ss
 
-        def unit_real(g):
+        def unit(g):
             c0 = work.tile([P, G, D], F32, name="c0", bufs=2)
-            nc.vector.tensor_tensor(out=c0[:], in0=st[("xr", g)][:], in1=st[("sr", g)][:], op=ALU.mult)
+            q = st[("sr", g)]
+            nc.vector.tensor_tensor(out=c0[:], in0=st[("xr", g)][:], in1=q[:], op=ALU.mult)
+            nc.vector.tensor_tensor(out=q[:], in0=st[("xi", g)][:], in1=q[:], op=ALU.mult)
             st[("c0", g)] = c0
             st[("x1", g)] = work.tile([P, G, D], F32, name="x1", bufs=4)
             st[("x2", g)] = work.tile([P, G, D], F32, name="x2", bufs=4)
             st[("sm", g)] = small.tile([P, 2, 2, G], F32, name="sm")
 
-        def unit_imag(g):
-            q = st[("sr", g)]
-            nc.vector.tensor_tensor(out=q[:], in0=st[("xi", g)][:], in1=q[:], op=ALU.mult)
-
         def product(g, tt, k):
             c0, q, cc, ss = st[("c0", g)], st[("sr", g)], st[("cc", g)], st[("ss", g)]
             out_t, in_t, sgn, trg, a, o = (
-                (st[("x1", g)], c0, 1.0, cc, 0, 0), (st[("x2", g)], q, 1.0, cc, 1, 1),
                 (c0, c0, 1.0, ss, 0, 1), (q, q, -1.0, ss, 1, 0),
+            )[k - 2] if k >= 2 else (
+                (st[("x1", g)], c0, 1.0, cc, 0, 0), (st[("x2", g)], q, 1.0, cc, 1, 1),
             )[k]
             nc.vector.scalar_tensor_tensor(
                 out=out_t[:, tt, :], in0=in_t[:, tt, :], scalar=sgn, in1=trg[:, tt, :],
@@ -305,85 +310,130 @@ def tile_quantumcoherencelayer_t_kernel(
             )
             st[("rstd", g)] = rstd
 
-        def weigh(g):
+        def to_features(g):
             xs_ = (st[("x1", g)], st[("x2", g)])
-            yt = work.tile([P, 4, 2, G, P], F32, name="yt", tag="yt", bufs=2, align_bytes=64)
+            banks = []
             for c in range(4):
-                d_ps = ps_d.tile([P, 2, G, P], F32, name="d_ps")
+                d_ps = ps_y.tile([P, 2, G, P], F32, name="d_ps", tag="turn")
                 for o in range(2):
                     for tt in range(G):
                         nc.tensor.transpose(d_ps[:, o, tt, :], xs_[o][:, tt, P * c : P * c + P], ident[:])
-                nc.scalar.activation(out=yt[:, c, :, :, :], in_=d_ps[:], func=ACT.Copy, scale=w_col[:, c : c + 1])
+                banks.append(d_ps)
+            st[("d_ps", g)] = banks
+
+        def weigh(g):
+            yt = work.tile([P, 4, 2, G, P], F32, name="yt", tag="yt", bufs=2, align_bytes=64)
+            for c in range(4):
+                nc.scalar.activation(
+                    out=yt[:, c, :, :, :], in_=st[("d_ps", g)][c][:], func=ACT.Copy, scale=w_col[:, c : c + 1]
+                )
             st[("yt", g)] = yt
+
+        def to_rows(g):
+            yt = st[("yt", g)]
+            banks = []
+            for o in range(2):
+                for tt in range(G):
+                    y_ps = ps_y.tile([P, D], F32, name="y_ps", tag="turn")
+                    for c in range(4):
+                        nc.tensor.transpose(y_ps[:, P * c : P * c + P], yt[:, c, o, tt, :], ident[:])
+                    banks.append(y_ps)
+            st[("y_ps", g)] = banks
 
         def finish(g):
             sl = slice(G * g, G * g + G)
-            rstd, yt = st[("rstd", g)], st[("yt", g)]
+            rstd = st[("rstd", g)]
             xs_ = (st[("x1", g)], st[("x2", g)])
             for o, o_d in enumerate((or_d, oi_d)):
                 for tt in range(G):
-                    y_ps = ps_y.tile([P, D], F32, name="y_ps")
-                    for c in range(4):
-                        nc.tensor.transpose(y_ps[:, P * c : P * c + P], yt[:, c, o, tt, :], ident[:])
                     nc.vector.scalar_tensor_tensor(
-                        out=xs_[o][:, tt, :], in0=y_ps[:], scalar=rstd[:, o, tt : tt + 1], in1=b_sb[:],
-                        op0=ALU.mult, op1=ALU.add,
+                        out=xs_[o][:, tt, :], in0=st[("y_ps", g)][G * o + tt][:], scalar=rstd[:, o, tt : tt + 1],
+                        in1=b_sb[:], op0=ALU.mult, op1=ALU.add,
                     )
                 nc.sync.dma_start(out=o_d[:, sl, :], in_=xs_[o][:])
 
-        ctx.enter_context(tc.manual_schedule(engines={ENG.DVE, ENG.Activation, ENG.Pool}))
+        ctx.enter_context(tc.manual_schedule(engines={ENG.DVE, ENG.Activation, ENG.Pool, ENG.PE}))
+
+        nc.scalar.activation(out=warm[:], in_=one_t[:], func=ACT.Abs_reciprocal_sqrt)
+        for g in range(HEAD):
+            squares_eps(g)
+            x_transposes(g, nc.vector.tensor_copy)
+            quantise(g)
+            eps_sum(g)
+            if g == 0:
+                phase_codes()
+        for g in range(HEAD):
+            root_eps(g)
+        for g in range(HEAD):
+            squares_plain(g)
+        pe_mm(0)
+        coh_sums(0)
+        gain_a(0)
+        gain_b(0)
+        gain_c(0)
+        reduce_range(0)
+        for g in range(HEAD):
+            square_sum(g, nc.vector)
+            root_plain(g)
+        trig(0)
+        norm_constants()
+        squares_plain(HEAD)
+        squares_eps(HEAD)
+        square_sum(HEAD, nc.gpsimd)
 
         def step(r):
-            nxt, cur, prv = r + 1, r, r - 1
-            if ok(r + 4):
-                squares(r + 4)
-            if ok(nxt):
-                coh_sums(nxt)
+            nxt, cur, prv, new = r + 1, r, r - 1, r + AHEAD
             if ok(prv):
-                var_sums(prv)
+                to_features(prv)
                 weigh(prv)
-            if ok(cur):
-                unit_real(cur)
-            if ok(nxt):
-                gain_a(nxt)
-            if ok(cur):
-                unit_imag(cur)
-            if ok(nxt):
-                gain_b(nxt)
-            if ok(cur):
-                product(cur, 0, 0)
-            if ok(nxt):
-                gain_c(nxt)
-            if ok(cur):
-                for tt in range(G):
-                    for k in range(4):
-                        if (tt, k) != (0, 0):
-                            product(cur, tt, k)
+                var_sums(prv)
             if ok(r + 2):
-                x_transposes(r + 2)
-            if r % 2 == 0:
-                roots([g for g in (r + 2, r + 3) if ok(g)])
+                x_transposes(r + 2, nc.scalar.copy)
+            if ok(new):
+                squares_plain(new)
+                squares_eps(new)
             if ok(nxt):
                 pe_mm(nxt)
+            if ok(prv):
+                to_rows(prv)
+            if ok(cur):
+                unit(cur)
+            if ok(nxt):
+                coh_sums(nxt)
+            small_steps = [gain_a, gain_b, gain_c] if ok(nxt) else []
+            for n in range(4 * G):
+                if ok(cur):
+                    product(cur, n // 4, n % 4)
+                if n < len(small_steps):
+                    small_steps[n](nxt)
+            if ok(nxt):
                 reduce_range(nxt)
             if ok(cur):
                 means(cur)
             if ok(prv):
                 stats(prv)
-            if ok(r + 4):
-                square_sum(r + 4)
+            if ok(new):
+                square_sum(new, nc.gpsimd)
             if ok(nxt):
                 trig(nxt)
+            if ok(cur) and not ok(nxt):
+                centre(cur)
             if ok(prv):
                 finish(prv)
-            if ok(cur):
+            if ok(cur) and ok(nxt):
                 centre(cur)
             if ok(r + 2):
                 quantise(r + 2)
-            if ok(r + 4):
-                eps_sum(r + 4)
-            if r >= 0 and ok(r + LOADS_AHEAD):
+            for g in range(HEAD if r == 0 else new, new + 1):
+                if ok(g):
+                    eps_sum(g)
+            if r % 2 == 0:
+                for g in (r + 2, r + 3):
+                    if ok(g):
+                        root_eps(g)
+                        root_plain(g)
+            if ok(r + LOADS_AHEAD):
                 load(r + LOADS_AHEAD)
 
-        for r in range(-4, NG + 1):
+        for r in range(NG + 1):
             step(r)

@@ -25,6 +25,7 @@ TWO_PI = 2.0 * math.pi
 LOADS_AHEAD = 6
 AHEAD = 3
 HEAD = 2
+LAG = 2
 
 FLOPS = 2 * ROWS * D * D
 
@@ -46,8 +47,8 @@ def tile_quantumcoherencelayer_t_kernel(
         ps_t = ctx.enter_context(tc.psum_pool(name="ps_t", bufs=1))
         ps_y = ctx.enter_context(tc.psum_pool(name="ps_y", bufs=5))
 
-        ph_raw = work.tile([P, 4, D], BF16, name="ph_raw", tag="yt", bufs=2, align_bytes=64)
-        ph_grp = work.tile([P, D, 4], BF16, name="ph_grp", tag="yt", bufs=2, align_bytes=64)
+        ph_raw = work.tile([P, 4, D], BF16, name="ph_raw", tag="yt", bufs=3, align_bytes=64)
+        ph_grp = work.tile([P, D, 4], BF16, name="ph_grp", tag="yt", bufs=3, align_bytes=64)
         ph_codes = keep.tile([P, D], U32, name="ph_codes", align_bytes=64)
         ph_scales = keep.tile([P, D], U8, name="ph_scales", align_bytes=64)
         b_row = keep.tile([P, D], BF16, name="b_row")
@@ -151,7 +152,7 @@ def tile_quantumcoherencelayer_t_kernel(
             sr = st[("sr", g)]
             nc.scalar.activation(out=sr[:], in_=sr[:], func=ACT.Abs_reciprocal_sqrt, bias=eps_t[:])
 
-        def x_transposes(g, copy):
+        def x_transposes(g):
             xr_words = st[("xr", g)][:].rearrange("p t d -> p (t d)").bitcast(F32).rearrange(
                 "p (t j u) -> p t u j", t=G, u=2
             )
@@ -159,9 +160,13 @@ def tile_quantumcoherencelayer_t_kernel(
             for tt in range(G):
                 for u in range(2):
                     nc.tensor.transpose(xt[:, tt, u, :], xr_words[:, tt, u, :], ident[:])
+            st[("xt", g)] = xt
+
+        def x_copy(g):
+            xt = st[("xt", g)]
             xg = work.tile([P, G * P * 4], BF16, name="xg", bufs=2, align_bytes=64)
             xg_w = xg[:].bitcast(F32).rearrange("p (t r u) -> p t r u", t=G, u=2)
-            copy(out=xg_w, in_=xt[:].rearrange("p t u r -> p t r u"))
+            nc.vector.tensor_copy(out=xg_w, in_=xt[:].rearrange("p t u r -> p t r u"))
             st[("xg", g)] = xg
 
         def quantise(g):
@@ -253,8 +258,8 @@ def tile_quantumcoherencelayer_t_kernel(
             nc.vector.tensor_tensor(out=c0[:], in0=st[("xr", g)][:], in1=q[:], op=ALU.mult)
             nc.vector.tensor_tensor(out=q[:], in0=st[("xi", g)][:], in1=q[:], op=ALU.mult)
             st[("c0", g)] = c0
-            st[("x1", g)] = work.tile([P, G, D], F32, name="x1", bufs=4)
-            st[("x2", g)] = work.tile([P, G, D], F32, name="x2", bufs=4)
+            st[("x1", g)] = work.tile([P, G, D], F32, name="x1", bufs=2)
+            st[("x2", g)] = work.tile([P, G, D], F32, name="x2", bufs=2)
             st[("sm", g)] = small.tile([P, 2, 2, G], F32, name="sm")
 
         def product(g, tt, k):
@@ -274,29 +279,21 @@ def tile_quantumcoherencelayer_t_kernel(
             msum = small.tile([P, 2, G], F32, name="msum")
             mean = small.tile([P, 2, G], F32, name="mean")
             nc.gpsimd.tensor_tensor(out=msum[:], in0=sm[:, 0, :, :], in1=sm[:, 1, :, :], op=ALU.add)
-            nc.gpsimd.tensor_scalar(out=mean[:], in0=msum[:], scalar1=1.0 / D, scalar2=0.0, op0=ALU.mult, op1=ALU.add)
+            nc.gpsimd.tensor_scalar(out=mean[:], in0=msum[:], scalar1=-1.0 / D, scalar2=0.0, op0=ALU.mult, op1=ALU.add)
             st[("mean", g)] = mean
 
-        def centre(g):
-            x1, x2, c0, q, mean = st[("x1", g)], st[("x2", g)], st[("c0", g)], st[("sr", g)], st[("mean", g)]
-            for tt in range(G):
-                nc.vector.scalar_tensor_tensor(
-                    out=x1[:, tt, :], in0=x1[:, tt, :], scalar=mean[:, 0, tt : tt + 1], in1=q[:, tt, :],
-                    op0=ALU.subtract, op1=ALU.add,
-                )
-                nc.vector.scalar_tensor_tensor(
-                    out=x2[:, tt, :], in0=x2[:, tt, :], scalar=mean[:, 1, tt : tt + 1], in1=c0[:, tt, :],
-                    op0=ALU.subtract, op1=ALU.add,
-                )
+        def spread(g):
+            mt = work.tile([P, 2 * G, P], F32, name="mt", bufs=2)
+            nc.vector.tensor_copy(
+                out=mt[:], in_=st[("mean", g)][:].rearrange("p o t -> p (o t)").unsqueeze(2).to_broadcast([P, 2 * G, P])
+            )
+            st[("mt", g)] = mt
 
         def var_sums(g):
             ssq = small.tile([P, 2, G], F32, name="ssq")
-            for tt in range(G):
-                for o, x in enumerate((st[("x1", g)], st[("x2", g)])):
-                    junk = work.tile([P, D], BF16, name="ajunk", bufs=2)
-                    nc.scalar.activation(
-                        out=junk[:], in_=x[:, tt, :], func=ACT.Square, accum_out=ssq[:, o, tt : tt + 1]
-                    )
+            nc.vector.tensor_reduce(
+                out=ssq[:].rearrange("p o t -> p (o t)"), in_=st[("v_ps", g)][:], axis=mybir.AxisListType.X, op=ALU.add
+            )
             st[("ssq", g)] = ssq
 
         def stats(g):
@@ -310,24 +307,46 @@ def tile_quantumcoherencelayer_t_kernel(
             )
             st[("rstd", g)] = rstd
 
+        def turn(out, in_, start, stop):
+            nc.tensor.matmul(out=out, lhsT=in_, rhs=ident[:], is_transpose=True, start=start, stop=stop)
+
         def to_features(g):
-            xs_ = (st[("x1", g)], st[("x2", g)])
+            terms = ((st[("x1", g)], st[("sr", g)]), (st[("x2", g)], st[("c0", g)]))
+            mt = st[("mt", g)]
             banks = []
             for c in range(4):
                 d_ps = ps_y.tile([P, 2, G, P], F32, name="d_ps", tag="turn")
+                cols = slice(P * c, P * c + P)
+                for k in range(2):
+                    for o in range(2):
+                        for tt in range(G):
+                            turn(d_ps[:, o, tt, :], terms[o][k][:, tt, cols], k == 0 and o == 0 and tt == 0, False)
                 for o in range(2):
                     for tt in range(G):
-                        nc.tensor.transpose(d_ps[:, o, tt, :], xs_[o][:, tt, P * c : P * c + P], ident[:])
+                        turn(d_ps[:, o, tt, :], mt[:, G * o + tt, :], False, o == 1 and tt == G - 1)
                 banks.append(d_ps)
             st[("d_ps", g)] = banks
 
         def weigh(g):
-            yt = work.tile([P, 4, 2, G, P], F32, name="yt", tag="yt", bufs=2, align_bytes=64)
+            yt = work.tile([P, 4, 2, G, P], F32, name="yt", tag="yt", bufs=3, align_bytes=64)
+            sq = work.tile([P, 4, 2, G, P], F32, name="sq", bufs=2)
             for c in range(4):
                 nc.scalar.activation(
                     out=yt[:, c, :, :, :], in_=st[("d_ps", g)][c][:], func=ACT.Copy, scale=w_col[:, c : c + 1]
                 )
+                nc.scalar.activation(out=sq[:, c, :, :, :], in_=st[("d_ps", g)][c][:], func=ACT.Square)
             st[("yt", g)] = yt
+            st[("sq", g)] = sq
+
+        def var_turn(g):
+            sq = st[("sq", g)]
+            v_ps = ps_y.tile([P, 2 * G, P], F32, name="v_ps", tag="turn")
+            for c in range(4):
+                for o in range(2):
+                    for tt in range(G):
+                        turn(v_ps[:, G * o + tt, :], sq[:, c, o, tt, :], c == 0 and o == 0 and tt == 0,
+                             c == 3 and o == 1 and tt == G - 1)
+            st[("v_ps", g)] = v_ps
 
         def to_rows(g):
             yt = st[("yt", g)]
@@ -343,21 +362,22 @@ def tile_quantumcoherencelayer_t_kernel(
         def finish(g):
             sl = slice(G * g, G * g + G)
             rstd = st[("rstd", g)]
-            xs_ = (st[("x1", g)], st[("x2", g)])
             for o, o_d in enumerate((or_d, oi_d)):
+                res = work.tile([P, G, D], F32, name="res", bufs=4)
                 for tt in range(G):
                     nc.vector.scalar_tensor_tensor(
-                        out=xs_[o][:, tt, :], in0=st[("y_ps", g)][G * o + tt][:], scalar=rstd[:, o, tt : tt + 1],
+                        out=res[:, tt, :], in0=st[("y_ps", g)][G * o + tt][:], scalar=rstd[:, o, tt : tt + 1],
                         in1=b_sb[:], op0=ALU.mult, op1=ALU.add,
                     )
-                nc.sync.dma_start(out=o_d[:, sl, :], in_=xs_[o][:])
+                nc.sync.dma_start(out=o_d[:, sl, :], in_=res[:])
 
         ctx.enter_context(tc.manual_schedule(engines={ENG.DVE, ENG.Activation, ENG.Pool, ENG.PE}))
 
         nc.scalar.activation(out=warm[:], in_=one_t[:], func=ACT.Abs_reciprocal_sqrt)
         for g in range(HEAD):
             squares_eps(g)
-            x_transposes(g, nc.vector.tensor_copy)
+            x_transposes(g)
+            x_copy(g)
             quantise(g)
             eps_sum(g)
             if g == 0:
@@ -382,20 +402,19 @@ def tile_quantumcoherencelayer_t_kernel(
         square_sum(HEAD, nc.gpsimd)
 
         def step(r):
-            nxt, cur, prv, new = r + 1, r, r - 1, r + AHEAD
-            if ok(prv):
-                to_features(prv)
-                weigh(prv)
-                var_sums(prv)
+            nxt, cur, prv, new, old = r + 1, r, r - 1, r + AHEAD, r - LAG
+            if ok(nxt):
+                pe_mm(nxt)
             if ok(r + 2):
-                x_transposes(r + 2, nc.scalar.copy)
+                x_transposes(r + 2)
+            if ok(old):
+                to_rows(old)
+            if ok(prv):
+                weigh(prv)
+                var_turn(prv)
             if ok(new):
                 squares_plain(new)
                 squares_eps(new)
-            if ok(nxt):
-                pe_mm(nxt)
-            if ok(prv):
-                to_rows(prv)
             if ok(cur):
                 unit(cur)
             if ok(nxt):
@@ -406,22 +425,25 @@ def tile_quantumcoherencelayer_t_kernel(
                     product(cur, n // 4, n % 4)
                 if n < len(small_steps):
                     small_steps[n](nxt)
+            if ok(r + 2):
+                x_copy(r + 2)
             if ok(nxt):
                 reduce_range(nxt)
             if ok(cur):
                 means(cur)
-            if ok(prv):
-                stats(prv)
+            if ok(old):
+                stats(old)
             if ok(new):
                 square_sum(new, nc.gpsimd)
             if ok(nxt):
                 trig(nxt)
-            if ok(cur) and not ok(nxt):
-                centre(cur)
+            if ok(old):
+                finish(old)
             if ok(prv):
-                finish(prv)
-            if ok(cur) and ok(nxt):
-                centre(cur)
+                var_sums(prv)
+            if ok(cur):
+                spread(cur)
+                to_features(cur)
             if ok(r + 2):
                 quantise(r + 2)
             for g in range(HEAD if r == 0 else new, new + 1):
@@ -435,5 +457,5 @@ def tile_quantumcoherencelayer_t_kernel(
             if ok(r + LOADS_AHEAD):
                 load(r + LOADS_AHEAD)
 
-        for r in range(NG + 1):
+        for r in range(NG + LAG):
             step(r)

@@ -18,14 +18,19 @@ P = 128
 D = 512
 ROWS = 4096
 NT = ROWS // P
-G = 2
-NG = NT // G
+SIZES = [2] * 16
+NG = len(SIZES)
+FIRST = [sum(SIZES[:g]) for g in range(NG)]
+GMAX = max(SIZES)
 EPS = 1e-8
 TWO_PI = 2.0 * math.pi
-LOADS_AHEAD = 6
+SA_BUFS = 5
+SR_BUFS = 5
 AHEAD = 3
 HEAD = 2
+LOADS_AHEAD = 6
 LAG = 2
+DRAIN = 3
 
 FLOPS = 2 * ROWS * D * D
 
@@ -65,7 +70,7 @@ def tile_quantumcoherencelayer_t_kernel(
         hpi_t = keep.tile([P, 1], F32, name="hpi_t")
         one_t = keep.tile([P, 1], F32, name="one_t")
         warm = keep.tile([P, 1], F32, name="warm")
-        mhalf = keep.tile([P, 2 * G], F32, name="mhalf")
+        mhalf = keep.tile([P, 2 * GMAX], F32, name="mhalf")
 
         st = {}
 
@@ -73,9 +78,10 @@ def tile_quantumcoherencelayer_t_kernel(
             return 0 <= g < NG
 
         def load(g):
-            sl = slice(G * g, G * g + G)
-            xr = work.tile([P, G, D], BF16, name="xr", bufs=LOADS_AHEAD, align_bytes=64)
-            xi = work.tile([P, G, D], BF16, name="xi", bufs=LOADS_AHEAD, align_bytes=64)
+            n = SIZES[g]
+            sl = slice(FIRST[g], FIRST[g] + n)
+            xr = work.tile([P, n, D], BF16, name="xr", bufs=LOADS_AHEAD, align_bytes=64)
+            xi = work.tile([P, n, D], BF16, name="xi", bufs=LOADS_AHEAD, align_bytes=64)
             nc.sync.dma_start(out=xr[:], in_=xr_d[:, sl, :])
             nc.sync.dma_start(out=xi[:], in_=xi_d[:, sl, :])
             st[("xr", g)] = xr
@@ -117,32 +123,33 @@ def tile_quantumcoherencelayer_t_kernel(
             nc.tensor.transpose(w_ps[:], w_rows[:], ident_bf[:])
             nc.vector.tensor_copy(out=w_col[:], in_=w_ps[:, 0:4])
 
+        def turn(out, in_, start, stop):
+            nc.tensor.matmul(out=out, lhsT=in_, rhs=ident[:], is_transpose=True, start=start, stop=stop)
+
         def squares_plain(g):
-            xr, xi = st[("xr", g)], st[("xi", g)]
-            s1 = work.tile([P, G, D], F32, name="s1", bufs=2)
-            si = work.tile([P, G, D], F32, name="si", bufs=2)
-            nc.scalar.activation(out=s1[:], in_=xr[:], func=ACT.Square)
-            nc.scalar.activation(out=si[:], in_=xi[:], func=ACT.Square)
-            st[("s1", g)] = s1
-            st[("si", g)] = si
+            n = SIZES[g]
+            sr = work.tile([P, n, D], F32, name="sr", bufs=SR_BUFS)
+            si = work.tile([P, n, D], F32, name="si", bufs=2)
+            nc.scalar.activation(out=sr[:], in_=st[("xr", g)][:], func=ACT.Square)
+            nc.scalar.activation(out=si[:], in_=st[("xi", g)][:], func=ACT.Square)
+            st[("sr", g)], st[("si", g)] = sr, si
 
         def squares_eps(g):
-            xr, xi = st[("xr", g)], st[("xi", g)]
-            sa = work.tile([P, G, D], F32, name="sa", bufs=5)
-            sb = work.tile([P, G, D], F32, name="sb", bufs=2)
-            nc.scalar.activation(out=sa[:], in_=xr[:], func=ACT.Square, bias=eps_t[:])
-            nc.scalar.activation(out=sb[:], in_=xi[:], func=ACT.Square, bias=eps_t[:])
-            st[("sa", g)] = sa
-            st[("sb", g)] = sb
+            n = SIZES[g]
+            sa = work.tile([P, n, D], F32, name="sa", bufs=SA_BUFS)
+            sb = work.tile([P, n, D], F32, name="sb", bufs=2)
+            nc.scalar.activation(out=sa[:], in_=st[("xr", g)][:], func=ACT.Square, bias=eps_t[:])
+            nc.scalar.activation(out=sb[:], in_=st[("xi", g)][:], func=ACT.Square, bias=eps_t[:])
+            st[("sa", g)], st[("sb", g)] = sa, sb
 
         def square_sum(g, eng):
-            sr = work.tile([P, G, D], F32, name="sr", bufs=5)
-            eng.tensor_tensor(out=sr[:], in0=st[("s1", g)][:], in1=st[("si", g)][:], op=ALU.add)
-            st[("sr", g)] = sr
+            sr = st[("sr", g)]
+            eng.tensor_tensor(out=sr[:], in0=sr[:], in1=st[("si", g)][:], op=ALU.add)
 
-        def eps_sum(g):
+        def eps_sum(g, eng, lo, hi):
             sa, sb = st[("sa", g)], st[("sb", g)]
-            nc.vector.tensor_tensor(out=sa[:], in0=sa[:], in1=sb[:], op=ALU.add)
+            if hi > lo:
+                eng.tensor_tensor(out=sa[:, lo:hi, :], in0=sa[:, lo:hi, :], in1=sb[:, lo:hi, :], op=ALU.add)
 
         def root_eps(g):
             sa = st[("sa", g)]
@@ -153,25 +160,27 @@ def tile_quantumcoherencelayer_t_kernel(
             nc.scalar.activation(out=sr[:], in_=sr[:], func=ACT.Abs_reciprocal_sqrt, bias=eps_t[:])
 
         def x_transposes(g):
+            n = SIZES[g]
             xr_words = st[("xr", g)][:].rearrange("p t d -> p (t d)").bitcast(F32).rearrange(
-                "p (t j u) -> p t u j", t=G, u=2
+                "p (t j u) -> p t u j", t=n, u=2
             )
-            xt = ps_t.tile([P, G, 2, P], F32, name="xt")
-            for tt in range(G):
+            xt = ps_t.tile([P, n, 2, P], F32, name="xt")
+            for tt in range(n):
                 for u in range(2):
                     nc.tensor.transpose(xt[:, tt, u, :], xr_words[:, tt, u, :], ident[:])
             st[("xt", g)] = xt
 
-        def x_copy(g):
-            xt = st[("xt", g)]
-            xg = work.tile([P, G * P * 4], BF16, name="xg", bufs=2, align_bytes=64)
-            xg_w = xg[:].bitcast(F32).rearrange("p (t r u) -> p t r u", t=G, u=2)
-            nc.vector.tensor_copy(out=xg_w, in_=xt[:].rearrange("p t u r -> p t r u"))
+        def x_copy(g, copy):
+            n = SIZES[g]
+            xg = work.tile([P, n * P * 4], BF16, name="xg", bufs=2, align_bytes=64)
+            xg_w = xg[:].bitcast(F32).rearrange("p (t r u) -> p t r u", t=n, u=2)
+            copy(out=xg_w, in_=st[("xt", g)][:].rearrange("p t u r -> p t r u"))
             st[("xg", g)] = xg
 
         def quantise(g):
-            xc = work.tile([P, G * P], U32, name="xc", bufs=3, align_bytes=64)
-            xs = work.tile([P, G * P], U8, name="xs", bufs=3, align_bytes=64)
+            n = SIZES[g]
+            xc = work.tile([P, n * P], U32, name="xc", bufs=3, align_bytes=64)
+            xs = work.tile([P, n * P], U8, name="xs", bufs=3, align_bytes=64)
             nc.vector.quantize_mx(out=xc[:].bitcast(FP8X4), scales=xs[:], in_=st[("xg", g)][:])
             st[("xc", g)] = xc
             st[("xs", g)] = xs
@@ -179,7 +188,7 @@ def tile_quantumcoherencelayer_t_kernel(
         def pe_mm(g):
             xc, xs = st[("xc", g)], st[("xs", g)]
             pts = []
-            for tt in range(G):
+            for tt in range(SIZES[g]):
                 pt = ps_p.tile([P, D], F32, name="pt")
                 cols = slice(P * tt, P * tt + P)
                 nc.tensor.matmul_mx(
@@ -195,9 +204,10 @@ def tile_quantumcoherencelayer_t_kernel(
             st[("pt", g)] = pts
 
         def coh_sums(g):
+            n = SIZES[g]
             sa = st[("sa", g)]
-            coh = small.tile([P, 2, G], F32, name="coh")
-            for tt in range(G):
+            coh = small.tile([P, 2, n], F32, name="coh")
+            for tt in range(n):
                 for o, x_h in enumerate((st[("xr", g)], st[("xi", g)])):
                     junk = work.tile([P, D], F32, name="vjunk", bufs=2)
                     nc.vector.scalar_tensor_tensor(
@@ -208,34 +218,35 @@ def tile_quantumcoherencelayer_t_kernel(
 
         def gain_a(g):
             coh = st[("coh", g)]
-            csq = small.tile([P, 2, G], F32, name="csq")
+            csq = small.tile([P, 2, SIZES[g]], F32, name="csq")
             nc.vector.tensor_tensor(out=csq[:], in0=coh[:], in1=coh[:], op=ALU.mult)
             st[("csq", g)] = csq
 
         def gain_b(g):
             csq = st[("csq", g)]
-            csum = small.tile([P, G], F32, name="csum")
+            csum = small.tile([P, SIZES[g]], F32, name="csum")
             nc.vector.tensor_tensor(out=csum[:], in0=csq[:, 0, :], in1=csq[:, 1, :], op=ALU.add)
             st[("csum", g)] = csum
 
         def gain_c(g):
-            gq = small.tile([P, G], F32, name="gq")
+            gq = small.tile([P, SIZES[g]], F32, name="gq")
             nc.vector.tensor_scalar(
                 out=gq[:], in0=st[("csum", g)][:], scalar1=ncf[:], scalar2=cfs[:], op0=ALU.mult, op1=ALU.add
             )
             st[("gq", g)] = gq
 
         def reduce_range(g):
+            n = SIZES[g]
             gq, pts = st[("gq", g)], st[("pt", g)]
-            fr = work.tile([P, G, D], F32, name="fr", bufs=2)
+            fr = work.tile([P, n, D], F32, name="fr", bufs=2)
             kks = []
-            for tt in range(G):
+            for tt in range(n):
                 kk = work.tile([P, D], I32, name="kk", bufs=2)
                 nc.vector.tensor_scalar(
                     out=kk[:], in0=pts[tt][:], scalar1=gq[:, tt : tt + 1], scalar2=None, op0=ALU.mult
                 )
                 kks.append(kk)
-            for tt in range(G):
+            for tt in range(n):
                 nc.vector.scalar_tensor_tensor(
                     out=fr[:, tt, :], in0=pts[tt][:], scalar=gq[:, tt : tt + 1], in1=kks[tt][:],
                     op0=ALU.mult, op1=ALU.subtract,
@@ -243,9 +254,10 @@ def tile_quantumcoherencelayer_t_kernel(
             st[("fr", g)] = fr
 
         def trig(g):
+            n = SIZES[g]
             fr = st[("fr", g)]
-            cc = work.tile([P, G, D], F32, name="cc", bufs=2)
-            ss = work.tile([P, G, D], F32, name="ss", bufs=2)
+            cc = work.tile([P, n, D], F32, name="cc", bufs=2)
+            ss = work.tile([P, n, D], F32, name="ss", bufs=2)
             nc.scalar.activation(out=cc[:], in_=fr[:], func=ACT.Abs)
             nc.scalar.activation(out=ss[:], in_=fr[:], func=ACT.Sin, scale=TWO_PI)
             nc.scalar.activation(out=cc[:], in_=cc[:], func=ACT.Sin, scale=-TWO_PI, bias=hpi_t[:])
@@ -253,14 +265,15 @@ def tile_quantumcoherencelayer_t_kernel(
             st[("ss", g)] = ss
 
         def unit(g):
-            c0 = work.tile([P, G, D], F32, name="c0", bufs=2)
+            n = SIZES[g]
+            c0 = work.tile([P, n, D], F32, name="c0", bufs=2)
             q = st[("sr", g)]
             nc.vector.tensor_tensor(out=c0[:], in0=st[("xr", g)][:], in1=q[:], op=ALU.mult)
             nc.vector.tensor_tensor(out=q[:], in0=st[("xi", g)][:], in1=q[:], op=ALU.mult)
             st[("c0", g)] = c0
-            st[("x1", g)] = work.tile([P, G, D], F32, name="x1", bufs=2)
-            st[("x2", g)] = work.tile([P, G, D], F32, name="x2", bufs=2)
-            st[("sm", g)] = small.tile([P, 2, 2, G], F32, name="sm")
+            st[("x1", g)] = work.tile([P, n, D], F32, name="x1", bufs=2)
+            st[("x2", g)] = work.tile([P, n, D], F32, name="x2", bufs=2)
+            st[("sm", g)] = small.tile([P, 2, 2, n], F32, name="sm")
 
         def product(g, tt, k):
             c0, q, cc, ss = st[("c0", g)], st[("sr", g)], st[("cc", g)], st[("ss", g)]
@@ -275,61 +288,63 @@ def tile_quantumcoherencelayer_t_kernel(
             )
 
         def means(g):
+            n = SIZES[g]
             sm = st[("sm", g)]
-            msum = small.tile([P, 2, G], F32, name="msum")
-            mean = small.tile([P, 2, G], F32, name="mean")
+            msum = small.tile([P, 2, n], F32, name="msum")
+            mean = small.tile([P, 2, n], F32, name="mean")
             nc.gpsimd.tensor_tensor(out=msum[:], in0=sm[:, 0, :, :], in1=sm[:, 1, :, :], op=ALU.add)
             nc.gpsimd.tensor_scalar(out=mean[:], in0=msum[:], scalar1=-1.0 / D, scalar2=0.0, op0=ALU.mult, op1=ALU.add)
             st[("mean", g)] = mean
 
         def spread(g):
-            mt = work.tile([P, 2 * G, P], F32, name="mt", bufs=2)
+            n = SIZES[g]
+            mt = work.tile([P, 2 * n, P], F32, name="mt", bufs=2)
             nc.vector.tensor_copy(
-                out=mt[:], in_=st[("mean", g)][:].rearrange("p o t -> p (o t)").unsqueeze(2).to_broadcast([P, 2 * G, P])
+                out=mt[:], in_=st[("mean", g)][:].rearrange("p o t -> p (o t)").unsqueeze(2).to_broadcast([P, 2 * n, P])
             )
             st[("mt", g)] = mt
 
         def var_sums(g):
-            ssq = small.tile([P, 2, G], F32, name="ssq")
+            ssq = small.tile([P, 2, SIZES[g]], F32, name="ssq")
             nc.vector.tensor_reduce(
                 out=ssq[:].rearrange("p o t -> p (o t)"), in_=st[("v_ps", g)][:], axis=mybir.AxisListType.X, op=ALU.add
             )
             st[("ssq", g)] = ssq
 
         def stats(g):
+            n = SIZES[g]
             ssq = st[("ssq", g)]
-            vare = small.tile([P, 2, G], F32, name="vare")
-            rstd = small.tile([P, 2, G], F32, name="rstd")
+            vare = small.tile([P, 2, n], F32, name="vare")
+            rstd = small.tile([P, 2, n], F32, name="rstd")
             nc.gpsimd.tensor_scalar(out=vare[:], in0=ssq[:], scalar1=1.0 / D, scalar2=EPS, op0=ALU.mult, op1=ALU.add)
             nc.gpsimd.tensor_tensor(
                 out=rstd[:].rearrange("p o t -> p (o t)"), in0=vare[:].rearrange("p o t -> p (o t)"),
-                in1=mhalf[:], op=ALU.pow,
+                in1=mhalf[:, 0 : 2 * n], op=ALU.pow,
             )
             st[("rstd", g)] = rstd
 
-        def turn(out, in_, start, stop):
-            nc.tensor.matmul(out=out, lhsT=in_, rhs=ident[:], is_transpose=True, start=start, stop=stop)
-
         def to_features(g):
+            n = SIZES[g]
             terms = ((st[("x1", g)], st[("sr", g)]), (st[("x2", g)], st[("c0", g)]))
             mt = st[("mt", g)]
             banks = []
             for c in range(4):
-                d_ps = ps_y.tile([P, 2, G, P], F32, name="d_ps", tag="turn")
+                d_ps = ps_y.tile([P, 2, n, P], F32, name="d_ps", tag="turn")
                 cols = slice(P * c, P * c + P)
                 for k in range(2):
                     for o in range(2):
-                        for tt in range(G):
+                        for tt in range(n):
                             turn(d_ps[:, o, tt, :], terms[o][k][:, tt, cols], k == 0 and o == 0 and tt == 0, False)
                 for o in range(2):
-                    for tt in range(G):
-                        turn(d_ps[:, o, tt, :], mt[:, G * o + tt, :], False, o == 1 and tt == G - 1)
+                    for tt in range(n):
+                        turn(d_ps[:, o, tt, :], mt[:, n * o + tt, :], False, o == 1 and tt == n - 1)
                 banks.append(d_ps)
             st[("d_ps", g)] = banks
 
         def weigh(g):
-            yt = work.tile([P, 4, 2, G, P], F32, name="yt", tag="yt", bufs=3, align_bytes=64)
-            sq = work.tile([P, 4, 2, G, P], F32, name="sq", bufs=2)
+            n = SIZES[g]
+            yt = work.tile([P, 4, 2, n, P], F32, name="yt", tag="yt", bufs=3, align_bytes=64)
+            sq = work.tile([P, 4, 2, n, P], F32, name="sq", bufs=2)
             for c in range(4):
                 nc.scalar.activation(
                     out=yt[:, c, :, :, :], in_=st[("d_ps", g)][c][:], func=ACT.Copy, scale=w_col[:, c : c + 1]
@@ -339,34 +354,33 @@ def tile_quantumcoherencelayer_t_kernel(
             st[("sq", g)] = sq
 
         def var_turn(g):
+            n = SIZES[g]
             sq = st[("sq", g)]
-            v_ps = ps_y.tile([P, 2 * G, P], F32, name="v_ps", tag="turn")
+            v_ps = ps_y.tile([P, 2 * n, P], F32, name="v_ps", tag="turn")
             for c in range(4):
                 for o in range(2):
-                    for tt in range(G):
-                        turn(v_ps[:, G * o + tt, :], sq[:, c, o, tt, :], c == 0 and o == 0 and tt == 0,
-                             c == 3 and o == 1 and tt == G - 1)
+                    for tt in range(n):
+                        turn(v_ps[:, n * o + tt, :], sq[:, c, o, tt, :], c == 0 and o == 0 and tt == 0,
+                             c == 3 and o == 1 and tt == n - 1)
             st[("v_ps", g)] = v_ps
 
-        def to_rows(g):
+        def to_rows(g, o):
             yt = st[("yt", g)]
-            banks = []
-            for o in range(2):
-                for tt in range(G):
-                    y_ps = ps_y.tile([P, D], F32, name="y_ps", tag="turn")
-                    for c in range(4):
-                        nc.tensor.transpose(y_ps[:, P * c : P * c + P], yt[:, c, o, tt, :], ident[:])
-                    banks.append(y_ps)
-            st[("y_ps", g)] = banks
+            for tt in range(SIZES[g]):
+                y_ps = ps_y.tile([P, D], F32, name="y_ps", tag="turn")
+                for c in range(4):
+                    nc.tensor.transpose(y_ps[:, P * c : P * c + P], yt[:, c, o, tt, :], ident[:])
+                st[("y_ps", g, o, tt)] = y_ps
 
         def finish(g):
-            sl = slice(G * g, G * g + G)
+            n = SIZES[g]
+            sl = slice(FIRST[g], FIRST[g] + n)
             rstd = st[("rstd", g)]
             for o, o_d in enumerate((or_d, oi_d)):
-                res = work.tile([P, G, D], F32, name="res", bufs=4)
-                for tt in range(G):
+                res = work.tile([P, n, D], F32, name="res", bufs=4)
+                for tt in range(n):
                     nc.vector.scalar_tensor_tensor(
-                        out=res[:, tt, :], in0=st[("y_ps", g)][G * o + tt][:], scalar=rstd[:, o, tt : tt + 1],
+                        out=res[:, tt, :], in0=st[("y_ps", g, o, tt)][:], scalar=rstd[:, o, tt : tt + 1],
                         in1=b_sb[:], op0=ALU.mult, op1=ALU.add,
                     )
                 nc.sync.dma_start(out=o_d[:, sl, :], in_=res[:])
@@ -377,9 +391,9 @@ def tile_quantumcoherencelayer_t_kernel(
         for g in range(HEAD):
             squares_eps(g)
             x_transposes(g)
-            x_copy(g)
+            x_copy(g, nc.vector.tensor_copy)
             quantise(g)
-            eps_sum(g)
+            eps_sum(g, nc.vector, 0, SIZES[g])
             if g == 0:
                 phase_codes()
         for g in range(HEAD):
@@ -399,7 +413,6 @@ def tile_quantumcoherencelayer_t_kernel(
         norm_constants()
         squares_plain(HEAD)
         squares_eps(HEAD)
-        square_sum(HEAD, nc.gpsimd)
 
         def step(r):
             nxt, cur, prv, new, old = r + 1, r, r - 1, r + AHEAD, r - LAG
@@ -407,11 +420,15 @@ def tile_quantumcoherencelayer_t_kernel(
                 pe_mm(nxt)
             if ok(r + 2):
                 x_transposes(r + 2)
-            if ok(old):
-                to_rows(old)
+            if ok(old) and ok(cur):
+                to_rows(old, 0)
+                to_rows(old, 1)
             if ok(prv):
                 weigh(prv)
                 var_turn(prv)
+            if ok(old) and not ok(cur):
+                to_rows(old, 0)
+                to_rows(old, 1)
             if ok(new):
                 squares_plain(new)
                 squares_eps(new)
@@ -420,35 +437,43 @@ def tile_quantumcoherencelayer_t_kernel(
             if ok(nxt):
                 coh_sums(nxt)
             small_steps = [gain_a, gain_b, gain_c] if ok(nxt) else []
-            for n in range(4 * G):
-                if ok(cur):
+            for n in range(max(4 * SIZES[cur] if ok(cur) else 0, len(small_steps))):
+                if ok(cur) and n < 4 * SIZES[cur]:
                     product(cur, n // 4, n % 4)
                 if n < len(small_steps):
                     small_steps[n](nxt)
             if ok(r + 2):
-                x_copy(r + 2)
+                x_copy(r + 2, nc.vector.tensor_copy)
             if ok(nxt):
                 reduce_range(nxt)
             if ok(cur):
                 means(cur)
-            if ok(old):
+            if ok(old) and old < NG - DRAIN:
                 stats(old)
-            if ok(new):
-                square_sum(new, nc.gpsimd)
+            for g in range(HEAD if r == 0 else new, new + 1):
+                if ok(g):
+                    square_sum(g, nc.gpsimd)
             if ok(nxt):
                 trig(nxt)
-            if ok(old):
+            if ok(cur) and not ok(nxt):
+                spread(cur)
+                to_features(cur)
+            if ok(old) and ok(nxt):
                 finish(old)
             if ok(prv):
                 var_sums(prv)
-            if ok(cur):
+                if prv >= NG - DRAIN:
+                    stats(prv)
+            if ok(old) and not ok(nxt):
+                finish(old)
+            if ok(cur) and ok(nxt):
                 spread(cur)
                 to_features(cur)
             if ok(r + 2):
                 quantise(r + 2)
             for g in range(HEAD if r == 0 else new, new + 1):
                 if ok(g):
-                    eps_sum(g)
+                    eps_sum(g, nc.vector, 0, SIZES[g])
             if r % 2 == 0:
                 for g in (r + 2, r + 3):
                     if ok(g):
@@ -456,6 +481,7 @@ def tile_quantumcoherencelayer_t_kernel(
                         root_plain(g)
             if ok(r + LOADS_AHEAD):
                 load(r + LOADS_AHEAD)
+
 
         for r in range(NG + LAG):
             step(r)

@@ -28,6 +28,7 @@ SA_BUFS = 5
 SR_BUFS = 5
 AHEAD = 3
 HEAD = 2
+SHORT = 1
 LOADS_AHEAD = 6
 LAG = 2
 DRAIN = 3
@@ -304,6 +305,29 @@ def tile_quantumcoherencelayer_t_kernel(
             )
             st[("mt", g)] = mt
 
+        def centre(g):
+            n = SIZES[g]
+            terms = ((st[("x1", g)], st[("sr", g)]), (st[("x2", g)], st[("c0", g)]))
+            mean = st[("mean", g)]
+            d = work.tile([P, 2, n, D], F32, name="d", tag="sq", bufs=2)
+            for o in range(2):
+                for tt in range(n):
+                    nc.vector.scalar_tensor_tensor(
+                        out=d[:, o, tt, :], in0=terms[o][0][:, tt, :], scalar=mean[:, o, tt : tt + 1],
+                        in1=terms[o][1][:, tt, :], op0=ALU.add, op1=ALU.add,
+                    )
+            st[("d", g)] = d
+
+        def var_direct(g):
+            n = SIZES[g]
+            d = st[("d", g)]
+            ssq = small.tile([P, 2, n], F32, name="ssq")
+            for o in range(2):
+                for tt in range(n):
+                    junk = work.tile([P, D], F32, name="sjunk", tag="vjunk", bufs=2)
+                    nc.scalar.activation(out=junk[:], in_=d[:, o, tt, :], func=ACT.Square, accum_out=ssq[:, o, tt : tt + 1])
+            st[("ssq", g)] = ssq
+
         def var_sums(g):
             ssq = small.tile([P, 2, SIZES[g]], F32, name="ssq")
             nc.vector.tensor_reduce(
@@ -326,9 +350,9 @@ def tile_quantumcoherencelayer_t_kernel(
         def to_features(g):
             n = SIZES[g]
             terms = ((st[("x1", g)], st[("sr", g)]), (st[("x2", g)], st[("c0", g)]))
-            mt = st[("mt", g)]
+            mt = st.get(("mt", g))
             banks = []
-            for c in range(4):
+            for c in range(4 if g < NG - SHORT else 0):
                 d_ps = ps_y.tile([P, 2, n, P], F32, name="d_ps", tag="turn")
                 cols = slice(P * c, P * c + P)
                 for k in range(2):
@@ -339,19 +363,26 @@ def tile_quantumcoherencelayer_t_kernel(
                     for tt in range(n):
                         turn(d_ps[:, o, tt, :], mt[:, n * o + tt, :], False, o == 1 and tt == n - 1)
                 banks.append(d_ps)
+            for c in range(4 if g >= NG - SHORT else 0):
+                d_ps = ps_y.tile([P, 2, n, P], F32, name="d_ps", tag="turn")
+                for o in range(2):
+                    for tt in range(n):
+                        nc.tensor.transpose(d_ps[:, o, tt, :], st[("d", g)][:, o, tt, P * c : P * c + P], ident[:])
+                banks.append(d_ps)
             st[("d_ps", g)] = banks
 
         def weigh(g):
             n = SIZES[g]
             yt = work.tile([P, 4, 2, n, P], F32, name="yt", tag="yt", bufs=3, align_bytes=64)
-            sq = work.tile([P, 4, 2, n, P], F32, name="sq", bufs=2)
+            if g < NG - SHORT:
+                st[("sq", g)] = work.tile([P, 4, 2, n, P], F32, name="sq", tag="sq", bufs=2)
             for c in range(4):
                 nc.scalar.activation(
                     out=yt[:, c, :, :, :], in_=st[("d_ps", g)][c][:], func=ACT.Copy, scale=w_col[:, c : c + 1]
                 )
-                nc.scalar.activation(out=sq[:, c, :, :, :], in_=st[("d_ps", g)][c][:], func=ACT.Square)
+                if g < NG - SHORT:
+                    nc.scalar.activation(out=st[("sq", g)][:, c, :, :, :], in_=st[("d_ps", g)][c][:], func=ACT.Square)
             st[("yt", g)] = yt
-            st[("sq", g)] = sq
 
         def var_turn(g):
             n = SIZES[g]
@@ -414,6 +445,9 @@ def tile_quantumcoherencelayer_t_kernel(
         squares_plain(HEAD)
         squares_eps(HEAD)
 
+        def short(g):
+            return g >= NG - SHORT
+
         def step(r):
             nxt, cur, prv, new, old = r + 1, r, r - 1, r + AHEAD, r - LAG
             if ok(nxt):
@@ -425,7 +459,8 @@ def tile_quantumcoherencelayer_t_kernel(
                 to_rows(old, 1)
             if ok(prv):
                 weigh(prv)
-                var_turn(prv)
+                if not short(prv):
+                    var_turn(prv)
             if ok(old) and not ok(cur):
                 to_rows(old, 0)
                 to_rows(old, 1)
@@ -455,18 +490,24 @@ def tile_quantumcoherencelayer_t_kernel(
                     square_sum(g, nc.gpsimd)
             if ok(nxt):
                 trig(nxt)
-            if ok(cur) and not ok(nxt):
+            if ok(cur) and short(cur):
+                centre(cur)
+                var_direct(cur)
+                to_features(cur)
+            elif ok(cur) and not ok(nxt):
                 spread(cur)
                 to_features(cur)
             if ok(old) and ok(nxt):
                 finish(old)
-            if ok(prv):
+            if ok(prv) and not short(prv):
                 var_sums(prv)
                 if prv >= NG - DRAIN:
                     stats(prv)
+            if ok(cur) and short(cur):
+                stats(cur)
             if ok(old) and not ok(nxt):
                 finish(old)
-            if ok(cur) and ok(nxt):
+            if ok(cur) and ok(nxt) and not short(cur):
                 spread(cur)
                 to_features(cur)
             if ok(r + 2):

@@ -49,9 +49,7 @@ def tile_quantumcoherencelayer_t_kernel(
         keep = ctx.enter_context(tc.tile_pool(name="keep", bufs=1))
         work = ctx.enter_context(tc.tile_pool(name="work", bufs=1))
         small = ctx.enter_context(tc.tile_pool(name="small", bufs=6))
-        ps_p = ctx.enter_context(tc.psum_pool(name="ps_p", bufs=2))
-        ps_t = ctx.enter_context(tc.psum_pool(name="ps_t", bufs=1))
-        ps_y = ctx.enter_context(tc.psum_pool(name="ps_y", bufs=5))
+        ps = ctx.enter_context(tc.psum_pool(name="ps", bufs=8))
 
         ph_raw = work.tile([P, 4, D], BF16, name="ph_raw", tag="yt", bufs=3, align_bytes=64)
         ph_grp = work.tile([P, D, 4], BF16, name="ph_grp", tag="yt", bufs=3, align_bytes=64)
@@ -117,10 +115,10 @@ def tile_quantumcoherencelayer_t_kernel(
             )
 
         def norm_constants():
-            b_ps = ps_y.tile([P, D], F32, name="b_ps", tag="turn")
+            b_ps = ps.tile([P, D], F32, name="b_ps", tag="bank")
             nc.tensor.matmul(out=b_ps[:], lhsT=ones[:], rhs=b_row[:], start=True, stop=True)
             nc.vector.tensor_copy(out=b_sb[:], in_=b_ps[:])
-            w_ps = ps_y.tile([P, P], BF16, name="w_ps", tag="turn")
+            w_ps = ps.tile([P, P], BF16, name="w_ps", tag="bank")
             nc.tensor.transpose(w_ps[:], w_rows[:], ident_bf[:])
             nc.vector.tensor_copy(out=w_col[:], in_=w_ps[:, 0:4])
 
@@ -165,7 +163,7 @@ def tile_quantumcoherencelayer_t_kernel(
             xr_words = st[("xr", g)][:].rearrange("p t d -> p (t d)").bitcast(F32).rearrange(
                 "p (t j u) -> p t u j", t=n, u=2
             )
-            xt = ps_t.tile([P, n, 2, P], F32, name="xt")
+            xt = ps.tile([P, n, 2, P], F32, name="xt", tag="bank")
             for tt in range(n):
                 for u in range(2):
                     nc.tensor.transpose(xt[:, tt, u, :], xr_words[:, tt, u, :], ident[:])
@@ -190,7 +188,7 @@ def tile_quantumcoherencelayer_t_kernel(
             xc, xs = st[("xc", g)], st[("xs", g)]
             pts = []
             for tt in range(SIZES[g]):
-                pt = ps_p.tile([P, D], F32, name="pt")
+                pt = ps.tile([P, D], F32, name="pt", tag="bank")
                 cols = slice(P * tt, P * tt + P)
                 nc.tensor.matmul_mx(
                     out=pt[:],
@@ -220,19 +218,14 @@ def tile_quantumcoherencelayer_t_kernel(
         def gain_a(g):
             coh = st[("coh", g)]
             csq = small.tile([P, 2, SIZES[g]], F32, name="csq")
-            nc.vector.tensor_tensor(out=csq[:], in0=coh[:], in1=coh[:], op=ALU.mult)
+            nc.vector.scalar_tensor_tensor(out=csq[:], in0=coh[:], scalar=ncf[:], in1=coh[:], op0=ALU.mult, op1=ALU.mult)
             st[("csq", g)] = csq
 
         def gain_b(g):
             csq = st[("csq", g)]
-            csum = small.tile([P, SIZES[g]], F32, name="csum")
-            nc.vector.tensor_tensor(out=csum[:], in0=csq[:, 0, :], in1=csq[:, 1, :], op=ALU.add)
-            st[("csum", g)] = csum
-
-        def gain_c(g):
             gq = small.tile([P, SIZES[g]], F32, name="gq")
-            nc.vector.tensor_scalar(
-                out=gq[:], in0=st[("csum", g)][:], scalar1=ncf[:], scalar2=cfs[:], op0=ALU.mult, op1=ALU.add
+            nc.vector.scalar_tensor_tensor(
+                out=gq[:], in0=csq[:, 0, :], scalar=cfs[:], in1=csq[:, 1, :], op0=ALU.add, op1=ALU.add
             )
             st[("gq", g)] = gq
 
@@ -265,16 +258,18 @@ def tile_quantumcoherencelayer_t_kernel(
             st[("cc", g)] = cc
             st[("ss", g)] = ss
 
-        def unit(g):
+        def unit_real(g):
             n = SIZES[g]
             c0 = work.tile([P, n, D], F32, name="c0", bufs=2)
-            q = st[("sr", g)]
-            nc.vector.tensor_tensor(out=c0[:], in0=st[("xr", g)][:], in1=q[:], op=ALU.mult)
-            nc.vector.tensor_tensor(out=q[:], in0=st[("xi", g)][:], in1=q[:], op=ALU.mult)
+            nc.vector.tensor_tensor(out=c0[:], in0=st[("xr", g)][:], in1=st[("sr", g)][:], op=ALU.mult)
             st[("c0", g)] = c0
             st[("x1", g)] = work.tile([P, n, D], F32, name="x1", bufs=2)
             st[("x2", g)] = work.tile([P, n, D], F32, name="x2", bufs=2)
             st[("sm", g)] = small.tile([P, 2, 2, n], F32, name="sm")
+
+        def unit_imag(g):
+            q = st[("sr", g)]
+            nc.vector.tensor_tensor(out=q[:], in0=st[("xi", g)][:], in1=q[:], op=ALU.mult)
 
         def product(g, tt, k):
             c0, q, cc, ss = st[("c0", g)], st[("sr", g)], st[("cc", g)], st[("ss", g)]
@@ -353,7 +348,7 @@ def tile_quantumcoherencelayer_t_kernel(
             mt = st.get(("mt", g))
             banks = []
             for c in range(4 if g < NG - SHORT else 0):
-                d_ps = ps_y.tile([P, 2, n, P], F32, name="d_ps", tag="turn")
+                d_ps = ps.tile([P, 2, n, P], F32, name="d_ps", tag="bank")
                 cols = slice(P * c, P * c + P)
                 for k in range(2):
                     for o in range(2):
@@ -364,7 +359,7 @@ def tile_quantumcoherencelayer_t_kernel(
                         turn(d_ps[:, o, tt, :], mt[:, n * o + tt, :], False, o == 1 and tt == n - 1)
                 banks.append(d_ps)
             for c in range(4 if g >= NG - SHORT else 0):
-                d_ps = ps_y.tile([P, 2, n, P], F32, name="d_ps", tag="turn")
+                d_ps = ps.tile([P, 2, n, P], F32, name="d_ps", tag="bank")
                 for o in range(2):
                     for tt in range(n):
                         nc.tensor.transpose(d_ps[:, o, tt, :], st[("d", g)][:, o, tt, P * c : P * c + P], ident[:])
@@ -387,7 +382,7 @@ def tile_quantumcoherencelayer_t_kernel(
         def var_turn(g):
             n = SIZES[g]
             sq = st[("sq", g)]
-            v_ps = ps_y.tile([P, 2 * n, P], F32, name="v_ps", tag="turn")
+            v_ps = ps.tile([P, 2 * n, P], F32, name="v_ps", tag="bank")
             for c in range(4):
                 for o in range(2):
                     for tt in range(n):
@@ -398,23 +393,21 @@ def tile_quantumcoherencelayer_t_kernel(
         def to_rows(g, o):
             yt = st[("yt", g)]
             for tt in range(SIZES[g]):
-                y_ps = ps_y.tile([P, D], F32, name="y_ps", tag="turn")
+                y_ps = ps.tile([P, D], F32, name="y_ps", tag="bank")
                 for c in range(4):
                     nc.tensor.transpose(y_ps[:, P * c : P * c + P], yt[:, c, o, tt, :], ident[:])
                 st[("y_ps", g, o, tt)] = y_ps
 
-        def finish(g):
+        def finish(g, o):
             n = SIZES[g]
-            sl = slice(FIRST[g], FIRST[g] + n)
             rstd = st[("rstd", g)]
-            for o, o_d in enumerate((or_d, oi_d)):
-                res = work.tile([P, n, D], F32, name="res", bufs=4)
-                for tt in range(n):
-                    nc.vector.scalar_tensor_tensor(
-                        out=res[:, tt, :], in0=st[("y_ps", g, o, tt)][:], scalar=rstd[:, o, tt : tt + 1],
-                        in1=b_sb[:], op0=ALU.mult, op1=ALU.add,
-                    )
-                nc.sync.dma_start(out=o_d[:, sl, :], in_=res[:])
+            res = work.tile([P, n, D], F32, name="res", bufs=4)
+            for tt in range(n):
+                nc.vector.scalar_tensor_tensor(
+                    out=res[:, tt, :], in0=st[("y_ps", g, o, tt)][:], scalar=rstd[:, o, tt : tt + 1],
+                    in1=b_sb[:], op0=ALU.mult, op1=ALU.add,
+                )
+            nc.sync.dma_start(out=(or_d, oi_d)[o][:, FIRST[g] : FIRST[g] + n, :], in_=res[:])
 
         ctx.enter_context(tc.manual_schedule(engines={ENG.DVE, ENG.Activation, ENG.Pool, ENG.PE}))
 
@@ -435,7 +428,6 @@ def tile_quantumcoherencelayer_t_kernel(
         coh_sums(0)
         gain_a(0)
         gain_b(0)
-        gain_c(0)
         reduce_range(0)
         for g in range(HEAD):
             square_sum(g, nc.vector)
@@ -467,11 +459,12 @@ def tile_quantumcoherencelayer_t_kernel(
             if ok(new):
                 squares_plain(new)
                 squares_eps(new)
-            if ok(cur):
-                unit(cur)
+            if r == 0:
+                unit_real(cur)
+                unit_imag(cur)
             if ok(nxt):
                 coh_sums(nxt)
-            small_steps = [gain_a, gain_b, gain_c] if ok(nxt) else []
+            small_steps = [gain_a, gain_b] if ok(nxt) else []
             for n in range(max(4 * SIZES[cur] if ok(cur) else 0, len(small_steps))):
                 if ok(cur) and n < 4 * SIZES[cur]:
                     product(cur, n // 4, n % 4)
@@ -491,30 +484,41 @@ def tile_quantumcoherencelayer_t_kernel(
             if ok(nxt):
                 trig(nxt)
             if ok(cur) and short(cur):
+                if ok(old):
+                    finish(old, 0)
                 centre(cur)
                 var_direct(cur)
                 to_features(cur)
             elif ok(cur) and not ok(nxt):
                 spread(cur)
                 to_features(cur)
-            if ok(old) and ok(nxt):
-                finish(old)
-            if ok(prv) and not short(prv):
+            early = ok(prv) and prv >= NG - DRAIN and not short(prv)
+            if early:
                 var_sums(prv)
-                if prv >= NG - DRAIN:
-                    stats(prv)
+                stats(prv)
+            if ok(old) and ok(nxt):
+                finish(old, 0)
+                finish(old, 1)
+            if ok(prv) and not short(prv) and not early:
+                var_sums(prv)
             if ok(cur) and short(cur):
                 stats(cur)
             if ok(old) and not ok(nxt):
-                finish(old)
+                if not (ok(cur) and short(cur)):
+                    finish(old, 0)
+                finish(old, 1)
             if ok(cur) and ok(nxt) and not short(cur):
                 spread(cur)
                 to_features(cur)
             if ok(r + 2):
                 quantise(r + 2)
+            if ok(nxt):
+                unit_real(nxt)
             for g in range(HEAD if r == 0 else new, new + 1):
                 if ok(g):
                     eps_sum(g, nc.vector, 0, SIZES[g])
+            if ok(nxt):
+                unit_imag(nxt)
             if r % 2 == 0:
                 for g in (r + 2, r + 3):
                     if ok(g):

@@ -24,8 +24,7 @@ FIRST = [sum(SIZES[:g]) for g in range(NG)]
 GMAX = max(SIZES)
 EPS = 1e-8
 TWO_PI = 2.0 * math.pi
-SA_BUFS = 5
-SR_BUFS = 5
+SUM_BUFS = 5
 AHEAD = 3
 HEAD = 2
 SHORT = 1
@@ -79,12 +78,12 @@ def tile_quantumcoherencelayer_t_kernel(
         def load(g):
             n = SIZES[g]
             sl = slice(FIRST[g], FIRST[g] + n)
-            xr = work.tile([P, n, D], BF16, name="xr", bufs=LOADS_AHEAD, align_bytes=64)
-            xi = work.tile([P, n, D], BF16, name="xi", bufs=LOADS_AHEAD, align_bytes=64)
-            nc.sync.dma_start(out=xr[:], in_=xr_d[:, sl, :])
-            nc.sync.dma_start(out=xi[:], in_=xi_d[:, sl, :])
-            st[("xr", g)] = xr
-            st[("xi", g)] = xi
+            x = work.tile([P, 2, n, D], BF16, name="x", bufs=LOADS_AHEAD, align_bytes=64)
+            nc.sync.dma_start(out=x[:, 0, :, :], in_=xr_d[:, sl, :])
+            nc.sync.dma_start(out=x[:, 1, :, :], in_=xi_d[:, sl, :])
+            st[("x", g)] = x
+            st[("xr", g)] = x[:, 0, :, :]
+            st[("xi", g)] = x[:, 1, :, :]
 
         load(0)
         nc.sync.dma_start(out=ph_raw[:], in_=phase_matrix.rearrange("(p j) n -> p j n", j=4))
@@ -125,30 +124,28 @@ def tile_quantumcoherencelayer_t_kernel(
         def turn(out, in_, start, stop):
             nc.tensor.matmul(out=out, lhsT=in_, rhs=ident[:], is_transpose=True, start=start, stop=stop)
 
+        def squares(g, key, **shift):
+            sq = work.tile([P, 2, SIZES[g], D], F32, name="x" + key, bufs=2)
+            nc.scalar.activation(out=sq[:], in_=st[("x", g)][:], func=ACT.Square, **shift)
+            st[("x" + key, g)] = sq
+
         def squares_plain(g):
-            n = SIZES[g]
-            sr = work.tile([P, n, D], F32, name="sr", bufs=SR_BUFS)
-            si = work.tile([P, n, D], F32, name="si", bufs=2)
-            nc.scalar.activation(out=sr[:], in_=st[("xr", g)][:], func=ACT.Square)
-            nc.scalar.activation(out=si[:], in_=st[("xi", g)][:], func=ACT.Square)
-            st[("sr", g)], st[("si", g)] = sr, si
+            squares(g, "sr")
 
         def squares_eps(g):
-            n = SIZES[g]
-            sa = work.tile([P, n, D], F32, name="sa", bufs=SA_BUFS)
-            sb = work.tile([P, n, D], F32, name="sb", bufs=2)
-            nc.scalar.activation(out=sa[:], in_=st[("xr", g)][:], func=ACT.Square, bias=eps_t[:])
-            nc.scalar.activation(out=sb[:], in_=st[("xi", g)][:], func=ACT.Square, bias=eps_t[:])
-            st[("sa", g)], st[("sb", g)] = sa, sb
+            squares(g, "sa", bias=eps_t[:])
+
+        def add_squares(g, key, eng):
+            sq = st[("x" + key, g)]
+            out = work.tile([P, SIZES[g], D], F32, name=key, bufs=SUM_BUFS)
+            eng.tensor_tensor(out=out[:], in0=sq[:, 0, :, :], in1=sq[:, 1, :, :], op=ALU.add)
+            st[(key, g)] = out
 
         def square_sum(g, eng):
-            sr = st[("sr", g)]
-            eng.tensor_tensor(out=sr[:], in0=sr[:], in1=st[("si", g)][:], op=ALU.add)
+            add_squares(g, "sr", eng)
 
-        def eps_sum(g, eng, lo, hi):
-            sa, sb = st[("sa", g)], st[("sb", g)]
-            if hi > lo:
-                eng.tensor_tensor(out=sa[:, lo:hi, :], in0=sa[:, lo:hi, :], in1=sb[:, lo:hi, :], op=ALU.add)
+        def eps_sum(g):
+            add_squares(g, "sa", nc.vector)
 
         def root_eps(g):
             sa = st[("sa", g)]
@@ -160,7 +157,7 @@ def tile_quantumcoherencelayer_t_kernel(
 
         def x_transposes(g):
             n = SIZES[g]
-            xr_words = st[("xr", g)][:].rearrange("p t d -> p (t d)").bitcast(F32).rearrange(
+            xr_words = st[("xr", g)].rearrange("p t d -> p (t d)").bitcast(F32).rearrange(
                 "p (t j u) -> p t u j", t=n, u=2
             )
             xt = ps.tile([P, n, 2, P], F32, name="xt", tag="bank")
@@ -250,66 +247,57 @@ def tile_quantumcoherencelayer_t_kernel(
         def trig(g):
             n = SIZES[g]
             fr = st[("fr", g)]
-            cc = work.tile([P, n, D], F32, name="cc", bufs=2)
-            ss = work.tile([P, n, D], F32, name="ss", bufs=2)
-            nc.scalar.activation(out=cc[:], in_=fr[:], func=ACT.Abs)
-            nc.scalar.activation(out=ss[:], in_=fr[:], func=ACT.Sin, scale=TWO_PI)
-            nc.scalar.activation(out=cc[:], in_=cc[:], func=ACT.Sin, scale=-TWO_PI, bias=hpi_t[:])
-            st[("cc", g)] = cc
-            st[("ss", g)] = ss
+            sc = work.tile([P, n, 2, D], F32, name="sc", bufs=2)
+            ss, cc = sc[:, :, 0, :], sc[:, :, 1, :]
+            nc.scalar.activation(out=cc, in_=fr[:], func=ACT.Abs)
+            nc.scalar.activation(out=ss, in_=fr[:], func=ACT.Sin, scale=TWO_PI)
+            nc.scalar.activation(out=cc, in_=cc, func=ACT.Sin, scale=-TWO_PI, bias=hpi_t[:])
+            st[("sc", g)] = sc
 
-        def unit_real(g):
+        def unit(g):
             n = SIZES[g]
-            c0 = work.tile([P, n, D], F32, name="c0", bufs=2)
-            nc.vector.tensor_tensor(out=c0[:], in0=st[("xr", g)][:], in1=st[("sr", g)][:], op=ALU.mult)
-            st[("c0", g)] = c0
-            st[("x1", g)] = work.tile([P, n, D], F32, name="x1", bufs=2)
-            st[("x2", g)] = work.tile([P, n, D], F32, name="x2", bufs=2)
-            st[("sm", g)] = small.tile([P, 2, 2, n], F32, name="sm")
+            u = work.tile([P, n, 2, D], F32, name="u", bufs=2)
+            nc.vector.tensor_tensor(
+                out=u[:], in0=st[("x", g)][:].rearrange("p k t d -> p t k d"),
+                in1=st[("sr", g)][:].unsqueeze(2).to_broadcast([P, n, 2, D]), op=ALU.mult,
+            )
+            st[("u", g)] = u
+            st[("v", g)] = work.tile([P, n, 2, D], F32, name="v", bufs=2)
+            st[("sm", g)] = small.tile([P, 3, n], F32, name="sm")
 
-        def unit_imag(g):
-            q = st[("sr", g)]
-            nc.vector.tensor_tensor(out=q[:], in0=st[("xi", g)][:], in1=q[:], op=ALU.mult)
-
-        def product(g, tt, k):
-            c0, q, cc, ss = st[("c0", g)], st[("sr", g)], st[("cc", g)], st[("ss", g)]
-            out_t, in_t, sgn, trg, a, o = (
-                (c0, c0, 1.0, ss, 0, 1), (q, q, -1.0, ss, 1, 0),
-            )[k - 2] if k >= 2 else (
-                (st[("x1", g)], c0, 1.0, cc, 0, 0), (st[("x2", g)], q, 1.0, cc, 1, 1),
-            )[k]
+        def product_imag(g, tt):
             nc.vector.scalar_tensor_tensor(
-                out=out_t[:, tt, :], in0=in_t[:, tt, :], scalar=sgn, in1=trg[:, tt, :],
-                op0=ALU.mult, op1=ALU.mult, accum_out=st[("sm", g)][:, a, o, tt : tt + 1],
+                out=st[("v", g)][:, tt, :, :], in0=st[("u", g)][:, tt, :, :], scalar=1.0, in1=st[("sc", g)][:, tt, :, :],
+                op0=ALU.mult, op1=ALU.mult, accum_out=st[("sm", g)][:, 1, tt : tt + 1],
+            )
+
+        def product_real(g, tt, k):
+            u = st[("u", g)][:, tt, k, :]
+            nc.vector.scalar_tensor_tensor(
+                out=u, in0=u, scalar=(1.0, -1.0)[k], in1=st[("sc", g)][:, tt, 1 - k, :],
+                op0=ALU.mult, op1=ALU.mult, accum_out=st[("sm", g)][:, 2 * k, tt : tt + 1],
             )
 
         def means(g):
             n = SIZES[g]
             sm = st[("sm", g)]
-            msum = small.tile([P, 2, n], F32, name="msum")
             mean = small.tile([P, 2, n], F32, name="mean")
-            nc.gpsimd.tensor_tensor(out=msum[:], in0=sm[:, 0, :, :], in1=sm[:, 1, :, :], op=ALU.add)
-            nc.gpsimd.tensor_scalar(out=mean[:], in0=msum[:], scalar1=-1.0 / D, scalar2=0.0, op0=ALU.mult, op1=ALU.add)
-            st[("mean", g)] = mean
-
-        def spread(g):
-            n = SIZES[g]
-            mt = work.tile([P, 2 * n, P], F32, name="mt", bufs=2)
-            nc.vector.tensor_copy(
-                out=mt[:], in_=st[("mean", g)][:].rearrange("p o t -> p (o t)").unsqueeze(2).to_broadcast([P, 2 * n, P])
+            nc.gpsimd.tensor_tensor(out=sm[:, 0, :], in0=sm[:, 0, :], in1=sm[:, 2, :], op=ALU.add)
+            nc.gpsimd.tensor_scalar(
+                out=mean[:], in0=sm[:, 0:2, :], scalar1=-1.0 / D, scalar2=0.0, op0=ALU.mult, op1=ALU.add
             )
-            st[("mt", g)] = mt
+            st[("mean", g)] = mean
 
         def centre(g):
             n = SIZES[g]
-            terms = ((st[("x1", g)], st[("sr", g)]), (st[("x2", g)], st[("c0", g)]))
+            terms = (st[("u", g)], st[("v", g)])
             mean = st[("mean", g)]
             d = work.tile([P, 2, n, D], F32, name="d", tag="sq", bufs=2)
             for o in range(2):
                 for tt in range(n):
                     nc.vector.scalar_tensor_tensor(
-                        out=d[:, o, tt, :], in0=terms[o][0][:, tt, :], scalar=mean[:, o, tt : tt + 1],
-                        in1=terms[o][1][:, tt, :], op0=ALU.add, op1=ALU.add,
+                        out=d[:, o, tt, :], in0=terms[o][:, tt, 0, :], scalar=mean[:, o, tt : tt + 1],
+                        in1=terms[o][:, tt, 1, :], op0=ALU.add, op1=ALU.add,
                     )
             st[("d", g)] = d
 
@@ -344,8 +332,8 @@ def tile_quantumcoherencelayer_t_kernel(
 
         def to_features(g):
             n = SIZES[g]
-            terms = ((st[("x1", g)], st[("sr", g)]), (st[("x2", g)], st[("c0", g)]))
-            mt = st.get(("mt", g))
+            terms = (st[("u", g)], st[("v", g)])
+            mean = st[("mean", g)]
             banks = []
             for c in range(4 if g < NG - SHORT else 0):
                 d_ps = ps.tile([P, 2, n, P], F32, name="d_ps", tag="bank")
@@ -353,10 +341,10 @@ def tile_quantumcoherencelayer_t_kernel(
                 for k in range(2):
                     for o in range(2):
                         for tt in range(n):
-                            turn(d_ps[:, o, tt, :], terms[o][k][:, tt, cols], k == 0 and o == 0 and tt == 0, False)
+                            turn(d_ps[:, o, tt, :], terms[o][:, tt, k, cols], k == 0 and o == 0 and tt == 0, False)
                 for o in range(2):
                     for tt in range(n):
-                        turn(d_ps[:, o, tt, :], mt[:, n * o + tt, :], False, o == 1 and tt == n - 1)
+                        turn(d_ps[:, o, tt, :], mean[:, o, tt : tt + 1].to_broadcast([P, P]), False, o == 1 and tt == n - 1)
                 banks.append(d_ps)
             for c in range(4 if g >= NG - SHORT else 0):
                 d_ps = ps.tile([P, 2, n, P], F32, name="d_ps", tag="bank")
@@ -417,7 +405,7 @@ def tile_quantumcoherencelayer_t_kernel(
             x_transposes(g)
             x_copy(g, nc.vector.tensor_copy)
             quantise(g)
-            eps_sum(g, nc.vector, 0, SIZES[g])
+            eps_sum(g)
             if g == 0:
                 phase_codes()
         for g in range(HEAD):
@@ -460,16 +448,21 @@ def tile_quantumcoherencelayer_t_kernel(
                 squares_plain(new)
                 squares_eps(new)
             if r == 0:
-                unit_real(cur)
-                unit_imag(cur)
+                unit(cur)
             if ok(nxt):
                 coh_sums(nxt)
-            small_steps = [gain_a, gain_b] if ok(nxt) else []
-            for n in range(max(4 * SIZES[cur] if ok(cur) else 0, len(small_steps))):
-                if ok(cur) and n < 4 * SIZES[cur]:
-                    product(cur, n // 4, n % 4)
-                if n < len(small_steps):
-                    small_steps[n](nxt)
+            if ok(cur):
+                product_imag(cur, 0)
+            if ok(nxt):
+                gain_a(nxt)
+            if ok(cur):
+                product_imag(cur, 1)
+            if ok(nxt):
+                gain_b(nxt)
+            if ok(cur):
+                for k in range(2):
+                    for tt in range(SIZES[cur]):
+                        product_real(cur, tt, k)
             if ok(r + 2):
                 x_copy(r + 2, nc.vector.tensor_copy)
             if ok(nxt):
@@ -490,7 +483,6 @@ def tile_quantumcoherencelayer_t_kernel(
                 var_direct(cur)
                 to_features(cur)
             elif ok(cur) and not ok(nxt):
-                spread(cur)
                 to_features(cur)
             early = ok(prv) and prv >= NG - DRAIN and not short(prv)
             if early:
@@ -508,17 +500,14 @@ def tile_quantumcoherencelayer_t_kernel(
                     finish(old, 0)
                 finish(old, 1)
             if ok(cur) and ok(nxt) and not short(cur):
-                spread(cur)
                 to_features(cur)
             if ok(r + 2):
                 quantise(r + 2)
-            if ok(nxt):
-                unit_real(nxt)
             for g in range(HEAD if r == 0 else new, new + 1):
                 if ok(g):
-                    eps_sum(g, nc.vector, 0, SIZES[g])
+                    eps_sum(g)
             if ok(nxt):
-                unit_imag(nxt)
+                unit(nxt)
             if r % 2 == 0:
                 for g in (r + 2, r + 3):
                     if ok(g):

@@ -27,10 +27,9 @@ TWO_PI = 2.0 * math.pi
 SUM_BUFS = 5
 AHEAD = 3
 HEAD = 2
-SHORT = 1
 LOADS_AHEAD = 6
 LAG = 2
-DRAIN = 3
+IDLE_SUMS = (NG - 4, NG - 3, NG - 2)
 
 FLOPS = 2 * ROWS * D * D
 
@@ -318,6 +317,17 @@ def tile_quantumcoherencelayer_t_kernel(
             )
             st[("ssq", g)] = ssq
 
+        def var_sums_scalar(g):
+            n = SIZES[g]
+            ssq = small.tile([P, 2, n], F32, name="ssq")
+            for o in range(2):
+                for tt in range(n):
+                    junk = work.tile([P, P], F32, name="cjunk", tag="vjunk", bufs=2)
+                    nc.scalar.activation(
+                        out=junk[:], in_=st[("v_ps", g)][:, n * o + tt, :], func=ACT.Copy, accum_out=ssq[:, o, tt : tt + 1]
+                    )
+            st[("ssq", g)] = ssq
+
         def stats(g):
             n = SIZES[g]
             ssq = st[("ssq", g)]
@@ -335,7 +345,7 @@ def tile_quantumcoherencelayer_t_kernel(
             terms = (st[("u", g)], st[("v", g)])
             mean = st[("mean", g)]
             banks = []
-            for c in range(4 if g < NG - SHORT else 0):
+            for c in range(4):
                 d_ps = ps.tile([P, 2, n, P], F32, name="d_ps", tag="bank")
                 cols = slice(P * c, P * c + P)
                 for k in range(2):
@@ -346,10 +356,14 @@ def tile_quantumcoherencelayer_t_kernel(
                     for tt in range(n):
                         turn(d_ps[:, o, tt, :], mean[:, o, tt : tt + 1].to_broadcast([P, P]), False, o == 1 and tt == n - 1)
                 banks.append(d_ps)
-            for c in range(4 if g >= NG - SHORT else 0):
-                d_ps = ps.tile([P, 2, n, P], F32, name="d_ps", tag="bank")
+            st[("d_ps", g)] = banks
+
+        def last_to_features(g):
+            banks = []
+            for c in range(4):
+                d_ps = ps.tile([P, 2, SIZES[g], P], F32, name="d_ps", tag="bank")
                 for o in range(2):
-                    for tt in range(n):
+                    for tt in range(SIZES[g]):
                         nc.tensor.transpose(d_ps[:, o, tt, :], st[("d", g)][:, o, tt, P * c : P * c + P], ident[:])
                 banks.append(d_ps)
             st[("d_ps", g)] = banks
@@ -357,13 +371,13 @@ def tile_quantumcoherencelayer_t_kernel(
         def weigh(g):
             n = SIZES[g]
             yt = work.tile([P, 4, 2, n, P], F32, name="yt", tag="yt", bufs=3, align_bytes=64)
-            if g < NG - SHORT:
+            if g < NG - 1:
                 st[("sq", g)] = work.tile([P, 4, 2, n, P], F32, name="sq", tag="sq", bufs=2)
             for c in range(4):
                 nc.scalar.activation(
                     out=yt[:, c, :, :, :], in_=st[("d_ps", g)][c][:], func=ACT.Copy, scale=w_col[:, c : c + 1]
                 )
-                if g < NG - SHORT:
+                if g < NG - 1:
                     nc.scalar.activation(out=st[("sq", g)][:, c, :, :, :], in_=st[("d_ps", g)][c][:], func=ACT.Square)
             st[("yt", g)] = yt
 
@@ -395,7 +409,10 @@ def tile_quantumcoherencelayer_t_kernel(
                     out=res[:, tt, :], in0=st[("y_ps", g, o, tt)][:], scalar=rstd[:, o, tt : tt + 1],
                     in1=b_sb[:], op0=ALU.mult, op1=ALU.add,
                 )
-            nc.sync.dma_start(out=(or_d, oi_d)[o][:, FIRST[g] : FIRST[g] + n, :], in_=res[:])
+                if g == NG - 1:
+                    nc.sync.dma_start(out=(or_d, oi_d)[o][:, FIRST[g] + tt, :], in_=res[:, tt, :])
+            if g < NG - 1:
+                nc.sync.dma_start(out=(or_d, oi_d)[o][:, FIRST[g] : FIRST[g] + n, :], in_=res[:])
 
         ctx.enter_context(tc.manual_schedule(engines={ENG.DVE, ENG.Activation, ENG.Pool, ENG.PE}))
 
@@ -405,9 +422,9 @@ def tile_quantumcoherencelayer_t_kernel(
             x_transposes(g)
             x_copy(g, nc.vector.tensor_copy)
             quantise(g)
-            eps_sum(g)
             if g == 0:
                 phase_codes()
+            eps_sum(g)
         for g in range(HEAD):
             root_eps(g)
         for g in range(HEAD):
@@ -425,89 +442,61 @@ def tile_quantumcoherencelayer_t_kernel(
         squares_plain(HEAD)
         squares_eps(HEAD)
 
-        def short(g):
-            return g >= NG - SHORT
+        def rotate(g, weave):
+            for tt in range(SIZES[g]):
+                product_imag(g, tt)
+                if weave:
+                    weave[tt](g + 1)
+            for k in range(2):
+                for tt in range(SIZES[g]):
+                    product_real(g, tt, k)
 
         def step(r):
             nxt, cur, prv, new, old = r + 1, r, r - 1, r + AHEAD, r - LAG
-            if ok(nxt):
-                pe_mm(nxt)
+            pe_mm(nxt)
             if ok(r + 2):
                 x_transposes(r + 2)
-            if ok(old) and ok(cur):
+            if ok(old):
                 to_rows(old, 0)
                 to_rows(old, 1)
             if ok(prv):
                 weigh(prv)
-                if not short(prv):
-                    var_turn(prv)
-            if ok(old) and not ok(cur):
-                to_rows(old, 0)
-                to_rows(old, 1)
+                var_turn(prv)
             if ok(new):
                 squares_plain(new)
                 squares_eps(new)
+            if r + 2 == NG - 1:
+                x_copy(r + 2, nc.scalar.copy)
             if r == 0:
                 unit(cur)
-            if ok(nxt):
-                coh_sums(nxt)
-            if ok(cur):
-                product_imag(cur, 0)
-            if ok(nxt):
-                gain_a(nxt)
-            if ok(cur):
-                product_imag(cur, 1)
-            if ok(nxt):
-                gain_b(nxt)
-            if ok(cur):
-                for k in range(2):
-                    for tt in range(SIZES[cur]):
-                        product_real(cur, tt, k)
-            if ok(r + 2):
+            coh_sums(nxt)
+            rotate(cur, (gain_a, gain_b))
+            if r + 2 < NG - 1:
                 x_copy(r + 2, nc.vector.tensor_copy)
-            if ok(nxt):
-                reduce_range(nxt)
-            if ok(cur):
-                means(cur)
-            if ok(old) and old < NG - DRAIN:
+            reduce_range(nxt)
+            means(cur)
+            if ok(old):
                 stats(old)
             for g in range(HEAD if r == 0 else new, new + 1):
                 if ok(g):
                     square_sum(g, nc.gpsimd)
-            if ok(nxt):
-                trig(nxt)
-            if ok(cur) and short(cur):
-                if ok(old):
-                    finish(old, 0)
-                centre(cur)
-                var_direct(cur)
-                to_features(cur)
-            elif ok(cur) and not ok(nxt):
-                to_features(cur)
-            early = ok(prv) and prv >= NG - DRAIN and not short(prv)
-            if early:
-                var_sums(prv)
+            if prv in IDLE_SUMS:
+                var_sums_scalar(prv)
+            trig(nxt)
+            if prv == NG - 3:
                 stats(prv)
-            if ok(old) and ok(nxt):
+            if ok(old):
                 finish(old, 0)
                 finish(old, 1)
-            if ok(prv) and not short(prv) and not early:
+            if ok(prv) and prv not in IDLE_SUMS:
                 var_sums(prv)
-            if ok(cur) and short(cur):
-                stats(cur)
-            if ok(old) and not ok(nxt):
-                if not (ok(cur) and short(cur)):
-                    finish(old, 0)
-                finish(old, 1)
-            if ok(cur) and ok(nxt) and not short(cur):
-                to_features(cur)
+            to_features(cur)
             if ok(r + 2):
                 quantise(r + 2)
             for g in range(HEAD if r == 0 else new, new + 1):
                 if ok(g):
                     eps_sum(g)
-            if ok(nxt):
-                unit(nxt)
+            unit(nxt)
             if r % 2 == 0:
                 for g in (r + 2, r + 3):
                     if ok(g):
@@ -516,6 +505,30 @@ def tile_quantumcoherencelayer_t_kernel(
             if ok(r + LOADS_AHEAD):
                 load(r + LOADS_AHEAD)
 
-
-        for r in range(NG + LAG):
+        for r in range(NG - 1):
             step(r)
+
+        a, b, c = NG - 3, NG - 2, NG - 1
+        to_rows(a, 0)
+        to_rows(a, 1)
+        weigh(b)
+        var_turn(b)
+        var_sums_scalar(b)
+        to_rows(b, 0)
+        to_rows(b, 1)
+        rotate(c, ())
+        means(c)
+        stats(b)
+        finish(a, 0)
+        finish(a, 1)
+        centre(c)
+        var_direct(c)
+        last_to_features(c)
+        weigh(c)
+        stats(c)
+        finish(b, 0)
+        finish(b, 1)
+        for o in range(2):
+            to_rows(c, o)
+        for o in range(2):
+            finish(c, o)

@@ -134,17 +134,22 @@ def tile_quantumcoherencelayer_t_kernel(
         def squares_eps(g):
             squares(g, "sa", bias=eps_t[:])
 
-        def add_squares(g, key, eng):
+        def add_squares(g, key, eng, lo=0, hi=2):
             sq = st[("x" + key, g)]
-            out = work.tile([P, SIZES[g], D], F32, name=key, bufs=SUM_BUFS)
-            eng.tensor_tensor(out=out[:], in0=sq[:, 0, :, :], in1=sq[:, 1, :, :], op=ALU.add)
-            st[(key, g)] = out
+            if lo == 0:
+                st[(key, g)] = work.tile([P, SIZES[g], D], F32, name=key, bufs=SUM_BUFS)
+            eng.tensor_tensor(
+                out=st[(key, g)][:, lo:hi, :], in0=sq[:, 0, lo:hi, :], in1=sq[:, 1, lo:hi, :], op=ALU.add
+            )
 
         def square_sum(g, eng):
             add_squares(g, "sr", eng)
 
+        def shared(g):
+            return g % 2 == 0 and 6 <= g
+
         def eps_sum(g):
-            add_squares(g, "sa", nc.vector)
+            add_squares(g, "sa", nc.vector, 1 if shared(g) else 0)
 
         def root_eps(g):
             sa = st[("sa", g)]
@@ -340,6 +345,13 @@ def tile_quantumcoherencelayer_t_kernel(
             )
             st[("rstd", g)] = rstd
 
+        def stats_scalar(g):
+            rstd = small.tile([P, 2, SIZES[g]], F32, name="rstd")
+            nc.scalar.activation(
+                out=rstd[:], in_=st[("ssq", g)][:], func=ACT.Abs_reciprocal_sqrt, scale=1.0 / D, bias=eps_t[:]
+            )
+            st[("rstd", g)] = rstd
+
         def to_features(g):
             n = SIZES[g]
             terms = (st[("u", g)], st[("v", g)])
@@ -475,11 +487,13 @@ def tile_quantumcoherencelayer_t_kernel(
                 x_copy(r + 2, nc.vector.tensor_copy)
             reduce_range(nxt)
             means(cur)
-            if ok(old):
+            if ok(old) and ("rstd", old) not in st:
                 stats(old)
             for g in range(HEAD if r == 0 else new, new + 1):
                 if ok(g):
                     square_sum(g, nc.gpsimd)
+                    if shared(g):
+                        add_squares(g, "sa", nc.gpsimd, 0, 1)
             if prv in IDLE_SUMS:
                 var_sums_scalar(prv)
             trig(nxt)
@@ -502,6 +516,8 @@ def tile_quantumcoherencelayer_t_kernel(
                     if ok(g):
                         root_eps(g)
                         root_plain(g)
+                if ok(prv) and ok(r + 2):
+                    stats_scalar(prv)
             if ok(r + LOADS_AHEAD):
                 load(r + LOADS_AHEAD)
 

@@ -145,11 +145,11 @@ def tile_quantumcoherencelayer_t_kernel(
         def square_sum(g, eng):
             add_squares(g, "sr", eng)
 
-        def shared(g):
+        def spare(g):
             return g % 2 == 0 and 6 <= g
 
         def eps_sum(g):
-            add_squares(g, "sa", nc.vector, 1 if shared(g) else 0)
+            add_squares(g, "sa", nc.vector, 1 if spare(g) else 0)
 
         def root_eps(g):
             sa = st[("sa", g)]
@@ -305,15 +305,20 @@ def tile_quantumcoherencelayer_t_kernel(
                     )
             st[("d", g)] = d
 
-        def var_direct(g):
+        def var_direct(g, o):
             n = SIZES[g]
-            d = st[("d", g)]
-            ssq = small.tile([P, 2, n], F32, name="ssq")
-            for o in range(2):
-                for tt in range(n):
-                    junk = work.tile([P, D], F32, name="sjunk", tag="vjunk", bufs=2)
-                    nc.scalar.activation(out=junk[:], in_=d[:, o, tt, :], func=ACT.Square, accum_out=ssq[:, o, tt : tt + 1])
-            st[("ssq", g)] = ssq
+            if o == 0:
+                st[("ssq", g)] = small.tile([P, 2, n], F32, name="ssq")
+                st[("rstd", g)] = small.tile([P, 2, n], F32, name="rstd")
+            ssq = st[("ssq", g)]
+            for tt in range(n):
+                junk = work.tile([P, D], F32, name="sjunk", tag="vjunk", bufs=2)
+                nc.scalar.activation(
+                    out=junk[:], in_=st[("d", g)][:, o, tt, :], func=ACT.Square, accum_out=ssq[:, o, tt : tt + 1]
+                )
+            nc.scalar.activation(
+                out=st[("rstd", g)][:, o, :], in_=ssq[:, o, :], func=ACT.Abs_reciprocal_sqrt, scale=1.0 / D, bias=eps_t[:]
+            )
 
         def var_sums(g):
             ssq = small.tile([P, 2, SIZES[g]], F32, name="ssq")
@@ -426,9 +431,12 @@ def tile_quantumcoherencelayer_t_kernel(
             if g < NG - 1:
                 nc.sync.dma_start(out=(or_d, oi_d)[o][:, FIRST[g] : FIRST[g] + n, :], in_=res[:])
 
+        def load_root_table():
+            nc.scalar.activation(out=warm[:], in_=one_t[:], func=ACT.Abs_reciprocal_sqrt)
+
         ctx.enter_context(tc.manual_schedule(engines={ENG.DVE, ENG.Activation, ENG.Pool, ENG.PE}))
 
-        nc.scalar.activation(out=warm[:], in_=one_t[:], func=ACT.Abs_reciprocal_sqrt)
+        load_root_table()
         for g in range(HEAD):
             squares_eps(g)
             x_transposes(g)
@@ -471,11 +479,14 @@ def tile_quantumcoherencelayer_t_kernel(
             if ok(old):
                 to_rows(old, 0)
                 to_rows(old, 1)
+            if ok(new) and spare(new):
+                squares_plain(new)
             if ok(prv):
                 weigh(prv)
                 var_turn(prv)
             if ok(new):
-                squares_plain(new)
+                if not spare(new):
+                    squares_plain(new)
                 squares_eps(new)
             if r + 2 == NG - 1:
                 x_copy(r + 2, nc.scalar.copy)
@@ -492,7 +503,7 @@ def tile_quantumcoherencelayer_t_kernel(
             for g in range(HEAD if r == 0 else new, new + 1):
                 if ok(g):
                     square_sum(g, nc.gpsimd)
-                    if shared(g):
+                    if spare(g):
                         add_squares(g, "sa", nc.gpsimd, 0, 1)
             if prv in IDLE_SUMS:
                 var_sums_scalar(prv)
@@ -529,20 +540,21 @@ def tile_quantumcoherencelayer_t_kernel(
         to_rows(a, 1)
         weigh(b)
         var_turn(b)
+        load_root_table()
         var_sums_scalar(b)
+        stats_scalar(b)
         to_rows(b, 0)
-        to_rows(b, 1)
         rotate(c, ())
         means(c)
-        stats(b)
         finish(a, 0)
-        finish(a, 1)
         centre(c)
-        var_direct(c)
+        var_direct(c, 0)
         last_to_features(c)
         weigh(c)
-        stats(c)
+        var_direct(c, 1)
+        finish(a, 1)
         finish(b, 0)
+        to_rows(b, 1)
         finish(b, 1)
         for o in range(2):
             to_rows(c, o)

@@ -123,16 +123,18 @@ def tile_quantumcoherencelayer_t_kernel(
         def turn(out, in_, start, stop):
             nc.tensor.matmul(out=out, lhsT=in_, rhs=ident[:], is_transpose=True, start=start, stop=stop)
 
-        def squares(g, key, **shift):
-            sq = work.tile([P, 2, SIZES[g], D], F32, name="x" + key, bufs=2)
-            nc.scalar.activation(out=sq[:], in_=st[("x", g)][:], func=ACT.Square, **shift)
-            st[("x" + key, g)] = sq
+        def squares(g, key, lo=0, hi=2, **shift):
+            if lo == 0:
+                st[("x" + key, g)] = work.tile([P, 2, SIZES[g], D], F32, name="x" + key, bufs=2)
+            nc.scalar.activation(
+                out=st[("x" + key, g)][:, :, lo:hi, :], in_=st[("x", g)][:, :, lo:hi, :], func=ACT.Square, **shift
+            )
 
         def squares_plain(g):
             squares(g, "sr")
 
-        def squares_eps(g):
-            squares(g, "sa", bias=eps_t[:])
+        def squares_eps(g, lo=0, hi=2):
+            squares(g, "sa", lo, hi, bias=eps_t[:])
 
         def add_squares(g, key, eng, lo=0, hi=2):
             sq = st[("x" + key, g)]
@@ -481,13 +483,16 @@ def tile_quantumcoherencelayer_t_kernel(
                 to_rows(old, 1)
             if ok(new) and spare(new):
                 squares_plain(new)
+                squares_eps(new, 0, 1)
             if ok(prv):
                 weigh(prv)
                 var_turn(prv)
             if ok(new):
                 if not spare(new):
                     squares_plain(new)
-                squares_eps(new)
+                    squares_eps(new)
+                else:
+                    squares_eps(new, 1, 2)
             if r + 2 == NG - 1:
                 x_copy(r + 2, nc.scalar.copy)
             if r == 0:
@@ -513,7 +518,7 @@ def tile_quantumcoherencelayer_t_kernel(
             if ok(old):
                 finish(old, 0)
                 finish(old, 1)
-            if ok(prv) and prv not in IDLE_SUMS:
+            if ok(prv) and prv not in IDLE_SUMS and not (ok(new) and spare(new)):
                 var_sums(prv)
             to_features(cur)
             if ok(r + 2):
@@ -522,6 +527,8 @@ def tile_quantumcoherencelayer_t_kernel(
                 if ok(g):
                     eps_sum(g)
             unit(nxt)
+            if ok(new) and spare(new):
+                var_sums(prv)
             if r % 2 == 0:
                 for g in (r + 2, r + 3):
                     if ok(g):

@@ -103,7 +103,9 @@ def tile_quantumcoherencelayer_t_kernel(
         make_identity(nc, ident_bf[:])
 
         def phase_codes():
-            nc.vector.tensor_copy(out=ph_grp[:], in_=ph_raw[:].rearrange("p j n -> p n j"))
+            nc.vector.tensor_copy(
+                out=ph_grp[:].rearrange("p (c i) j -> p c j i", i=4), in_=ph_raw[:].rearrange("p j (c i) -> p c j i", i=4)
+            )
             nc.vector.tensor_scalar(out=cfs[:], in0=cf_bf[:], scalar1=1.0 / TWO_PI, scalar2=None, op0=ALU.mult)
             nc.vector.tensor_scalar(
                 out=ncf[:], in0=cf_bf[:], scalar1=-1.0 / (TWO_PI * D * D), scalar2=None, op0=ALU.mult
@@ -442,12 +444,11 @@ def tile_quantumcoherencelayer_t_kernel(
         for g in range(HEAD):
             squares_eps(g)
             x_transposes(g)
-            x_copy(g, nc.vector.tensor_copy)
-            quantise(g)
-            if g == 0:
-                phase_codes()
-            eps_sum(g)
+        x_copy(0, nc.vector.tensor_copy)
+        quantise(0)
+        phase_codes()
         for g in range(HEAD):
+            eps_sum(g)
             root_eps(g)
         for g in range(HEAD):
             squares_plain(g)
@@ -460,6 +461,9 @@ def tile_quantumcoherencelayer_t_kernel(
             square_sum(g, nc.vector)
             root_plain(g)
         trig(0)
+        for g in range(1, HEAD):
+            x_copy(g, nc.vector.tensor_copy)
+            quantise(g)
         norm_constants()
         squares_plain(HEAD)
         squares_eps(HEAD)

@@ -402,16 +402,19 @@ def tile_quantumcoherencelayer_t_kernel(
                     nc.scalar.activation(out=st[("sq", g)][:, c, :, :, :], in_=st[("d_ps", g)][c][:], func=ACT.Square)
             st[("yt", g)] = yt
 
+        def var_bank(g):
+            v_ps = ps.tile([P, 2 * SIZES[g], P], F32, name="v_ps", tag="bank")
+            st[("v_ps", g)] = v_ps
+
         def var_turn(g):
             n = SIZES[g]
             sq = st[("sq", g)]
-            v_ps = ps.tile([P, 2 * n, P], F32, name="v_ps", tag="bank")
+            v_ps = st[("v_ps", g)]
             for c in range(4):
                 for o in range(2):
                     for tt in range(n):
                         turn(v_ps[:, n * o + tt, :], sq[:, c, o, tt, :], c == 0 and o == 0 and tt == 0,
                              c == 3 and o == 1 and tt == n - 1)
-            st[("v_ps", g)] = v_ps
 
         def to_rows(g, o):
             yt = st[("yt", g)]
@@ -490,7 +493,9 @@ def tile_quantumcoherencelayer_t_kernel(
                 squares_eps(new, 0, 1)
             if ok(prv):
                 weigh(prv)
-                var_turn(prv)
+                var_bank(prv)
+                if not (ok(new) and spare(new)):
+                    var_turn(prv)
             if ok(new):
                 if not spare(new):
                     squares_plain(new)
@@ -503,6 +508,8 @@ def tile_quantumcoherencelayer_t_kernel(
                 unit(cur)
             coh_sums(nxt)
             rotate(cur, (gain_a, gain_b))
+            if ok(old) and ok(new - 1) and spare(new - 1):
+                var_sums(old)
             if r + 2 < NG - 1:
                 x_copy(r + 2, nc.vector.tensor_copy)
             reduce_range(nxt)
@@ -525,14 +532,14 @@ def tile_quantumcoherencelayer_t_kernel(
             if ok(prv) and prv not in IDLE_SUMS and not (ok(new) and spare(new)):
                 var_sums(prv)
             to_features(cur)
+            if ok(new) and spare(new):
+                var_turn(prv)
             if ok(r + 2):
                 quantise(r + 2)
             for g in range(HEAD if r == 0 else new, new + 1):
                 if ok(g):
                     eps_sum(g)
             unit(nxt)
-            if ok(new) and spare(new):
-                var_sums(prv)
             if r % 2 == 0:
                 for g in (r + 2, r + 3):
                     if ok(g):
@@ -550,6 +557,7 @@ def tile_quantumcoherencelayer_t_kernel(
         to_rows(a, 0)
         to_rows(a, 1)
         weigh(b)
+        var_bank(b)
         var_turn(b)
         load_root_table()
         var_sums_scalar(b)

import math
from contextlib import ExitStack

import concourse.mybir as mybir
from concourse.masks import make_identity

F32 = mybir.dt.float32
BF16 = mybir.dt.bfloat16
I32 = mybir.dt.int32
U32 = mybir.dt.uint32
U8 = mybir.dt.uint8
FP8X4 = mybir.dt.float8_e4m3fn_x4
ALU = mybir.AluOpType
ACT = mybir.ActivationFunctionType
ENG = mybir.EngineType

P = 128
D = 512
ROWS = 4096
NT = ROWS // P
SIZES = [2] * 16
NG = len(SIZES)
FIRST = [sum(SIZES[:g]) for g in range(NG)]
GMAX = max(SIZES)
EPS = 1e-8
TWO_PI = 2.0 * math.pi
SUM_BUFS = 5
AHEAD = 3
HEAD = 2
LOADS_AHEAD = 6
LAG = 2
IDLE_SUMS = (NG - 4, NG - 3, NG - 2)

FLOPS = 2 * ROWS * D * D


def tile_quantumcoherencelayer_t_kernel(
    tc, x_real, x_imag, phase_matrix, coherence_factor, ln_weight, ln_bias, out_0, out_1
):
    nc = tc.nc
    xr_d = x_real.flatten_outer_dims().rearrange("(p t) d -> p t d", t=NT)
    xi_d = x_imag.flatten_outer_dims().rearrange("(p t) d -> p t d", t=NT)
    or_d = out_0.flatten_outer_dims().rearrange("(p t) d -> p t d", t=NT)
    oi_d = out_1.flatten_outer_dims().rearrange("(p t) d -> p t d", t=NT)

    with ExitStack() as ctx:
        keep = ctx.enter_context(tc.tile_pool(name="keep", bufs=1))
        work = ctx.enter_context(tc.tile_pool(name="work", bufs=1))
        small = ctx.enter_context(tc.tile_pool(name="small", bufs=6))
        ps = ctx.enter_context(tc.psum_pool(name="ps", bufs=8))

        ph_raw = work.tile([P, 4, D], BF16, name="ph_raw", tag="yt", bufs=3, align_bytes=64)
        ph_grp = work.tile([P, D, 4], BF16, name="ph_grp", tag="yt", bufs=3, align_bytes=64)
        ph_codes = keep.tile([P, D], U32, name="ph_codes", align_bytes=64)
        ph_scales = keep.tile([P, D], U8, name="ph_scales", align_bytes=64)
        b_row = keep.tile([P, D], BF16, name="b_row")
        w_rows = keep.tile([P, P], BF16, name="w_rows")
        ident_bf = keep.tile([P, P], BF16, name="ident_bf")
        b_sb = keep.tile([P, D], F32, name="b_sb")
        w_col = keep.tile([P, 4], F32, name="w_col")
        ones = keep.tile([P, P], BF16, name="ones")
        ident = keep.tile([P, P], F32, name="ident")
        cf_bf = keep.tile([P, 1], BF16, name="cf_bf")
        cfs = keep.tile([P, 1], F32, name="cfs")
        ncf = keep.tile([P, 1], F32, name="ncf")
        eps_t = keep.tile([P, 1], F32, name="eps_t")
        hpi_t = keep.tile([P, 1], F32, name="hpi_t")
        one_t = keep.tile([P, 1], F32, name="one_t")
        warm = keep.tile([P, 1], F32, name="warm")
        mhalf = keep.tile([P, 2 * GMAX], F32, name="mhalf")

        st = {}

        def ok(g):
            return 0 <= g < NG

        def load(g):
            n = SIZES[g]
            sl = slice(FIRST[g], FIRST[g] + n)
            x = work.tile([P, 2, n, D], BF16, name="x", bufs=LOADS_AHEAD, align_bytes=64)
            nc.sync.dma_start(out=x[:, 0, :, :], in_=xr_d[:, sl, :])
            nc.sync.dma_start(out=x[:, 1, :, :], in_=xi_d[:, sl, :])
            st[("x", g)] = x
            st[("xr", g)] = x[:, 0, :, :]
            st[("xi", g)] = x[:, 1, :, :]

        load(0)
        nc.sync.dma_start(out=ph_raw[:], in_=phase_matrix.rearrange("(p j) n -> p j n", j=4))
        load(1)
        nc.vector.memset(one_t[:], 1.0)
        nc.vector.memset(eps_t[:], EPS)
        nc.vector.memset(b_row[:], 0.0)
        nc.vector.memset(w_rows[:], 0.0)
        nc.sync.dma_start(out=cf_bf[:], in_=coherence_factor.partition_broadcast(P))
        nc.sync.dma_start(out=w_rows[0:4, :], in_=ln_weight.rearrange("(c j) -> c j", c=4))
        nc.sync.dma_start(out=b_row[0:1, :], in_=ln_bias.unsqueeze(0))
        for g in range(2, LOADS_AHEAD):
            load(g)
        nc.vector.memset(ones[:], 1.0)
        nc.vector.tensor_scalar(out=hpi_t[:], in0=one_t[:], scalar1=0.5 * math.pi, scalar2=None, op0=ALU.mult)
        nc.vector.memset(mhalf[:], -0.5)
        make_identity(nc, ident[:])
        make_identity(nc, ident_bf[:])

        def phase_codes():
            nc.vector.tensor_copy(
                out=ph_grp[:].rearrange("p (c i) j -> p c j i", i=4), in_=ph_raw[:].rearrange("p j (c i) -> p c j i", i=4)
            )
            nc.vector.tensor_scalar(out=cfs[:], in0=cf_bf[:], scalar1=1.0 / TWO_PI, scalar2=None, op0=ALU.mult)
            nc.vector.tensor_scalar(
                out=ncf[:], in0=cf_bf[:], scalar1=-1.0 / (TWO_PI * D * D), scalar2=None, op0=ALU.mult
            )
            nc.vector.quantize_mx(
                out=ph_codes[:].bitcast(FP8X4), scales=ph_scales[:], in_=ph_grp[:].rearrange("p n j -> p (n j)")
            )

        def norm_constants():
            b_ps = ps.tile([P, D], F32, name="b_ps", tag="bank")
            nc.tensor.matmul(out=b_ps[:], lhsT=ones[:], rhs=b_row[:], start=True, stop=True)
            nc.vector.tensor_copy(out=b_sb[:], in_=b_ps[:])
            w_ps = ps.tile([P, P], BF16, name="w_ps", tag="bank")
            nc.tensor.transpose(w_ps[:], w_rows[:], ident_bf[:])
            nc.vector.tensor_copy(out=w_col[:], in_=w_ps[:, 0:4])

        def turn(out, in_, start, stop):
            nc.tensor.matmul(out=out, lhsT=in_, rhs=ident[:], is_transpose=True, start=start, stop=stop)

        def squares(g, key, lo=0, hi=2, **shift):
            if lo == 0:
                st[("x" + key, g)] = work.tile([P, 2, SIZES[g], D], F32, name="x" + key, bufs=2)
            nc.scalar.activation(
                out=st[("x" + key, g)][:, :, lo:hi, :], in_=st[("x", g)][:, :, lo:hi, :], func=ACT.Square, **shift
            )

        def squares_plain(g):
            squares(g, "sr")

        def squares_eps(g, lo=0, hi=2):
            squares(g, "sa", lo, hi, bias=eps_t[:])

        def add_squares(g, key, eng, lo=0, hi=2):
            sq = st[("x" + key, g)]
            if lo == 0:
                st[(key, g)] = work.tile([P, SIZES[g], D], F32, name=key, bufs=SUM_BUFS)
            eng.tensor_tensor(
                out=st[(key, g)][:, lo:hi, :], in0=sq[:, 0, lo:hi, :], in1=sq[:, 1, lo:hi, :], op=ALU.add
            )

        def square_sum(g, eng):
            add_squares(g, "sr", eng)

        def spare(g):
            return g % 2 == 0 and 6 <= g

        def eps_sum(g):
            add_squares(g, "sa", nc.vector, 1 if spare(g) else 0)

        def root_eps(g):
            sa = st[("sa", g)]
            nc.scalar.activation(out=sa[:], in_=sa[:], func=ACT.Abs_reciprocal_sqrt)

        def root_plain(g):
            sr = st[("sr", g)]
            nc.scalar.activation(out=sr[:], in_=sr[:], func=ACT.Abs_reciprocal_sqrt, bias=eps_t[:])

        def x_transposes(g):
            n = SIZES[g]
            xr_words = st[("xr", g)].rearrange("p t d -> p (t d)").bitcast(F32).rearrange(
                "p (t j u) -> p t u j", t=n, u=2
            )
            xt = ps.tile([P, n, 2, P], F32, name="xt", tag="bank")
            for tt in range(n):
                for u in range(2):
                    nc.tensor.transpose(xt[:, tt, u, :], xr_words[:, tt, u, :], ident[:])
            st[("xt", g)] = xt

        def x_copy(g, copy):
            n = SIZES[g]
            xg = work.tile([P, n * P * 4], BF16, name="xg", bufs=2, align_bytes=64)
            xg_w = xg[:].bitcast(F32).rearrange("p (t r u) -> p t r u", t=n, u=2)
            copy(out=xg_w, in_=st[("xt", g)][:].rearrange("p t u r -> p t r u"))
            st[("xg", g)] = xg

        def quantise(g):
            n = SIZES[g]
            xc = work.tile([P, n * P], U32, name="xc", bufs=3, align_bytes=64)
            xs = work.tile([P, n * P], U8, name="xs", bufs=3, align_bytes=64)
            nc.vector.quantize_mx(out=xc[:].bitcast(FP8X4), scales=xs[:], in_=st[("xg", g)][:])
            st[("xc", g)] = xc
            st[("xs", g)] = xs

        def pe_mm(g):
            xc, xs = st[("xc", g)], st[("xs", g)]
            pts = []
            for tt in range(SIZES[g]):
                pt = ps.tile([P, D], F32, name="pt", tag="bank")
                cols = slice(P * tt, P * tt + P)
                nc.tensor.matmul_mx(
                    out=pt[:],
                    lhsT=xc[:, cols].bitcast(FP8X4),
                    lhsT_scale=xs[:, cols],
                    rhs=ph_codes[:].bitcast(FP8X4),
                    rhs_scale=ph_scales[:],
                    start=True,
                    stop=True,
                )
                pts.append(pt)
            st[("pt", g)] = pts

        def coh_sums(g):
            n = SIZES[g]
            sa = st[("sa", g)]
            coh = small.tile([P, 2, n], F32, name="coh")
            for tt in range(n):
                for o, x_h in enumerate((st[("xr", g)], st[("xi", g)])):
                    junk = work.tile([P, D], F32, name="vjunk", bufs=2)
                    nc.vector.scalar_tensor_tensor(
                        out=junk[:], in0=x_h[:, tt, :], scalar=EPS, in1=sa[:, tt, :],
                        op0=ALU.add, op1=ALU.mult, accum_out=coh[:, o, tt : tt + 1],
                    )
            st[("coh", g)] = coh

        def gain_a(g):
            coh = st[("coh", g)]
            csq = small.tile([P, 2, SIZES[g]], F32, name="csq")
            nc.vector.scalar_tensor_tensor(out=csq[:], in0=coh[:], scalar=ncf[:], in1=coh[:], op0=ALU.mult, op1=ALU.mult)
            st[("csq", g)] = csq

        def gain_b(g):
            csq = st[("csq", g)]
            gq = small.tile([P, SIZES[g]], F32, name="gq")
            nc.vector.scalar_tensor_tensor(
                out=gq[:], in0=csq[:, 0, :], scalar=cfs[:], in1=csq[:, 1, :], op0=ALU.add, op1=ALU.add
            )
            st[("gq", g)] = gq

        def reduce_range(g):
            n = SIZES[g]
            gq, pts = st[("gq", g)], st[("pt", g)]
            fr = work.tile([P, n, D], F32, name="fr", bufs=2)
            kks = []
            for tt in range(n):
                kk = work.tile([P, D], I32, name="kk", bufs=2)
                nc.vector.tensor_scalar(
                    out=kk[:], in0=pts[tt][:], scalar1=gq[:, tt : tt + 1], scalar2=None, op0=ALU.mult
                )
                kks.append(kk)
            for tt in range(n):
                nc.vector.scalar_tensor_tensor(
                    out=fr[:, tt, :], in0=pts[tt][:], scalar=gq[:, tt : tt + 1], in1=kks[tt][:],
                    op0=ALU.mult, op1=ALU.subtract,
                )
            st[("fr", g)] = fr

        def trig(g):
            n = SIZES[g]
            fr = st[("fr", g)]
            sc = work.tile([P, n, 2, D], F32, name="sc", bufs=2)
            ss, cc = sc[:, :, 0, :], sc[:, :, 1, :]
            nc.scalar.activation(out=cc, in_=fr[:], func=ACT.Abs)
            nc.scalar.activation(out=ss, in_=fr[:], func=ACT.Sin, scale=TWO_PI)
            nc.scalar.activation(out=cc, in_=cc, func=ACT.Sin, scale=-TWO_PI, bias=hpi_t[:])
            st[("sc", g)] = sc

        def unit(g):
            n = SIZES[g]
            u = work.tile([P, n, 2, D], F32, name="u", bufs=2)
            nc.vector.tensor_tensor(
                out=u[:], in0=st[("x", g)][:].rearrange("p k t d -> p t k d"),
                in1=st[("sr", g)][:].unsqueeze(2).to_broadcast([P, n, 2, D]), op=ALU.mult,
            )
            st[("u", g)] = u
            st[("v", g)] = work.tile([P, n, 2, D], F32, name="v", bufs=2)
            st[("sm", g)] = small.tile([P, 3, n], F32, name="sm")

        def product_imag(g, tt):
            nc.vector.scalar_tensor_tensor(
                out=st[("v", g)][:, tt, :, :], in0=st[("u", g)][:, tt, :, :], scalar=1.0, in1=st[("sc", g)][:, tt, :, :],
                op0=ALU.mult, op1=ALU.mult, accum_out=st[("sm", g)][:, 1, tt : tt + 1],
            )

        def product_real(g, tt, k):
            u = st[("u", g)][:, tt, k, :]
            nc.vector.scalar_tensor_tensor(
                out=u, in0=u, scalar=(1.0, -1.0)[k], in1=st[("sc", g)][:, tt, 1 - k, :],
                op0=ALU.mult, op1=ALU.mult, accum_out=st[("sm", g)][:, 2 * k, tt : tt + 1],
            )

        def means(g):
            n = SIZES[g]
            sm = st[("sm", g)]
            mean = small.tile([P, 2, n], F32, name="mean")
            nc.gpsimd.tensor_tensor(out=sm[:, 0, :], in0=sm[:, 0, :], in1=sm[:, 2, :], op=ALU.add)
            nc.gpsimd.tensor_scalar(
                out=mean[:], in0=sm[:, 0:2, :], scalar1=-1.0 / D, scalar2=0.0, op0=ALU.mult, op1=ALU.add
            )
            st[("mean", g)] = mean

        def centre(g):
            n = SIZES[g]
            terms = (st[("u", g)], st[("v", g)])
            mean = st[("mean", g)]
            d = work.tile([P, 2, n, D], F32, name="d", tag="sq", bufs=2)
            for o in range(2):
                for tt in range(n):
                    nc.vector.scalar_tensor_tensor(
                        out=d[:, o, tt, :], in0=terms[o][:, tt, 0, :], scalar=mean[:, o, tt : tt + 1],
                        in1=terms[o][:, tt, 1, :], op0=ALU.add, op1=ALU.add,
                    )
            st[("d", g)] = d

        def var_direct(g, o):
            n = SIZES[g]
            if o == 0:
                st[("ssq", g)] = small.tile([P, 2, n], F32, name="ssq")
                st[("rstd", g)] = small.tile([P, 2, n], F32, name="rstd")
            ssq = st[("ssq", g)]
            for tt in range(n):
                junk = work.tile([P, D], F32, name="sjunk", tag="vjunk", bufs=2)
                nc.scalar.activation(
                    out=junk[:], in_=st[("d", g)][:, o, tt, :], func=ACT.Square, accum_out=ssq[:, o, tt : tt + 1]
                )
            nc.scalar.activation(
                out=st[("rstd", g)][:, o, :], in_=ssq[:, o, :], func=ACT.Abs_reciprocal_sqrt, scale=1.0 / D, bias=eps_t[:]
            )

        def var_sums(g):
            ssq = small.tile([P, 2, SIZES[g]], F32, name="ssq")
            nc.vector.tensor_reduce(
                out=ssq[:].rearrange("p o t -> p (o t)"), in_=st[("v_ps", g)][:], axis=mybir.AxisListType.X, op=ALU.add
            )
            st[("ssq", g)] = ssq

        def var_sums_scalar(g):
            n = SIZES[g]
            ssq = small.tile([P, 2, n], F32, name="ssq")
            for o in range(2):
                for tt in range(n):
                    junk = work.tile([P, P], F32, name="cjunk", tag="vjunk", bufs=2)
                    nc.scalar.activation(
                        out=junk[:], in_=st[("v_ps", g)][:, n * o + tt, :], func=ACT.Copy, accum_out=ssq[:, o, tt : tt + 1]
                    )
            st[("ssq", g)] = ssq

        def stats(g):
            n = SIZES[g]
            ssq = st[("ssq", g)]
            vare = small.tile([P, 2, n], F32, name="vare")
            rstd = small.tile([P, 2, n], F32, name="rstd")
            nc.gpsimd.tensor_scalar(out=vare[:], in0=ssq[:], scalar1=1.0 / D, scalar2=EPS, op0=ALU.mult, op1=ALU.add)
            nc.gpsimd.tensor_tensor(
                out=rstd[:].rearrange("p o t -> p (o t)"), in0=vare[:].rearrange("p o t -> p (o t)"),
                in1=mhalf[:, 0 : 2 * n], op=ALU.pow,
            )
            st[("rstd", g)] = rstd

        def stats_scalar(g):
            rstd = small.tile([P, 2, SIZES[g]], F32, name="rstd")
            nc.scalar.activation(
                out=rstd[:], in_=st[("ssq", g)][:], func=ACT.Abs_reciprocal_sqrt, scale=1.0 / D, bias=eps_t[:]
            )
            st[("rstd", g)] = rstd

        def to_features(g):
            n = SIZES[g]
            terms = (st[("u", g)], st[("v", g)])
            mean = st[("mean", g)]
            banks = []
            for c in range(4):
                d_ps = ps.tile([P, 2, n, P], F32, name="d_ps", tag="bank")
                cols = slice(P * c, P * c + P)
                for k in range(2):
                    for o in range(2):
                        for tt in range(n):
                            turn(d_ps[:, o, tt, :], terms[o][:, tt, k, cols], k == 0 and o == 0 and tt == 0, False)
                for o in range(2):
                    for tt in range(n):
                        turn(d_ps[:, o, tt, :], mean[:, o, tt : tt + 1].to_broadcast([P, P]), False, o == 1 and tt == n - 1)
                banks.append(d_ps)
            st[("d_ps", g)] = banks

        def last_to_features(g):
            banks = []
            for c in range(4):
                d_ps = ps.tile([P, 2, SIZES[g], P], F32, name="d_ps", tag="bank")
                for o in range(2):
                    for tt in range(SIZES[g]):
                        nc.tensor.transpose(d_ps[:, o, tt, :], st[("d", g)][:, o, tt, P * c : P * c + P], ident[:])
                banks.append(d_ps)
            st[("d_ps", g)] = banks

        def weigh(g):
            n = SIZES[g]
            yt = work.tile([P, 4, 2, n, P], F32, name="yt", tag="yt", bufs=3, align_bytes=64)
            if g < NG - 1:
                st[("sq", g)] = work.tile([P, 4, 2, n, P], F32, name="sq", tag="sq", bufs=2)
            for c in range(4):
                nc.scalar.activation(
                    out=yt[:, c, :, :, :], in_=st[("d_ps", g)][c][:], func=ACT.Copy, scale=w_col[:, c : c + 1]
                )
                if g < NG - 1:
                    nc.scalar.activation(out=st[("sq", g)][:, c, :, :, :], in_=st[("d_ps", g)][c][:], func=ACT.Square)
            st[("yt", g)] = yt

        def var_bank(g):
            v_ps = ps.tile([P, 2 * SIZES[g], P], F32, name="v_ps", tag="bank")
            st[("v_ps", g)] = v_ps

        def var_turn(g):
            n = SIZES[g]
            sq = st[("sq", g)]
            v_ps = st[("v_ps", g)]
            for c in range(4):
                for o in range(2):
                    for tt in range(n):
                        turn(v_ps[:, n * o + tt, :], sq[:, c, o, tt, :], c == 0 and o == 0 and tt == 0,
                             c == 3 and o == 1 and tt == n - 1)

        def to_rows(g, o):
            yt = st[("yt", g)]
            for tt in range(SIZES[g]):
                y_ps = ps.tile([P, D], F32, name="y_ps", tag="bank")
                for c in range(4):
                    nc.tensor.transpose(y_ps[:, P * c : P * c + P], yt[:, c, o, tt, :], ident[:])
                st[("y_ps", g, o, tt)] = y_ps

        def finish(g, o):
            n = SIZES[g]
            rstd = st[("rstd", g)]
            res = work.tile([P, n, D], F32, name="res", bufs=4)
            for tt in range(n):
                nc.vector.scalar_tensor_tensor(
                    out=res[:, tt, :], in0=st[("y_ps", g, o, tt)][:], scalar=rstd[:, o, tt : tt + 1],
                    in1=b_sb[:], op0=ALU.mult, op1=ALU.add,
                )
                if g == NG - 1:
                    nc.sync.dma_start(out=(or_d, oi_d)[o][:, FIRST[g] + tt, :], in_=res[:, tt, :])
            if g < NG - 1:
                nc.sync.dma_start(out=(or_d, oi_d)[o][:, FIRST[g] : FIRST[g] + n, :], in_=res[:])

        def load_root_table():
            nc.scalar.activation(out=warm[:], in_=one_t[:], func=ACT.Abs_reciprocal_sqrt)

        ctx.enter_context(tc.manual_schedule(engines={ENG.DVE, ENG.Activation, ENG.Pool, ENG.PE}))

        load_root_table()
        for g in range(HEAD):
            squares_eps(g)
            x_transposes(g)
        x_copy(0, nc.vector.tensor_copy)
        quantise(0)
        phase_codes()
        for g in range(HEAD):
            eps_sum(g)
            root_eps(g)
        for g in range(HEAD):
            squares_plain(g)
        pe_mm(0)
        coh_sums(0)
        gain_a(0)
        gain_b(0)
        reduce_range(0)
        for g in range(HEAD):
            square_sum(g, nc.vector)
            root_plain(g)
        trig(0)
        for g in range(1, HEAD):
            x_copy(g, nc.vector.tensor_copy)
            quantise(g)
        norm_constants()
        squares_plain(HEAD)
        squares_eps(HEAD)

        def rotate(g, weave):
            for tt in range(SIZES[g]):
                product_imag(g, tt)
                if weave:
                    weave[tt](g + 1)
            for k in range(2):
                for tt in range(SIZES[g]):
                    product_real(g, tt, k)

        def step(r):
            nxt, cur, prv, new, old = r + 1, r, r - 1, r + AHEAD, r - LAG
            pe_mm(nxt)
            if ok(r + 2):
                x_transposes(r + 2)
            if ok(old):
                to_rows(old, 0)
                to_rows(old, 1)
            if ok(new) and spare(new):
                squares_plain(new)
                squares_eps(new, 0, 1)
            if ok(prv):
                weigh(prv)
                var_bank(prv)
                if not (ok(new) and spare(new)):
                    var_turn(prv)
            if ok(new):
                if not spare(new):
                    squares_plain(new)
                    squares_eps(new)
                else:
                    squares_eps(new, 1, 2)
            if r + 2 == NG - 1:
                x_copy(r + 2, nc.scalar.copy)
            if r == 0:
                unit(cur)
            coh_sums(nxt)
            rotate(cur, (gain_a, gain_b))
            if ok(old) and ok(new - 1) and spare(new - 1):
                var_sums(old)
            if r + 2 < NG - 1:
                x_copy(r + 2, nc.vector.tensor_copy)
            reduce_range(nxt)
            means(cur)
            if ok(old) and ("rstd", old) not in st:
                stats(old)
            for g in range(HEAD if r == 0 else new, new + 1):
                if ok(g):
                    square_sum(g, nc.gpsimd)
                    if spare(g):
                        add_squares(g, "sa", nc.gpsimd, 0, 1)
            if prv in IDLE_SUMS:
                var_sums_scalar(prv)
            trig(nxt)
            if prv == NG - 3:
                stats(prv)
            if ok(old):
                finish(old, 0)
                finish(old, 1)
            if ok(prv) and prv not in IDLE_SUMS and not (ok(new) and spare(new)):
                var_sums(prv)
            to_features(cur)
            if ok(new) and spare(new):
                var_turn(prv)
            if ok(r + 2):
                quantise(r + 2)
            for g in range(HEAD if r == 0 else new, new + 1):
                if ok(g):
                    eps_sum(g)
            unit(nxt)
            if r % 2 == 0:
                for g in (r + 2, r + 3):
                    if ok(g):
                        root_eps(g)
                        root_plain(g)
                if ok(prv) and ok(r + 2):
                    stats_scalar(prv)
            if ok(r + LOADS_AHEAD):
                load(r + LOADS_AHEAD)

        for r in range(NG - 1):
            step(r)

        a, b, c = NG - 3, NG - 2, NG - 1
        to_rows(a, 0)
        to_rows(a, 1)
        weigh(b)
        var_bank(b)
        var_turn(b)
        load_root_table()
        var_sums_scalar(b)
        stats_scalar(b)
        to_rows(b, 0)
        rotate(c, ())
        means(c)
        finish(a, 0)
        centre(c)
        var_direct(c, 0)
        last_to_features(c)
        weigh(c)
        var_direct(c, 1)
        finish(a, 1)
        finish(b, 0)
        to_rows(b, 1)
        finish(b, 1)
        for o in range(2):
            to_rows(c, o)
        for o in range(2):
            finish(c, o)
